import numpy as np
import ml_dtypes


def mxq(x, axis, fmt="e4m3"):
    dtype, down = {"e4m3": (ml_dtypes.float8_e4m3fn, 7), "e5m2": (ml_dtypes.float8_e5m2, 14)}[fmt]
    v = np.moveaxis(np.asarray(x, np.float32).astype(ml_dtypes.bfloat16).astype(np.float64), axis, -1)
    blocks = v.reshape(v.shape[:-1] + (-1, 32))
    amax = np.abs(blocks).max(-1, keepdims=True)
    byte = np.maximum(np.where(amax > 0, np.frexp(amax)[1] - 1 + 127, 0) - down, 1)
    scale = np.exp2(byte - 127.0)
    codes = (blocks / scale).astype(np.float32).astype(dtype).astype(np.float64)
    return np.moveaxis((codes * scale).reshape(v.shape), -1, axis)


WIDE = False


def mx_kscale(k):
    if not WIDE:
        return np.ones(k)
    levels = np.array([10, -10, 5, -5, 0])
    a = np.random.permutation(np.resize(levels, k // 512 * 4)).reshape(k // 512, 4)
    idx = np.arange(k)
    return np.exp2(a[idx // 512, idx % 128 // 32])


BF16 = ml_dtypes.bfloat16


def bf(x):
    return np.asarray(x, np.float32).astype(BF16)


def f64(x):
    return np.asarray(x).astype(np.float64)


E2M1 = np.array([0.0, 0.5, 1.0, 1.5, 2.0, 3.0, 4.0, 6.0, -0.0, -0.5, -1.0, -1.5, -2.0, -3.0, -4.0, -6.0])


def pack_weight(w, fmt):
    k, n = w.shape
    w = f64(bf(w)).reshape(k // 32, 32, n)
    amax = np.abs(w).max(1)
    if fmt == "e4m3":
        byte = np.frexp(amax)[1] - 1 + 127 - 7
    else:
        mant, ex = np.frexp(amax / 6.0)
        byte = np.where(mant > 0.5, ex, ex - 1) + 127
    byte = np.clip(np.where(amax > 0, byte, 1), 1, 254)
    scaled = (w * np.exp2(127.0 - byte)[:, None, :]).reshape(k, n).astype(np.float32)
    by_word = np.ascontiguousarray(scaled.reshape(k // 512, 128, 4, n).transpose(0, 1, 3, 2))
    if fmt == "e4m3":
        words = by_word.astype(ml_dtypes.float8_e4m3fn).view(np.uint8)
    else:
        c = by_word.astype(ml_dtypes.float4_e2m1fn).view(np.uint8) & 0xF
        words = c[..., 0::2] | (c[..., 1::2] << 4)
    return np.ascontiguousarray(words), np.ascontiguousarray(byte.astype(np.uint8).reshape(k // 512, 16, n))


def unpack_weight(words, scales, fmt):
    g, p, n, _ = words.shape
    if fmt == "e4m3":
        vals = np.ascontiguousarray(words).view(ml_dtypes.float8_e4m3fn).astype(np.float64)
    else:
        nib = np.empty((g, p, n, 4), np.uint8)
        nib[..., 0::2] = words & 0xF
        nib[..., 1::2] = words >> 4
        vals = E2M1[nib]
    vals = vals * np.repeat(np.exp2(scales.astype(np.float64) - 127.0), 8, axis=1)[..., None]
    return vals.transpose(0, 1, 3, 2).reshape(g * 512, n)


B, N, F_NODE, F_EDGE, H = 8, 16, 64, 32, 1024
FMT = "e4m3"


def setup_inputs():
    s, t = mx_kscale(H), mx_kscale(H)
    w1 = np.random.standard_normal((3 * H, H)) / np.sqrt(3 * H) * t
    w1[2 * H:] = w1[2 * H:] / s[:, None]
    h = bf(np.random.standard_normal((B, N, H)))
    e = bf(np.random.standard_normal((B, N, N, H)) * s)
    adj_mask = bf(np.random.uniform(size=(B, N, N, 1)) < 0.5)
    w1_words, w1_scales = pack_weight(w1, FMT)
    b_m1 = bf(np.random.standard_normal(H) * 0.3 * t)
    w2_words, w2_scales = pack_weight(np.random.standard_normal((H, H)) * 2.0 / np.sqrt(H * N) / t[:, None], FMT)
    b_m2 = bf(np.random.standard_normal(H) * 0.4 / np.sqrt(N))
    return {"h": h,
            "e": e,
            "adj_mask": adj_mask,
            "W_m1_words": w1_words,
            "W_m1_scales": w1_scales,
            "b_m1": b_m1,
            "W_m2_words": w2_words,
            "W_m2_scales": w2_scales,
            "b_m2": b_m2}


def reference(h, e, adj_mask, W_m1_words, W_m1_scales, b_m1, W_m2_words, W_m2_scales, b_m2):
    h = f64(h)
    w1 = unpack_weight(W_m1_words, W_m1_scales, FMT)
    hq = mxq(h, 2, "e4m3")
    a_i = hq @ w1[:H]
    a_j = hq @ w1[H:2 * H]
    a_e = mxq(f64(e), 3, "e4m3") @ w1[2 * H:]
    m = a_i[:, :, None, :] + a_j[:, None, :, :] + a_e + f64(b_m1)
    m = np.maximum(m, 0.0)
    m = (mxq(m, 3, "e4m3") @ unpack_weight(W_m2_words, W_m2_scales, FMT)) + f64(b_m2)
    m = m * f64(adj_mask)
    return m.sum(axis=-2) + h

@@ -1,0 +1,245 @@
+from contextlib import ExitStack
+
+import concourse.mybir as mybir
+from concourse.masks import make_identity
+
+F32 = mybir.dt.float32
+BF16 = mybir.dt.bfloat16
+I32 = mybir.dt.int32
+U32 = mybir.dt.uint32
+U8 = mybir.dt.uint8
+FP8X4 = mybir.dt.float8_e4m3fn_x4
+ADD = mybir.AluOpType.add
+MULT = mybir.AluOpType.mult
+RELU = mybir.ActivationFunctionType.Relu
+
+P = 128
+GRAPHS = 8
+NODES = 16
+WIDTH = 1024
+PACK = 4
+K_PASS = P * PACK
+PASSES = WIDTH // K_PASS
+N_TILE = 512
+HALVES = WIDTH // N_TILE
+PLANE_ROWS = 4
+QUADRANT = 32
+E_CHUNK = 4
+E_LEAD = 2
+SUM_LEAD = 4
+
+FLOPS = 2 * (2 * GRAPHS * NODES * NODES + 2 * GRAPHS * NODES) * WIDTH * WIDTH
+
+
+def tile_messagepassing_pa_kernel(
+    tc, h, e, adj_mask, W_m1_words, W_m1_scales, b_m1, W_m2_words, W_m2_scales, b_m2, out
+):
+    nc = tc.nc
+    with ExitStack() as stack:
+        keep = stack.enter_context(tc.tile_pool(name="keep", bufs=1))
+        stage = stack.enter_context(tc.tile_pool(name="stage", bufs=3))
+        sorts = stack.enter_context(tc.tile_pool(name="sorts", bufs=E_CHUNK + 1))
+        sums = stack.enter_context(tc.tile_pool(name="sums", bufs=SUM_LEAD + 2))
+        banks = stack.enter_context(tc.psum_pool(name="banks", bufs=5))
+        flips = stack.enter_context(tc.psum_pool(name="flips", bufs=3))
+        stack.enter_context(tc.manual_schedule())
+
+        ident_f32 = keep.tile([P, P], F32)
+        ident_bf16 = keep.tile([P, P], BF16)
+        h_rows = keep.tile([P, WIDTH], BF16)
+        e_rows = keep.tile([P, NODES, WIDTH], BF16)
+        w1_words = keep.tile([P, 3 * PASSES, PACK * WIDTH], U8, align_bytes=64)
+        w2_words = keep.tile([P, PASSES, PACK * WIDTH], U8, align_bytes=64)
+        planes_a = keep.tile([P, WIDTH], U8, align_bytes=64)
+        planes_b = keep.tile([P, WIDTH], U8, align_bytes=64)
+        h_codes = keep.tile([P, PASSES * P], U32, align_bytes=64)
+        h_planes = keep.tile([P, PASSES * P], U8, align_bytes=64)
+        e_codes = keep.tile([P, NODES, PASSES * P], U32, align_bytes=64)
+        e_planes = keep.tile([P, NODES, PASSES * P], U8, align_bytes=64)
+        b1_all = keep.tile([P, WIDTH], BF16)
+        b2_all = keep.tile([P, WIDTH], BF16)
+        mask_bf16 = keep.tile([P, NODES], BF16)
+        mask_f32 = keep.tile([P, NODES], F32)
+        degree = keep.tile([P, 1], F32)
+        target_term = keep.tile([P, HALVES, PACK, P], F32)
+        source_term = keep.tile([P, HALVES, PACK, P], F32)
+        result = keep.tile([P, WIDTH], F32)
+
+        make_identity(nc, ident_f32[:])
+        make_identity(nc, ident_bf16[:])
+        nc.vector.memset(planes_a[:].bitcast(I32), 0)
+        nc.vector.memset(planes_b[:].bitcast(I32), 0)
+
+        def load_words(tile, dram, first, count):
+            nc.sync.dma_start(
+                out=tile[:, first : first + count, :].bitcast(I32),
+                in_=dram[first : first + count].rearrange("g p n t -> p g (n t)").bitcast(I32),
+            )
+
+        def load_planes(tile, first_plane, dram, first, count):
+            for q in range(P // QUADRANT):
+                row = QUADRANT * q + PLANE_ROWS * first_plane
+                nc.sync.dma_start(
+                    out=tile[row : row + PLANE_ROWS * count, :].bitcast(I32),
+                    in_=dram[first : first + count, PLANE_ROWS * q : PLANE_ROWS * (q + 1), :].bitcast(I32),
+                )
+
+        def load_e(chunk):
+            nc.sync.dma_start(
+                out=e_rows[:, E_CHUNK * chunk : E_CHUNK * (chunk + 1), :].rearrange("r j k -> r (j k)"),
+                in_=e[:, :, E_CHUNK * chunk : E_CHUNK * (chunk + 1), :].rearrange("b i j k -> i b (j k)"),
+            )
+
+        nc.sync.dma_start(out=h_rows[:], in_=h.rearrange("b i k -> i b k"))
+        load_planes(planes_a, 0, W_m1_scales, 0, 4)
+        load_words(w1_words, W_m1_words, 2, 2)
+        load_words(w1_words, W_m1_words, 0, 2)
+        nc.sync.dma_start(out=b1_all[:], in_=b_m1.partition_broadcast(P))
+        load_e(0)
+
+        def sort_words(rows):
+            sorted_words = sorts.tile([P, PASSES, 2, P], F32)
+            nc.scalar.copy(
+                out=sorted_words[:], in_=rows.bitcast(F32).rearrange("r (c p u) -> r c u p", c=PASSES, u=2)
+            )
+            return sorted_words
+
+        def quantise_rows(sorted_words, codes, planes):
+            flipped = flips.tile([P, PASSES, 2, P], F32, tag="flip")
+            for c in range(PASSES):
+                for u in range(2):
+                    nc.tensor.transpose(flipped[:, c, u, :], sorted_words[:, c, u, :], ident_f32[:])
+            grouped = stage.tile([P, PASSES, P, PACK], BF16, align_bytes=64)
+            flat = grouped[:].rearrange("p c r t -> p (c r t)")
+            nc.scalar.copy(
+                out=flat.bitcast(F32).rearrange("p (c r u) -> p c r u", c=PASSES, u=2),
+                in_=flipped[:].rearrange("p c u r -> p c r u"),
+            )
+            nc.vector.quantize_mx(out=codes.bitcast(FP8X4), scales=planes, in_=flat)
+
+        def mx_product(bank, codes, planes, words, first_group, w_planes, first_plane, half):
+            for c in range(PASSES):
+                row = PLANE_ROWS * (first_plane + c)
+                nc.tensor.matmul_mx(
+                    out=bank[:],
+                    lhsT=codes[:, P * c : P * (c + 1)].bitcast(FP8X4),
+                    lhsT_scale=planes[:, P * c : P * (c + 1)],
+                    rhs=words[:, first_group + c, PACK * N_TILE * half : PACK * N_TILE * (half + 1)].bitcast(FP8X4),
+                    rhs_scale=w_planes[row:P, N_TILE * half : N_TILE * (half + 1)],
+                    start=(c == 0),
+                    stop=(c == PASSES - 1),
+                )
+
+        def by_slot(ap):
+            return ap.rearrange("r (p t) -> r t p", t=PACK)
+
+        quantise_rows(sort_words(h_rows[:]), h_codes[:], h_planes[:])
+        for half in range(HALVES):
+            source_bank = banks.tile([P, N_TILE], F32, tag="bank")
+            mx_product(source_bank, h_codes[:], h_planes[:], w1_words, 2, planes_a, 2, half)
+            if half == 0:
+                nc.scalar.copy(out=source_term[:, half], in_=by_slot(source_bank[:]))
+            else:
+                nc.vector.tensor_copy(out=source_term[:, half], in_=by_slot(source_bank[:]))
+        scratch = out.rearrange("b i n -> (b i) n")
+        nc.sync.dma_start(out=scratch, in_=source_term[:].rearrange("r g t p -> r (g t p)"))
+        for half in range(HALVES):
+            target_bank = banks.tile([P, N_TILE], F32, tag="bank")
+            mx_product(target_bank, h_codes[:], h_planes[:], w1_words, 0, planes_a, 0, half)
+            nc.vector.tensor_tensor(
+                out=target_term[:, half],
+                in0=by_slot(target_bank[:]),
+                in1=by_slot(b1_all[:, N_TILE * half : N_TILE * (half + 1)]),
+                op=ADD,
+            )
+
+        node_sums = {}
+        pre_relus = {}
+        r_operands = {}
+
+        def load_node_sum(j):
+            node_sum = sums.tile([P, HALVES, PACK, P], F32)
+            nc.sync.dma_start(
+                out=node_sum[:].rearrange("r g t p -> r (g t p)"),
+                in_=scratch[GRAPHS * j : GRAPHS * (j + 1), :].unsqueeze(0).to_broadcast([NODES, GRAPHS, WIDTH]),
+            )
+            for half in range(HALVES):
+                nc.gpsimd.tensor_tensor(
+                    out=node_sum[:, half], in0=node_sum[:, half], in1=target_term[:, half], op=ADD
+                )
+            node_sums[j] = node_sum
+
+        def first_layer(j):
+            pre_relu = stage.tile([P, HALVES, PACK, P], BF16)
+            for half in range(HALVES):
+                edge_bank = banks.tile([P, N_TILE], F32, tag="bank")
+                mx_product(edge_bank, e_codes[:, j, :], e_planes[:, j, :], w1_words, 4, planes_b, 0, half)
+                nc.vector.tensor_tensor(
+                    out=pre_relu[:, half], in0=by_slot(edge_bank[:]), in1=node_sums[j][:, half], op=ADD
+                )
+            pre_relus[j] = pre_relu
+
+        def quantise_hidden(j):
+            flipped = flips.tile([P, PASSES, PACK, P], BF16, tag="flip")
+            for c in range(PASSES):
+                for t in range(PACK):
+                    nc.tensor.transpose(flipped[:, c, t, :], pre_relus[j][:, c, t, :], ident_bf16[:])
+            hidden = stage.tile([P, PASSES, P, PACK], BF16, align_bytes=64)
+            nc.scalar.activation(out=hidden[:], in_=flipped[:].rearrange("p c t r -> p c r t"), func=RELU)
+            r_codes = stage.tile([P, PASSES * P], U32, align_bytes=64)
+            r_planes = stage.tile([P, PASSES * P], U8, align_bytes=64)
+            nc.vector.quantize_mx(
+                out=r_codes[:].bitcast(FP8X4), scales=r_planes[:], in_=hidden[:].rearrange("p c r t -> p (c r t)")
+            )
+            r_operands[j] = (r_codes, r_planes)
+
+        def second_layer(j):
+            r_codes, r_planes = r_operands[j]
+            for half in range(HALVES):
+                message_bank = banks.tile([P, N_TILE], F32, tag="bank")
+                mx_product(message_bank, r_codes[:], r_planes[:], w2_words, 0, planes_b, 2, half)
+                columns = result[:, N_TILE * half : N_TILE * (half + 1)]
+                nc.vector.scalar_tensor_tensor(
+                    out=columns, in0=message_bank[:], scalar=mask_f32[:, j : j + 1], in1=columns, op0=MULT, op1=ADD
+                )
+
+        sorted_e = {}
+        for j in range(E_CHUNK):
+            sorted_e[j] = sort_words(e_rows[:, j, :])
+        load_planes(planes_b, 0, W_m1_scales, 4, 2)
+        load_words(w1_words, W_m1_words, 4, 2)
+        load_node_sum(0)
+        load_node_sum(1)
+        load_e(1)
+        load_node_sum(2)
+        load_node_sum(3)
+        load_planes(planes_b, 2, W_m2_scales, 0, 2)
+        load_words(w2_words, W_m2_words, 0, 2)
+        nc.sync.dma_start(out=mask_bf16[:], in_=adj_mask.rearrange("b i j o -> i b (j o)"))
+        nc.sync.dma_start(out=b2_all[:], in_=b_m2.partition_broadcast(P))
+        for j in range(E_CHUNK):
+            quantise_rows(sorted_e[j], e_codes[:, j, :], e_planes[:, j, :])
+        nc.vector.tensor_copy(out=mask_f32[:], in_=mask_bf16[:])
+        nc.vector.reduce_sum(out=degree[:], in_=mask_f32[:], axis=mybir.AxisListType.X)
+        nc.vector.scalar_tensor_tensor(
+            out=result[:], in0=b2_all[:], scalar=degree[:, 0:1], in1=h_rows[:], op0=MULT, op1=ADD
+        )
+        for step in range(NODES + 2):
+            if step < NODES:
+                first_layer(step)
+            if 1 <= step <= NODES:
+                quantise_hidden(step - 1)
+            if E_CHUNK <= step + E_LEAD < NODES:
+                j = step + E_LEAD
+                quantise_rows(sorted_e[j], e_codes[:, j, :], e_planes[:, j, :])
+            if E_CHUNK <= step + E_LEAD + 1 < NODES:
+                j = step + E_LEAD + 1
+                sorted_e[j] = sort_words(e_rows[:, j, :])
+            if step + SUM_LEAD < NODES:
+                load_node_sum(step + SUM_LEAD)
+            if step % E_CHUNK == 0 and step + 2 * E_CHUNK < NODES:
+                load_e(step // E_CHUNK + 2)
+            if step >= 2:
+                second_layer(step - 2)
+
+        nc.sync.dma_start(out=out.rearrange("b i n -> i b n"), in_=result[:])

@@ -56,8 +56,10 @@ def tile_messagepassing_pa_kernel(
         h_planes = keep.tile([P, PASSES * P], U8, align_bytes=64)
         e_codes = keep.tile([P, NODES, PASSES * P], U32, align_bytes=64)
         e_planes = keep.tile([P, NODES, PASSES * P], U8, align_bytes=64)
-        b1_all = keep.tile([P, WIDTH], BF16)
-        b2_all = keep.tile([P, WIDTH], BF16)
+        ones = keep.tile([P, P], BF16)
+        bias_rows = keep.tile([P, 2, WIDTH], BF16)
+        b1_all = keep.tile([P, WIDTH], F32)
+        b2_all = keep.tile([P, WIDTH], F32)
         mask_bf16 = keep.tile([P, NODES], BF16)
         mask_f32 = keep.tile([P, NODES], F32)
         degree = keep.tile([P, 1], F32)
@@ -69,6 +71,8 @@ def tile_messagepassing_pa_kernel(
         make_identity(nc, ident_bf16[:])
         nc.vector.memset(planes_a[:].bitcast(I32), 0)
         nc.vector.memset(planes_b[:].bitcast(I32), 0)
+        nc.vector.memset(bias_rows[:].rearrange("r v n -> r (v n)").bitcast(I32), 0)
+        nc.vector.memset(ones[:], 1.0)
 
         def load_words(tile, dram, first, count):
             nc.sync.dma_start(
@@ -87,14 +91,15 @@ def tile_messagepassing_pa_kernel(
         def load_e(chunk):
             nc.sync.dma_start(
                 out=e_rows[:, E_CHUNK * chunk : E_CHUNK * (chunk + 1), :].rearrange("r j k -> r (j k)"),
-                in_=e[:, :, E_CHUNK * chunk : E_CHUNK * (chunk + 1), :].rearrange("b i j k -> i b (j k)"),
+                in_=e[:, :, E_CHUNK * chunk : E_CHUNK * (chunk + 1), :].rearrange("b i j k -> (b i) (j k)"),
             )
 
-        nc.sync.dma_start(out=h_rows[:], in_=h.rearrange("b i k -> i b k"))
+        nc.sync.dma_start(out=h_rows[:], in_=h.rearrange("b i k -> (b i) k"))
         load_planes(planes_a, 0, W_m1_scales, 0, 4)
         load_words(w1_words, W_m1_words, 2, 2)
         load_words(w1_words, W_m1_words, 0, 2)
-        nc.sync.dma_start(out=b1_all[:], in_=b_m1.partition_broadcast(P))
+        nc.sync.dma_start(out=bias_rows[0:1, 0, :], in_=b_m1.unsqueeze(0))
+        nc.sync.dma_start(out=bias_rows[0:1, 1, :], in_=b_m2.unsqueeze(0))
         load_e(0)
 
         def sort_words(rows):
@@ -130,6 +135,18 @@ def tile_messagepassing_pa_kernel(
                     stop=(c == PASSES - 1),
                 )
 
+        def spread_bias(which, spread):
+            for half in range(HALVES):
+                bias_bank = banks.tile([P, N_TILE], F32, tag="bank")
+                nc.tensor.matmul(
+                    out=bias_bank[:],
+                    lhsT=ones[:],
+                    rhs=bias_rows[:, which, N_TILE * half : N_TILE * (half + 1)],
+                    start=True,
+                    stop=True,
+                )
+                nc.scalar.copy(out=spread[:, N_TILE * half : N_TILE * (half + 1)], in_=bias_bank[:])
+
         def by_slot(ap):
             return ap.rearrange("r (p t) -> r t p", t=PACK)
 
@@ -143,6 +160,7 @@ def tile_messagepassing_pa_kernel(
                 nc.vector.tensor_copy(out=source_term[:, half], in_=by_slot(source_bank[:]))
         scratch = out.rearrange("b i n -> (b i) n")
         nc.sync.dma_start(out=scratch, in_=source_term[:].rearrange("r g t p -> r (g t p)"))
+        spread_bias(0, b1_all)
         for half in range(HALVES):
             target_bank = banks.tile([P, N_TILE], F32, tag="bank")
             mx_product(target_bank, h_codes[:], h_planes[:], w1_words, 0, planes_a, 0, half)
@@ -161,7 +179,7 @@ def tile_messagepassing_pa_kernel(
             node_sum = sums.tile([P, HALVES, PACK, P], F32)
             nc.sync.dma_start(
                 out=node_sum[:].rearrange("r g t p -> r (g t p)"),
-                in_=scratch[GRAPHS * j : GRAPHS * (j + 1), :].unsqueeze(0).to_broadcast([NODES, GRAPHS, WIDTH]),
+                in_=out[:, j, :].unsqueeze(1).to_broadcast([GRAPHS, NODES, WIDTH]),
             )
             for half in range(HALVES):
                 nc.gpsimd.tensor_tensor(
@@ -215,10 +233,10 @@ def tile_messagepassing_pa_kernel(
         load_node_sum(3)
         load_planes(planes_b, 2, W_m2_scales, 0, 2)
         load_words(w2_words, W_m2_words, 0, 2)
-        nc.sync.dma_start(out=mask_bf16[:], in_=adj_mask.rearrange("b i j o -> i b (j o)"))
-        nc.sync.dma_start(out=b2_all[:], in_=b_m2.partition_broadcast(P))
+        nc.sync.dma_start(out=mask_bf16[:], in_=adj_mask.rearrange("b i j o -> (b i) (j o)"))
         for j in range(E_CHUNK):
             quantise_rows(sorted_e[j], e_codes[:, j, :], e_planes[:, j, :])
+        spread_bias(1, b2_all)
         nc.vector.tensor_copy(out=mask_f32[:], in_=mask_bf16[:])
         nc.vector.reduce_sum(out=degree[:], in_=mask_f32[:], axis=mybir.AxisListType.X)
         nc.vector.scalar_tensor_tensor(
@@ -242,4 +260,4 @@ def tile_messagepassing_pa_kernel(
             if step >= 2:
                 second_layer(step - 2)
 
-        nc.sync.dma_start(out=out.rearrange("b i n -> i b n"), in_=result[:])
+        nc.sync.dma_start(out=scratch, in_=result[:])

@@ -27,6 +27,7 @@ QUADRANT = 32
 E_CHUNK = 4
 E_LEAD = 2
 SUM_LEAD = 4
+ADD_LEAD = 2
 
 FLOPS = 2 * (2 * GRAPHS * NODES * NODES + 2 * GRAPHS * NODES) * WIDTH * WIDTH
 
@@ -181,11 +182,10 @@ def tile_messagepassing_pa_kernel(
                 out=node_sum[:].rearrange("r g t p -> r (g t p)"),
                 in_=out[:, j, :].unsqueeze(1).to_broadcast([GRAPHS, NODES, WIDTH]),
             )
-            for half in range(HALVES):
-                nc.gpsimd.tensor_tensor(
-                    out=node_sum[:, half], in0=node_sum[:, half], in1=target_term[:, half], op=ADD
-                )
             node_sums[j] = node_sum
+
+        def add_target_term(j):
+            nc.vector.tensor_tensor(out=node_sums[j][:], in0=node_sums[j][:], in1=target_term[:], op=ADD)
 
         def first_layer(j):
             pre_relu = stage.tile([P, HALVES, PACK, P], BF16)
@@ -233,6 +233,8 @@ def tile_messagepassing_pa_kernel(
         load_node_sum(3)
         load_planes(planes_b, 2, W_m2_scales, 0, 2)
         load_words(w2_words, W_m2_words, 0, 2)
+        for j in range(ADD_LEAD):
+            add_target_term(j)
         nc.sync.dma_start(out=mask_bf16[:], in_=adj_mask.rearrange("b i j o -> (b i) (j o)"))
         for j in range(E_CHUNK):
             quantise_rows(sorted_e[j], e_codes[:, j, :], e_planes[:, j, :])
@@ -253,6 +255,8 @@ def tile_messagepassing_pa_kernel(
             if E_CHUNK <= step + E_LEAD + 1 < NODES:
                 j = step + E_LEAD + 1
                 sorted_e[j] = sort_words(e_rows[:, j, :])
+            if step + ADD_LEAD < NODES:
+                add_target_term(step + ADD_LEAD)
             if step + SUM_LEAD < NODES:
                 load_node_sum(step + SUM_LEAD)
             if step % E_CHUNK == 0 and step + 2 * E_CHUNK < NODES:

@@ -27,7 +27,6 @@ QUADRANT = 32
 E_CHUNK = 4
 E_LEAD = 2
 SUM_LEAD = 4
-ADD_LEAD = 2
 
 FLOPS = 2 * (2 * GRAPHS * NODES * NODES + 2 * GRAPHS * NODES) * WIDTH * WIDTH
 
@@ -64,8 +63,8 @@ def tile_messagepassing_pa_kernel(
         mask_bf16 = keep.tile([P, NODES], BF16)
         mask_f32 = keep.tile([P, NODES], F32)
         degree = keep.tile([P, 1], F32)
-        target_term = keep.tile([P, HALVES, PACK, P], F32)
-        source_term = keep.tile([P, HALVES, PACK, P], F32)
+        target_term = keep.tile([P, HALVES, N_TILE], F32)
+        source_term = keep.tile([P, HALVES, N_TILE], F32)
         result = keep.tile([P, WIDTH], F32)
 
         make_identity(nc, ident_f32[:])
@@ -148,27 +147,25 @@ def tile_messagepassing_pa_kernel(
                 )
                 nc.scalar.copy(out=spread[:, N_TILE * half : N_TILE * (half + 1)], in_=bias_bank[:])
 
-        def by_slot(ap):
-            return ap.rearrange("r (p t) -> r t p", t=PACK)
 
         quantise_rows(sort_words(h_rows[:]), h_codes[:], h_planes[:])
         for half in range(HALVES):
             source_bank = banks.tile([P, N_TILE], F32, tag="bank")
             mx_product(source_bank, h_codes[:], h_planes[:], w1_words, 2, planes_a, 2, half)
             if half == 0:
-                nc.scalar.copy(out=source_term[:, half], in_=by_slot(source_bank[:]))
+                nc.scalar.copy(out=source_term[:, half], in_=source_bank[:])
             else:
-                nc.vector.tensor_copy(out=source_term[:, half], in_=by_slot(source_bank[:]))
+                nc.vector.tensor_copy(out=source_term[:, half], in_=source_bank[:])
         scratch = out.rearrange("b i n -> (b i) n")
-        nc.sync.dma_start(out=scratch, in_=source_term[:].rearrange("r g t p -> r (g t p)"))
+        nc.sync.dma_start(out=scratch, in_=source_term[:].rearrange("r g n -> r (g n)"))
         spread_bias(0, b1_all)
         for half in range(HALVES):
             target_bank = banks.tile([P, N_TILE], F32, tag="bank")
             mx_product(target_bank, h_codes[:], h_planes[:], w1_words, 0, planes_a, 0, half)
             nc.vector.tensor_tensor(
                 out=target_term[:, half],
-                in0=by_slot(target_bank[:]),
-                in1=by_slot(b1_all[:, N_TILE * half : N_TILE * (half + 1)]),
+                in0=target_bank[:],
+                in1=b1_all[:, N_TILE * half : N_TILE * (half + 1)],
                 op=ADD,
             )
 
@@ -177,15 +174,16 @@ def tile_messagepassing_pa_kernel(
         r_operands = {}
 
         def load_node_sum(j):
-            node_sum = sums.tile([P, HALVES, PACK, P], F32)
+            node_sum = sums.tile([P, HALVES, N_TILE], F32)
             nc.sync.dma_start(
-                out=node_sum[:].rearrange("r g t p -> r (g t p)"),
+                out=node_sum[:].rearrange("r g n -> r (g n)"),
                 in_=out[:, j, :].unsqueeze(1).to_broadcast([GRAPHS, NODES, WIDTH]),
             )
+            for half in range(HALVES):
+                nc.gpsimd.tensor_tensor(
+                    out=node_sum[:, half], in0=node_sum[:, half], in1=target_term[:, half], op=ADD
+                )
             node_sums[j] = node_sum
-
-        def add_target_term(j):
-            nc.vector.tensor_tensor(out=node_sums[j][:], in0=node_sums[j][:], in1=target_term[:], op=ADD)
 
         def first_layer(j):
             pre_relu = stage.tile([P, HALVES, PACK, P], BF16)
@@ -193,7 +191,10 @@ def tile_messagepassing_pa_kernel(
                 edge_bank = banks.tile([P, N_TILE], F32, tag="bank")
                 mx_product(edge_bank, e_codes[:, j, :], e_planes[:, j, :], w1_words, 4, planes_b, 0, half)
                 nc.vector.tensor_tensor(
-                    out=pre_relu[:, half], in0=by_slot(edge_bank[:]), in1=node_sums[j][:, half], op=ADD
+                    out=pre_relu[:, half].rearrange("r t p -> r p t"),
+                    in0=edge_bank[:].rearrange("r (p t) -> r p t", t=PACK),
+                    in1=node_sums[j][:, half].rearrange("r (p t) -> r p t", t=PACK),
+                    op=ADD,
                 )
             pre_relus[j] = pre_relu
 
@@ -233,8 +234,6 @@ def tile_messagepassing_pa_kernel(
         load_node_sum(3)
         load_planes(planes_b, 2, W_m2_scales, 0, 2)
         load_words(w2_words, W_m2_words, 0, 2)
-        for j in range(ADD_LEAD):
-            add_target_term(j)
         nc.sync.dma_start(out=mask_bf16[:], in_=adj_mask.rearrange("b i j o -> (b i) (j o)"))
         for j in range(E_CHUNK):
             quantise_rows(sorted_e[j], e_codes[:, j, :], e_planes[:, j, :])
@@ -255,8 +254,6 @@ def tile_messagepassing_pa_kernel(
             if E_CHUNK <= step + E_LEAD + 1 < NODES:
                 j = step + E_LEAD + 1
                 sorted_e[j] = sort_words(e_rows[:, j, :])
-            if step + ADD_LEAD < NODES:
-                add_target_term(step + ADD_LEAD)
             if step + SUM_LEAD < NODES:
                 load_node_sum(step + SUM_LEAD)
             if step % E_CHUNK == 0 and step + 2 * E_CHUNK < NODES:

@@ -100,6 +100,7 @@ def tile_messagepassing_pa_kernel(
         load_words(w1_words, W_m1_words, 0, 2)
         nc.sync.dma_start(out=bias_rows[0:1, 0, :], in_=b_m1.unsqueeze(0))
         nc.sync.dma_start(out=bias_rows[0:1, 1, :], in_=b_m2.unsqueeze(0))
+        nc.sync.dma_start(out=mask_bf16[:], in_=adj_mask.rearrange("b i j o -> (b i) (j o)"))
         load_e(0)
 
         def sort_words(rows):
@@ -234,7 +235,6 @@ def tile_messagepassing_pa_kernel(
         load_node_sum(3)
         load_planes(planes_b, 2, W_m2_scales, 0, 2)
         load_words(w2_words, W_m2_words, 0, 2)
-        nc.sync.dma_start(out=mask_bf16[:], in_=adj_mask.rearrange("b i j o -> (b i) (j o)"))
         for j in range(E_CHUNK):
             quantise_rows(sorted_e[j], e_codes[:, j, :], e_planes[:, j, :])
         spread_bias(1, b2_all)

@@ -24,9 +24,7 @@ N_TILE = 512
 HALVES = WIDTH // N_TILE
 PLANE_ROWS = 4
 QUADRANT = 32
-E_CHUNK = 4
-E_LEAD = 2
-SUM_LEAD = 4
+SUM_LEAD = 6
 
 FLOPS = 2 * (2 * GRAPHS * NODES * NODES + 2 * GRAPHS * NODES) * WIDTH * WIDTH
 
@@ -38,18 +36,20 @@ def tile_messagepassing_pa_kernel(
     with ExitStack() as stack:
         keep = stack.enter_context(tc.tile_pool(name="keep", bufs=1))
         stage = stack.enter_context(tc.tile_pool(name="stage", bufs=3))
-        sorts = stack.enter_context(tc.tile_pool(name="sorts", bufs=E_CHUNK + 1))
+        sorts = stack.enter_context(tc.tile_pool(name="sorts", bufs=5))
         sums = stack.enter_context(tc.tile_pool(name="sums", bufs=SUM_LEAD + 2))
-        banks = stack.enter_context(tc.psum_pool(name="banks", bufs=5))
-        flips = stack.enter_context(tc.psum_pool(name="flips", bufs=3))
+        banks = stack.enter_context(tc.psum_pool(name="banks", bufs=6))
+        flips = stack.enter_context(tc.psum_pool(name="flips", bufs=2))
         stack.enter_context(tc.manual_schedule())
 
         ident_f32 = keep.tile([P, P], F32)
-        ident_bf16 = keep.tile([P, P], BF16)
         h_rows = keep.tile([P, WIDTH], BF16)
         e_rows = keep.tile([P, NODES, WIDTH], BF16)
-        w1_words = keep.tile([P, 3 * PASSES, PACK * WIDTH], U8, align_bytes=64)
-        w2_words = keep.tile([P, PASSES, PACK * WIDTH], U8, align_bytes=64)
+        w1_raw = keep.tile([P, 3 * PASSES, WIDTH], I32)
+        w1_words = keep.tile([P, 3 * PASSES, WIDTH], I32, align_bytes=64)
+        w2_words = keep.tile([P, PASSES, WIDTH], I32, align_bytes=64)
+        planes_a_raw = keep.tile([P, WIDTH], U8, align_bytes=64)
+        planes_b_raw = keep.tile([P, WIDTH], U8, align_bytes=64)
         planes_a = keep.tile([P, WIDTH], U8, align_bytes=64)
         planes_b = keep.tile([P, WIDTH], U8, align_bytes=64)
         h_codes = keep.tile([P, PASSES * P], U32, align_bytes=64)
@@ -57,28 +57,24 @@ def tile_messagepassing_pa_kernel(
         e_codes = keep.tile([P, NODES, PASSES * P], U32, align_bytes=64)
         e_planes = keep.tile([P, NODES, PASSES * P], U8, align_bytes=64)
         ones = keep.tile([P, P], BF16)
-        bias_rows = keep.tile([P, 2, WIDTH], BF16)
-        b1_all = keep.tile([P, WIDTH], F32)
+        bias_row = keep.tile([P, WIDTH], BF16)
+        b1_cols = keep.tile([P, HALVES, PACK], BF16)
         b2_all = keep.tile([P, WIDTH], F32)
         mask_bf16 = keep.tile([P, NODES], BF16)
         mask_f32 = keep.tile([P, NODES], F32)
         degree = keep.tile([P, 1], F32)
-        target_term = keep.tile([P, HALVES, N_TILE], F32)
-        source_term = keep.tile([P, HALVES, N_TILE], F32)
+        target_term = keep.tile([P, HALVES, P, PACK], F32)
+        source_term = keep.tile([P, HALVES, P, PACK], F32)
         result = keep.tile([P, WIDTH], F32)
 
         make_identity(nc, ident_f32[:])
-        make_identity(nc, ident_bf16[:])
-        nc.vector.memset(planes_a[:].bitcast(I32), 0)
-        nc.vector.memset(planes_b[:].bitcast(I32), 0)
-        nc.vector.memset(bias_rows[:].rearrange("r v n -> r (v n)").bitcast(I32), 0)
+        nc.vector.memset(planes_a_raw[:].bitcast(I32), 0)
+        nc.vector.memset(planes_b_raw[:].bitcast(I32), 0)
+        nc.vector.memset(bias_row[:].bitcast(I32), 0)
         nc.vector.memset(ones[:], 1.0)
 
-        def load_words(tile, dram, first, count):
-            nc.sync.dma_start(
-                out=tile[:, first : first + count, :].bitcast(I32),
-                in_=dram[first : first + count].rearrange("g p n t -> p g (n t)").bitcast(I32),
-            )
+        def load_words(tile, dram, group):
+            nc.sync.dma_start(out=tile[:, group, :], in_=dram[group].rearrange("p n t -> p (n t)").bitcast(I32))
 
         def load_planes(tile, first_plane, dram, first, count):
             for q in range(P // QUADRANT):
@@ -88,20 +84,30 @@ def tile_messagepassing_pa_kernel(
                     in_=dram[first : first + count, PLANE_ROWS * q : PLANE_ROWS * (q + 1), :].bitcast(I32),
                 )
 
-        def load_e(chunk):
+        def load_e(first, count):
             nc.sync.dma_start(
-                out=e_rows[:, E_CHUNK * chunk : E_CHUNK * (chunk + 1), :].rearrange("r j k -> r (j k)"),
-                in_=e[:, :, E_CHUNK * chunk : E_CHUNK * (chunk + 1), :].rearrange("b i j k -> (b i) (j k)"),
+                out=e_rows[:, first : first + count, :].rearrange("r j k -> r (j k)"),
+                in_=e[:, :, first : first + count, :].rearrange("b i j k -> (b i) (j k)"),
             )
 
         nc.sync.dma_start(out=h_rows[:], in_=h.rearrange("b i k -> (b i) k"))
-        load_planes(planes_a, 0, W_m1_scales, 0, 4)
-        load_words(w1_words, W_m1_words, 2, 2)
-        load_words(w1_words, W_m1_words, 0, 2)
-        nc.sync.dma_start(out=bias_rows[0:1, 0, :], in_=b_m1.unsqueeze(0))
-        nc.sync.dma_start(out=bias_rows[0:1, 1, :], in_=b_m2.unsqueeze(0))
+        load_planes(planes_a_raw, 0, W_m1_scales, 0, 4)
+        load_planes(planes_b_raw, 0, W_m1_scales, 4, 2)
+        load_planes(planes_b_raw, 2, W_m2_scales, 0, 2)
+        nc.sync.dma_start(out=bias_row[0:1, :], in_=b_m2.unsqueeze(0))
         nc.sync.dma_start(out=mask_bf16[:], in_=adj_mask.rearrange("b i j o -> (b i) (j o)"))
-        load_e(0)
+        nc.sync.dma_start(out=b1_cols[:], in_=b_m1.rearrange("(a p t) -> p a t", a=HALVES, t=PACK))
+        for group in (2, 3, 0, 1):
+            load_words(w1_raw, W_m1_words, group)
+        load_e(0, 2)
+        for group in (4, 5):
+            load_words(w1_raw, W_m1_words, group)
+        load_e(2, 2)
+        for group in range(PASSES):
+            load_words(w2_words, W_m2_words, group)
+        load_e(4, 4)
+        load_e(8, 4)
+        load_e(12, 4)
 
         def sort_words(rows):
             sorted_words = sorts.tile([P, PASSES, 2, P], F32)
@@ -110,155 +116,204 @@ def tile_messagepassing_pa_kernel(
             )
             return sorted_words
 
-        def quantise_rows(sorted_words, codes, planes):
+        def flip_rows(sorted_words):
             flipped = flips.tile([P, PASSES, 2, P], F32, tag="flip")
             for c in range(PASSES):
                 for u in range(2):
                     nc.tensor.transpose(flipped[:, c, u, :], sorted_words[:, c, u, :], ident_f32[:])
-            grouped = stage.tile([P, PASSES, P, PACK], BF16, align_bytes=64)
-            flat = grouped[:].rearrange("p c r t -> p (c r t)")
+            return flipped
+
+        def group_rows(flipped):
+            grouped = stage.tile([P, PASSES * P * PACK], BF16, align_bytes=64)
             nc.scalar.copy(
-                out=flat.bitcast(F32).rearrange("p (c r u) -> p c r u", c=PASSES, u=2),
+                out=grouped[:].bitcast(F32).rearrange("p (c r u) -> p c r u", c=PASSES, u=2),
                 in_=flipped[:].rearrange("p c u r -> p c r u"),
             )
-            nc.vector.quantize_mx(out=codes.bitcast(FP8X4), scales=planes, in_=flat)
+            return grouped
 
-        def mx_product(bank, codes, planes, words, first_group, w_planes, first_plane, half):
-            for c in range(PASSES):
-                row = PLANE_ROWS * (first_plane + c)
-                nc.tensor.matmul_mx(
-                    out=bank[:],
-                    lhsT=codes[:, P * c : P * (c + 1)].bitcast(FP8X4),
-                    lhsT_scale=planes[:, P * c : P * (c + 1)],
-                    rhs=words[:, first_group + c, PACK * N_TILE * half : PACK * N_TILE * (half + 1)].bitcast(FP8X4),
-                    rhs_scale=w_planes[row:P, N_TILE * half : N_TILE * (half + 1)],
-                    start=(c == 0),
-                    stop=(c == PASSES - 1),
-                )
+        def permute_words(group):
+            nc.vector.tensor_copy(
+                out=w1_words[:, group, :].rearrange("p (a t m) -> p a t m", a=HALVES, t=PACK),
+                in_=w1_raw[:, group, :].rearrange("p (a m t) -> p a t m", a=HALVES, t=PACK),
+            )
 
-        def spread_bias(which, spread):
-            for half in range(HALVES):
-                bias_bank = banks.tile([P, N_TILE], F32, tag="bank")
-                nc.tensor.matmul(
-                    out=bias_bank[:],
-                    lhsT=ones[:],
-                    rhs=bias_rows[:, which, N_TILE * half : N_TILE * (half + 1)],
-                    start=True,
-                    stop=True,
-                )
-                nc.scalar.copy(out=spread[:, N_TILE * half : N_TILE * (half + 1)], in_=bias_bank[:])
+        def permute_planes(engine, permuted, raw):
+            engine.tensor_copy(
+                out=permuted[:].rearrange("p (a t m) -> p a m t", a=HALVES, t=PACK),
+                in_=raw[:].rearrange("p (a m t) -> p a m t", a=HALVES, t=PACK),
+            )
 
+        def channel_product(first_group, w_planes, first_plane, a, codes, planes):
+            bank = banks.tile([P, PACK, P], F32, tag="bank")
+            for t in range(PACK):
+                first = P * (PACK * a + t)
+                for c in range(PASSES):
+                    row = PLANE_ROWS * (first_plane + c)
+                    nc.tensor.matmul_mx(
+                        out=bank[:, t, :],
+                        lhsT=w1_words[:, first_group + c, first : first + P].bitcast(FP8X4),
+                        lhsT_scale=w_planes[row:P, first : first + P],
+                        rhs=codes[:, P * c : P * (c + 1)].bitcast(FP8X4),
+                        rhs_scale=planes[:, P * c : P * (c + 1)],
+                        start=(c == 0),
+                        stop=(c == PASSES - 1),
+                    )
+            return bank
 
-        quantise_rows(sort_words(h_rows[:]), h_codes[:], h_planes[:])
+        h_grouped = group_rows(flip_rows(sort_words(h_rows[:])))
+        nc.vector.quantize_mx(out=h_codes[:].bitcast(FP8X4), scales=h_planes[:], in_=h_grouped[:])
+        permute_planes(nc.vector, planes_a, planes_a_raw)
+        permute_planes(nc.gpsimd, planes_b, planes_b_raw)
+
         for half in range(HALVES):
-            source_bank = banks.tile([P, N_TILE], F32, tag="bank")
-            mx_product(source_bank, h_codes[:], h_planes[:], w1_words, 2, planes_a, 2, half)
-            if half == 0:
-                nc.scalar.copy(out=source_term[:, half], in_=source_bank[:])
-            else:
-                nc.vector.tensor_copy(out=source_term[:, half], in_=source_bank[:])
-        scratch = out.rearrange("b i n -> (b i) n")
-        nc.sync.dma_start(out=scratch, in_=source_term[:].rearrange("r g n -> r (g n)"))
-        spread_bias(0, b1_all)
-        for half in range(HALVES):
-            target_bank = banks.tile([P, N_TILE], F32, tag="bank")
-            mx_product(target_bank, h_codes[:], h_planes[:], w1_words, 0, planes_a, 0, half)
-            nc.vector.tensor_tensor(
-                out=target_term[:, half],
-                in0=target_bank[:],
-                in1=b1_all[:, N_TILE * half : N_TILE * (half + 1)],
-                op=ADD,
+            bias_bank = banks.tile([P, N_TILE], F32, tag="bank")
+            nc.tensor.matmul(
+                out=bias_bank[:],
+                lhsT=ones[:],
+                rhs=bias_row[:, N_TILE * half : N_TILE * (half + 1)],
+                start=True,
+                stop=True,
             )
-
-        node_sums = {}
-        pre_relus = {}
-        r_operands = {}
-
-        def load_node_sum(j):
-            node_sum = sums.tile([P, HALVES, N_TILE], F32)
-            nc.sync.dma_start(
-                out=node_sum[:].rearrange("r g n -> r (g n)"),
-                in_=out[:, j, :].unsqueeze(1).to_broadcast([GRAPHS, NODES, WIDTH]),
-            )
-            for half in range(HALVES):
-                nc.gpsimd.tensor_tensor(
-                    out=node_sum[:, half], in0=node_sum[:, half], in1=target_term[:, half], op=ADD
-                )
-            node_sums[j] = node_sum
-
-        def first_layer(j):
-            pre_relu = stage.tile([P, HALVES, PACK, P], BF16)
-            for half in range(HALVES):
-                edge_bank = banks.tile([P, N_TILE], F32, tag="bank")
-                mx_product(edge_bank, e_codes[:, j, :], e_planes[:, j, :], w1_words, 4, planes_b, 0, half)
-                nc.vector.tensor_tensor(
-                    out=pre_relu[:, half].rearrange("r t p -> r p t"),
-                    in0=edge_bank[:].rearrange("r (p t) -> r p t", t=PACK),
-                    in1=node_sums[j][:, half].rearrange("r (p t) -> r p t", t=PACK),
-                    op=ADD,
-                )
-            pre_relus[j] = pre_relu
-
-        def quantise_hidden(j):
-            flipped = flips.tile([P, PASSES, PACK, P], BF16, tag="flip")
-            for c in range(PASSES):
-                for t in range(PACK):
-                    nc.tensor.transpose(flipped[:, c, t, :], pre_relus[j][:, c, t, :], ident_bf16[:])
-            hidden = stage.tile([P, PASSES, P, PACK], BF16, align_bytes=64)
-            nc.scalar.activation(out=hidden[:], in_=flipped[:].rearrange("p c t r -> p c r t"), func=RELU)
-            r_codes = stage.tile([P, PASSES * P], U32, align_bytes=64)
-            r_planes = stage.tile([P, PASSES * P], U8, align_bytes=64)
-            nc.vector.quantize_mx(
-                out=r_codes[:].bitcast(FP8X4), scales=r_planes[:], in_=hidden[:].rearrange("p c r t -> p (c r t)")
-            )
-            r_operands[j] = (r_codes, r_planes)
-
-        def second_layer(j):
-            r_codes, r_planes = r_operands[j]
-            for half in range(HALVES):
-                message_bank = banks.tile([P, N_TILE], F32, tag="bank")
-                mx_product(message_bank, r_codes[:], r_planes[:], w2_words, 0, planes_b, 2, half)
-                columns = result[:, N_TILE * half : N_TILE * (half + 1)]
-                nc.vector.scalar_tensor_tensor(
-                    out=columns, in0=message_bank[:], scalar=mask_f32[:, j : j + 1], in1=columns, op0=MULT, op1=ADD
-                )
-
-        sorted_e = {}
-        for j in range(E_CHUNK):
-            sorted_e[j] = sort_words(e_rows[:, j, :])
-        load_planes(planes_b, 0, W_m1_scales, 4, 2)
-        load_words(w1_words, W_m1_words, 4, 2)
-        load_node_sum(0)
-        load_node_sum(1)
-        load_e(1)
-        load_node_sum(2)
-        load_node_sum(3)
-        load_planes(planes_b, 2, W_m2_scales, 0, 2)
-        load_words(w2_words, W_m2_words, 0, 2)
-        for j in range(E_CHUNK):
-            quantise_rows(sorted_e[j], e_codes[:, j, :], e_planes[:, j, :])
-        spread_bias(1, b2_all)
+            nc.scalar.copy(out=b2_all[:, N_TILE * half : N_TILE * (half + 1)], in_=bias_bank[:])
         nc.vector.tensor_copy(out=mask_f32[:], in_=mask_bf16[:])
         nc.vector.reduce_sum(out=degree[:], in_=mask_f32[:], axis=mybir.AxisListType.X)
         nc.vector.scalar_tensor_tensor(
             out=result[:], in0=b2_all[:], scalar=degree[:, 0:1], in1=h_rows[:], op0=MULT, op1=ADD
         )
-        for step in range(NODES + 2):
-            if step < NODES:
-                first_layer(step)
-            if 1 <= step <= NODES:
-                quantise_hidden(step - 1)
-            if E_CHUNK <= step + E_LEAD < NODES:
-                j = step + E_LEAD
-                quantise_rows(sorted_e[j], e_codes[:, j, :], e_planes[:, j, :])
-            if E_CHUNK <= step + E_LEAD + 1 < NODES:
-                j = step + E_LEAD + 1
-                sorted_e[j] = sort_words(e_rows[:, j, :])
-            if step + SUM_LEAD < NODES:
-                load_node_sum(step + SUM_LEAD)
-            if step % E_CHUNK == 0 and step + 2 * E_CHUNK < NODES:
-                load_e(step // E_CHUNK + 2)
-            if step >= 2:
-                second_layer(step - 2)
 
-        nc.sync.dma_start(out=scratch, in_=result[:])
+        permute_words(2)
+        permute_words(3)
+        for a in range(HALVES):
+            source_bank = channel_product(2, planes_a, 2, a, h_codes[:], h_planes[:])
+            nc.scalar.copy(out=source_term[:, a], in_=source_bank[:].rearrange("p t r -> p r t"))
+        permute_words(0)
+        permute_words(1)
+        for a in range(HALVES):
+            target_bank = channel_product(0, planes_a, 0, a, h_codes[:], h_planes[:])
+            nc.vector.tensor_tensor(
+                out=target_term[:, a],
+                in0=target_bank[:].rearrange("p t r -> p r t"),
+                in1=b1_cols[:, a, :].unsqueeze(1).to_broadcast([P, P, PACK]),
+                op=ADD,
+            )
+
+        node_sums = {}
+        sorted_e = {}
+        flipped_e = {}
+        edge_banks = {}
+        r_operands = {}
+        message_banks = {}
+
+        def sum_node_terms(j):
+            node_sum = sums.tile([P, HALVES, P, PACK], F32)
+            nc.gpsimd.tensor_tensor(
+                out=node_sum[:].rearrange("p a (b i) t -> p (a b) i t", i=NODES),
+                in0=target_term[:].rearrange("p a (b i) t -> p (a b) i t", i=NODES),
+                in1=source_term[:]
+                .rearrange("p a (b j) t -> p (a b) j t", j=NODES)[:, :, j, :]
+                .unsqueeze(2)
+                .to_broadcast([P, HALVES * GRAPHS, NODES, PACK]),
+                op=ADD,
+            )
+            node_sums[j] = node_sum
+
+        def first_layer(j):
+            edge_banks[j] = []
+            for a in range(HALVES):
+                edge_banks[j].append(channel_product(4, planes_b, 0, a, e_codes[:, j, :], e_planes[:, j, :]))
+
+        def add_and_relu(j):
+            pre_relu = stage.tile([P, HALVES, P, PACK], BF16)
+            for a in range(HALVES):
+                nc.vector.tensor_tensor(
+                    out=pre_relu[:, a],
+                    in0=edge_banks[j][a][:].rearrange("p t r -> p r t"),
+                    in1=node_sums[j][:, a],
+                    op=ADD,
+                )
+            hidden = stage.tile([P, WIDTH], BF16, align_bytes=64)
+            nc.scalar.activation(out=hidden[:], in_=pre_relu[:].rearrange("p a r t -> p (a r t)"), func=RELU)
+            return hidden
+
+        def quantise_hidden(j, hidden):
+            r_codes = stage.tile([P, PASSES * P], U32, align_bytes=64)
+            r_planes = stage.tile([P, PASSES * P], U8, align_bytes=64)
+            nc.vector.quantize_mx(out=r_codes[:].bitcast(FP8X4), scales=r_planes[:], in_=hidden[:])
+            r_operands[j] = (r_codes, r_planes)
+
+        def second_layer(j):
+            r_codes, r_planes = r_operands[j]
+            message_banks[j] = []
+            for half in range(HALVES):
+                message_bank = banks.tile([P, N_TILE], F32, tag="bank")
+                for c in range(PASSES):
+                    row = PLANE_ROWS * (2 + c)
+                    nc.tensor.matmul_mx(
+                        out=message_bank[:],
+                        lhsT=r_codes[:, P * c : P * (c + 1)].bitcast(FP8X4),
+                        lhsT_scale=r_planes[:, P * c : P * (c + 1)],
+                        rhs=w2_words[:, c, N_TILE * half : N_TILE * (half + 1)].bitcast(FP8X4),
+                        rhs_scale=planes_b_raw[row:P, N_TILE * half : N_TILE * (half + 1)],
+                        start=(c == 0),
+                        stop=(c == PASSES - 1),
+                    )
+                message_banks[j].append(message_bank)
+
+        def gather_messages(j, half):
+            columns = result[:, N_TILE * half : N_TILE * (half + 1)]
+            nc.vector.scalar_tensor_tensor(
+                out=columns,
+                in0=message_banks[j][half][:],
+                scalar=mask_f32[:, j : j + 1],
+                in1=columns,
+                op0=MULT,
+                op1=ADD,
+            )
+
+        for j in range(SUM_LEAD):
+            sum_node_terms(j)
+        for j in range(4):
+            sorted_e[j] = sort_words(e_rows[:, j, :])
+        grouped_e = {}
+        flipped_e[0] = flip_rows(sorted_e[0])
+        grouped_e[0] = group_rows(flipped_e[0])
+        flipped_e[1] = flip_rows(sorted_e[1])
+        grouped_e[1] = group_rows(flipped_e[1])
+        flipped_e[2] = flip_rows(sorted_e[2])
+        for j in range(2):
+            nc.vector.quantize_mx(out=e_codes[:, j, :].bitcast(FP8X4), scales=e_planes[:, j, :], in_=grouped_e[j][:])
+        permute_words(4)
+        permute_words(5)
+        first_layer(0)
+
+        scratch = out.rearrange("b i n -> (b i) n")
+        for step in range(NODES + 1):
+            if step + 2 < NODES:
+                grouped_e[step + 2] = group_rows(flipped_e[step + 2])
+            if step + 4 < NODES:
+                sorted_e[step + 4] = sort_words(e_rows[:, step + 4, :])
+            if step >= 1:
+                second_layer(step - 1)
+            if step < NODES:
+                hidden = add_and_relu(step)
+            if step >= 1:
+                for half in range(HALVES):
+                    gather_messages(step - 1, half)
+                    if step == NODES:
+                        nc.sync.dma_start(
+                            out=scratch[:, N_TILE * half : N_TILE * (half + 1)],
+                            in_=result[:, N_TILE * half : N_TILE * (half + 1)],
+                        )
+            if step + 1 < NODES:
+                first_layer(step + 1)
+            if step + 3 < NODES:
+                flipped_e[step + 3] = flip_rows(sorted_e[step + 3])
+            if step + 2 < NODES:
+                j = step + 2
+                nc.vector.quantize_mx(
+                    out=e_codes[:, j, :].bitcast(FP8X4), scales=e_planes[:, j, :], in_=grouped_e[j][:]
+                )
+            if step < NODES:
+                quantise_hidden(step, hidden)
+            if step + SUM_LEAD < NODES:
+                sum_node_terms(step + SUM_LEAD)

@@ -24,7 +24,7 @@ N_TILE = 512
 HALVES = WIDTH // N_TILE
 PLANE_ROWS = 4
 QUADRANT = 32
-SUM_LEAD = 6
+SUM_LEAD = 2
 
 FLOPS = 2 * (2 * GRAPHS * NODES * NODES + 2 * GRAPHS * NODES) * WIDTH * WIDTH
 
@@ -37,7 +37,7 @@ def tile_messagepassing_pa_kernel(
         keep = stack.enter_context(tc.tile_pool(name="keep", bufs=1))
         stage = stack.enter_context(tc.tile_pool(name="stage", bufs=3))
         sorts = stack.enter_context(tc.tile_pool(name="sorts", bufs=5))
-        sums = stack.enter_context(tc.tile_pool(name="sums", bufs=SUM_LEAD + 2))
+        sums = stack.enter_context(tc.tile_pool(name="sums", bufs=SUM_LEAD * HALVES))
         banks = stack.enter_context(tc.psum_pool(name="banks", bufs=6))
         flips = stack.enter_context(tc.psum_pool(name="flips", bufs=2))
         stack.enter_context(tc.manual_schedule())
@@ -103,9 +103,10 @@ def tile_messagepassing_pa_kernel(
         for group in (4, 5):
             load_words(w1_raw, W_m1_words, group)
         load_e(2, 2)
+        load_e(4, 2)
         for group in range(PASSES):
             load_words(w2_words, W_m2_words, group)
-        load_e(4, 4)
+        load_e(6, 2)
         load_e(8, 4)
         load_e(12, 4)
 
@@ -204,18 +205,18 @@ def tile_messagepassing_pa_kernel(
         r_operands = {}
         message_banks = {}
 
-        def sum_node_terms(j):
-            node_sum = sums.tile([P, HALVES, P, PACK], F32)
+        def sum_node_terms(j, a):
+            node_sum = sums.tile([P, P, PACK], F32)
             nc.gpsimd.tensor_tensor(
-                out=node_sum[:].rearrange("p a (b i) t -> p (a b) i t", i=NODES),
-                in0=target_term[:].rearrange("p a (b i) t -> p (a b) i t", i=NODES),
-                in1=source_term[:]
-                .rearrange("p a (b j) t -> p (a b) j t", j=NODES)[:, :, j, :]
+                out=node_sum[:].rearrange("p (b i) t -> p b i t", i=NODES),
+                in0=target_term[:, a].rearrange("p (b i) t -> p b i t", i=NODES),
+                in1=source_term[:, a]
+                .rearrange("p (b j) t -> p b j t", j=NODES)[:, :, j, :]
                 .unsqueeze(2)
-                .to_broadcast([P, HALVES * GRAPHS, NODES, PACK]),
+                .to_broadcast([P, GRAPHS, NODES, PACK]),
                 op=ADD,
             )
-            node_sums[j] = node_sum
+            node_sums[(j, a)] = node_sum
 
         def first_layer(j):
             edge_banks[j] = []
@@ -224,15 +225,21 @@ def tile_messagepassing_pa_kernel(
 
         def add_and_relu(j):
             pre_relu = stage.tile([P, HALVES, P, PACK], BF16)
+            hidden = stage.tile([P, WIDTH], BF16, align_bytes=64)
             for a in range(HALVES):
                 nc.vector.tensor_tensor(
                     out=pre_relu[:, a],
                     in0=edge_banks[j][a][:].rearrange("p t r -> p r t"),
-                    in1=node_sums[j][:, a],
+                    in1=node_sums[(j, a)][:],
                     op=ADD,
                 )
-            hidden = stage.tile([P, WIDTH], BF16, align_bytes=64)
-            nc.scalar.activation(out=hidden[:], in_=pre_relu[:].rearrange("p a r t -> p (a r t)"), func=RELU)
+                nc.scalar.activation(
+                    out=hidden[:, N_TILE * a : N_TILE * (a + 1)],
+                    in_=pre_relu[:, a].rearrange("p r t -> p (r t)"),
+                    func=RELU,
+                )
+                if j + SUM_LEAD < NODES:
+                    sum_node_terms(j + SUM_LEAD, a)
             return hidden
 
         def quantise_hidden(j, hidden):
@@ -270,32 +277,40 @@ def tile_messagepassing_pa_kernel(
                 op1=ADD,
             )
 
+        def quantise_edges(j):
+            nc.vector.quantize_mx(out=e_codes[:, j, :].bitcast(FP8X4), scales=e_planes[:, j, :], in_=grouped_e[j][:])
+
         for j in range(SUM_LEAD):
-            sum_node_terms(j)
+            for a in range(HALVES):
+                sum_node_terms(j, a)
         for j in range(4):
             sorted_e[j] = sort_words(e_rows[:, j, :])
         grouped_e = {}
-        flipped_e[0] = flip_rows(sorted_e[0])
-        grouped_e[0] = group_rows(flipped_e[0])
-        flipped_e[1] = flip_rows(sorted_e[1])
-        grouped_e[1] = group_rows(flipped_e[1])
-        flipped_e[2] = flip_rows(sorted_e[2])
-        for j in range(2):
-            nc.vector.quantize_mx(out=e_codes[:, j, :].bitcast(FP8X4), scales=e_planes[:, j, :], in_=grouped_e[j][:])
+        hiddens = {}
+        for j in range(3):
+            flipped_e[j] = flip_rows(sorted_e[j])
+            grouped_e[j] = group_rows(flipped_e[j])
+        flipped_e[3] = flip_rows(sorted_e[3])
+        quantise_edges(0)
+        quantise_edges(1)
         permute_words(4)
         permute_words(5)
         first_layer(0)
+        sorted_e[4] = sort_words(e_rows[:, 4, :])
 
         scratch = out.rearrange("b i n -> (b i) n")
         for step in range(NODES + 1):
+            if step + 3 < NODES:
+                grouped_e[step + 3] = group_rows(flipped_e[step + 3])
+            if step + 5 < NODES:
+                sorted_e[step + 5] = sort_words(e_rows[:, step + 5, :])
             if step + 2 < NODES:
-                grouped_e[step + 2] = group_rows(flipped_e[step + 2])
-            if step + 4 < NODES:
-                sorted_e[step + 4] = sort_words(e_rows[:, step + 4, :])
+                quantise_edges(step + 2)
             if step >= 1:
+                quantise_hidden(step - 1, hiddens[step - 1])
                 second_layer(step - 1)
             if step < NODES:
-                hidden = add_and_relu(step)
+                hiddens[step] = add_and_relu(step)
             if step >= 1:
                 for half in range(HALVES):
                     gather_messages(step - 1, half)
@@ -306,14 +321,5 @@ def tile_messagepassing_pa_kernel(
                         )
             if step + 1 < NODES:
                 first_layer(step + 1)
-            if step + 3 < NODES:
-                flipped_e[step + 3] = flip_rows(sorted_e[step + 3])
-            if step + 2 < NODES:
-                j = step + 2
-                nc.vector.quantize_mx(
-                    out=e_codes[:, j, :].bitcast(FP8X4), scales=e_planes[:, j, :], in_=grouped_e[j][:]
-                )
-            if step < NODES:
-                quantise_hidden(step, hidden)
-            if step + SUM_LEAD < NODES:
-                sum_node_terms(step + SUM_LEAD)
+            if step + 4 < NODES:
+                flipped_e[step + 4] = flip_rows(sorted_e[step + 4])

@@ -37,7 +37,7 @@ def tile_messagepassing_pa_kernel(
         keep = stack.enter_context(tc.tile_pool(name="keep", bufs=1))
         stage = stack.enter_context(tc.tile_pool(name="stage", bufs=3))
         sorts = stack.enter_context(tc.tile_pool(name="sorts", bufs=5))
-        sums = stack.enter_context(tc.tile_pool(name="sums", bufs=SUM_LEAD * HALVES))
+        sums = stack.enter_context(tc.tile_pool(name="sums", bufs=(SUM_LEAD + 1) * HALVES))
         banks = stack.enter_context(tc.psum_pool(name="banks", bufs=6))
         flips = stack.enter_context(tc.psum_pool(name="flips", bufs=2))
         stack.enter_context(tc.manual_schedule())
@@ -205,18 +205,21 @@ def tile_messagepassing_pa_kernel(
         r_operands = {}
         message_banks = {}
 
-        def sum_node_terms(j, a):
-            node_sum = sums.tile([P, P, PACK], F32)
-            nc.gpsimd.tensor_tensor(
-                out=node_sum[:].rearrange("p (b i) t -> p b i t", i=NODES),
-                in0=target_term[:, a].rearrange("p (b i) t -> p b i t", i=NODES),
-                in1=source_term[:, a]
-                .rearrange("p (b j) t -> p b j t", j=NODES)[:, :, j, :]
-                .unsqueeze(2)
-                .to_broadcast([P, GRAPHS, NODES, PACK]),
-                op=ADD,
-            )
-            node_sums[(j, a)] = node_sum
+        def sum_node_terms(j, gated):
+            for a in range(HALVES):
+                source = source_term[:, a].rearrange("p (b j) t -> p b j t", j=NODES)[:, :, j, :]
+                if gated and a == 0:
+                    handed = stage.tile([P, GRAPHS, PACK], F32)
+                    nc.vector.tensor_copy(out=handed[:], in_=source)
+                    source = handed[:]
+                node_sum = sums.tile([P, P, PACK], F32)
+                nc.gpsimd.tensor_tensor(
+                    out=node_sum[:].rearrange("p (b i) t -> p b i t", i=NODES),
+                    in0=target_term[:, a].rearrange("p (b i) t -> p b i t", i=NODES),
+                    in1=source.unsqueeze(2).to_broadcast([P, GRAPHS, NODES, PACK]),
+                    op=ADD,
+                )
+                node_sums[(j, a)] = node_sum
 
         def first_layer(j):
             edge_banks[j] = []
@@ -238,8 +241,6 @@ def tile_messagepassing_pa_kernel(
                     in_=pre_relu[:, a].rearrange("p r t -> p (r t)"),
                     func=RELU,
                 )
-                if j + SUM_LEAD < NODES:
-                    sum_node_terms(j + SUM_LEAD, a)
             return hidden
 
         def quantise_hidden(j, hidden):
@@ -281,8 +282,7 @@ def tile_messagepassing_pa_kernel(
             nc.vector.quantize_mx(out=e_codes[:, j, :].bitcast(FP8X4), scales=e_planes[:, j, :], in_=grouped_e[j][:])
 
         for j in range(SUM_LEAD):
-            for a in range(HALVES):
-                sum_node_terms(j, a)
+            sum_node_terms(j, False)
         for j in range(4):
             sorted_e[j] = sort_words(e_rows[:, j, :])
         grouped_e = {}
@@ -309,6 +309,8 @@ def tile_messagepassing_pa_kernel(
             if step >= 1:
                 quantise_hidden(step - 1, hiddens[step - 1])
                 second_layer(step - 1)
+            if step + SUM_LEAD < NODES:
+                sum_node_terms(step + SUM_LEAD, True)
             if step < NODES:
                 hiddens[step] = add_and_relu(step)
             if step >= 1:

@@ -49,9 +49,10 @@ def tile_messagepassing_pa_kernel(
         w1_words = keep.tile([P, 3 * PASSES, WIDTH], I32, align_bytes=64)
         w2_words = keep.tile([P, PASSES, WIDTH], I32, align_bytes=64)
         planes_a_raw = keep.tile([P, WIDTH], U8, align_bytes=64)
-        planes_b_raw = keep.tile([P, WIDTH], U8, align_bytes=64)
+        planes_e_raw = keep.tile([P, WIDTH], U8, align_bytes=64)
         planes_a = keep.tile([P, WIDTH], U8, align_bytes=64)
-        planes_b = keep.tile([P, WIDTH], U8, align_bytes=64)
+        planes_e = keep.tile([P, WIDTH], U8, align_bytes=64)
+        planes_2 = keep.tile([P, WIDTH], U8, align_bytes=64)
         h_codes = keep.tile([P, PASSES * P], U32, align_bytes=64)
         h_planes = keep.tile([P, PASSES * P], U8, align_bytes=64)
         e_codes = keep.tile([P, NODES, PASSES * P], U32, align_bytes=64)
@@ -69,9 +70,10 @@ def tile_messagepassing_pa_kernel(
 
         make_identity(nc, ident_f32[:])
         nc.vector.memset(planes_a_raw[:].bitcast(I32), 0)
-        nc.vector.memset(planes_b_raw[:].bitcast(I32), 0)
         nc.vector.memset(bias_row[:].bitcast(I32), 0)
         nc.vector.memset(ones[:], 1.0)
+        nc.vector.memset(planes_e_raw[:].bitcast(I32), 0)
+        nc.vector.memset(planes_2[:].bitcast(I32), 0)
 
         def load_words(tile, dram, group):
             nc.sync.dma_start(out=tile[:, group, :], in_=dram[group].rearrange("p n t -> p (n t)").bitcast(I32))
@@ -92,16 +94,16 @@ def tile_messagepassing_pa_kernel(
 
         nc.sync.dma_start(out=h_rows[:], in_=h.rearrange("b i k -> (b i) k"))
         load_planes(planes_a_raw, 0, W_m1_scales, 0, 4)
-        load_planes(planes_b_raw, 0, W_m1_scales, 4, 2)
-        load_planes(planes_b_raw, 2, W_m2_scales, 0, 2)
-        nc.sync.dma_start(out=bias_row[0:1, :], in_=b_m2.unsqueeze(0))
-        nc.sync.dma_start(out=mask_bf16[:], in_=adj_mask.rearrange("b i j o -> (b i) (j o)"))
-        nc.sync.dma_start(out=b1_cols[:], in_=b_m1.rearrange("(a p t) -> p a t", a=HALVES, t=PACK))
         for group in (2, 3, 0, 1):
             load_words(w1_raw, W_m1_words, group)
+        nc.sync.dma_start(out=b1_cols[:], in_=b_m1.rearrange("(a p t) -> p a t", a=HALVES, t=PACK))
+        nc.sync.dma_start(out=mask_bf16[:], in_=adj_mask.rearrange("b i j o -> (b i) (j o)"))
+        nc.sync.dma_start(out=bias_row[0:1, :], in_=b_m2.unsqueeze(0))
+        load_planes(planes_e_raw, 0, W_m1_scales, 4, 2)
         load_e(0, 2)
         for group in (4, 5):
             load_words(w1_raw, W_m1_words, group)
+        load_planes(planes_2, 0, W_m2_scales, 0, 2)
         load_e(2, 2)
         load_e(4, 2)
         for group in range(PASSES):
@@ -164,23 +166,7 @@ def tile_messagepassing_pa_kernel(
         h_grouped = group_rows(flip_rows(sort_words(h_rows[:])))
         nc.vector.quantize_mx(out=h_codes[:].bitcast(FP8X4), scales=h_planes[:], in_=h_grouped[:])
         permute_planes(nc.vector, planes_a, planes_a_raw)
-        permute_planes(nc.gpsimd, planes_b, planes_b_raw)
-
-        for half in range(HALVES):
-            bias_bank = banks.tile([P, N_TILE], F32, tag="bank")
-            nc.tensor.matmul(
-                out=bias_bank[:],
-                lhsT=ones[:],
-                rhs=bias_row[:, N_TILE * half : N_TILE * (half + 1)],
-                start=True,
-                stop=True,
-            )
-            nc.scalar.copy(out=b2_all[:, N_TILE * half : N_TILE * (half + 1)], in_=bias_bank[:])
-        nc.vector.tensor_copy(out=mask_f32[:], in_=mask_bf16[:])
-        nc.vector.reduce_sum(out=degree[:], in_=mask_f32[:], axis=mybir.AxisListType.X)
-        nc.vector.scalar_tensor_tensor(
-            out=result[:], in0=b2_all[:], scalar=degree[:, 0:1], in1=h_rows[:], op0=MULT, op1=ADD
-        )
+        permute_planes(nc.gpsimd, planes_e, planes_e_raw)
 
         permute_words(2)
         permute_words(3)
@@ -197,6 +183,22 @@ def tile_messagepassing_pa_kernel(
                 in1=b1_cols[:, a, :].unsqueeze(1).to_broadcast([P, P, PACK]),
                 op=ADD,
             )
+
+        for half in range(HALVES):
+            bias_bank = banks.tile([P, N_TILE], F32, tag="bank")
+            nc.tensor.matmul(
+                out=bias_bank[:],
+                lhsT=ones[:],
+                rhs=bias_row[:, N_TILE * half : N_TILE * (half + 1)],
+                start=True,
+                stop=True,
+            )
+            nc.scalar.copy(out=b2_all[:, N_TILE * half : N_TILE * (half + 1)], in_=bias_bank[:])
+        nc.vector.tensor_copy(out=mask_f32[:], in_=mask_bf16[:])
+        nc.vector.reduce_sum(out=degree[:], in_=mask_f32[:], axis=mybir.AxisListType.X)
+        nc.vector.scalar_tensor_tensor(
+            out=result[:], in0=b2_all[:], scalar=degree[:, 0:1], in1=h_rows[:], op0=MULT, op1=ADD
+        )
 
         node_sums = {}
         sorted_e = {}
@@ -224,7 +226,7 @@ def tile_messagepassing_pa_kernel(
         def first_layer(j):
             edge_banks[j] = []
             for a in range(HALVES):
-                edge_banks[j].append(channel_product(4, planes_b, 0, a, e_codes[:, j, :], e_planes[:, j, :]))
+                edge_banks[j].append(channel_product(4, planes_e, 0, a, e_codes[:, j, :], e_planes[:, j, :]))
 
         def add_and_relu(j):
             pre_relu = stage.tile([P, HALVES, P, PACK], BF16)
@@ -255,13 +257,13 @@ def tile_messagepassing_pa_kernel(
             for half in range(HALVES):
                 message_bank = banks.tile([P, N_TILE], F32, tag="bank")
                 for c in range(PASSES):
-                    row = PLANE_ROWS * (2 + c)
+                    row = PLANE_ROWS * c
                     nc.tensor.matmul_mx(
                         out=message_bank[:],
                         lhsT=r_codes[:, P * c : P * (c + 1)].bitcast(FP8X4),
                         lhsT_scale=r_planes[:, P * c : P * (c + 1)],
                         rhs=w2_words[:, c, N_TILE * half : N_TILE * (half + 1)].bitcast(FP8X4),
-                        rhs_scale=planes_b_raw[row:P, N_TILE * half : N_TILE * (half + 1)],
+                        rhs_scale=planes_2[row:P, N_TILE * half : N_TILE * (half + 1)],
                         start=(c == 0),
                         stop=(c == PASSES - 1),
                     )

@@ -25,6 +25,7 @@ HALVES = WIDTH // N_TILE
 PLANE_ROWS = 4
 QUADRANT = 32
 SUM_LEAD = 2
+VECTOR_BLOCKS = 4
 
 FLOPS = 2 * (2 * GRAPHS * NODES * NODES + 2 * GRAPHS * NODES) * WIDTH * WIDTH
 
@@ -37,7 +38,7 @@ def tile_messagepassing_pa_kernel(
         keep = stack.enter_context(tc.tile_pool(name="keep", bufs=1))
         stage = stack.enter_context(tc.tile_pool(name="stage", bufs=3))
         sorts = stack.enter_context(tc.tile_pool(name="sorts", bufs=5))
-        sums = stack.enter_context(tc.tile_pool(name="sums", bufs=(SUM_LEAD + 1) * HALVES))
+        sums = stack.enter_context(tc.tile_pool(name="sums", bufs=SUM_LEAD + 1))
         banks = stack.enter_context(tc.psum_pool(name="banks", bufs=6))
         flips = stack.enter_context(tc.psum_pool(name="flips", bufs=2))
         stack.enter_context(tc.manual_schedule())
@@ -208,20 +209,30 @@ def tile_messagepassing_pa_kernel(
         message_banks = {}
 
         def sum_node_terms(j, gated):
-            for a in range(HALVES):
-                source = source_term[:, a].rearrange("p (b j) t -> p b j t", j=NODES)[:, :, j, :]
-                if gated and a == 0:
-                    handed = stage.tile([P, GRAPHS, PACK], F32)
-                    nc.vector.tensor_copy(out=handed[:], in_=source)
-                    source = handed[:]
-                node_sum = sums.tile([P, P, PACK], F32)
-                nc.gpsimd.tensor_tensor(
-                    out=node_sum[:].rearrange("p (b i) t -> p b i t", i=NODES),
-                    in0=target_term[:, a].rearrange("p (b i) t -> p b i t", i=NODES),
-                    in1=source.unsqueeze(2).to_broadcast([P, GRAPHS, NODES, PACK]),
+            blocks = HALVES * GRAPHS
+            source = source_term[:].rearrange("p a (b j) t -> p (a b) j t", j=NODES)[:, :, j, :]
+            node_sum = sums.tile([P, HALVES, P, PACK], F32)
+            summed = node_sum[:].rearrange("p a (b i) t -> p (a b) i t", i=NODES)
+            target = target_term[:].rearrange("p a (b i) t -> p (a b) i t", i=NODES)
+            first = 0
+            if gated:
+                first = VECTOR_BLOCKS
+                nc.vector.tensor_tensor(
+                    out=summed[:, :first],
+                    in0=target[:, :first],
+                    in1=source[:, :first].unsqueeze(2).to_broadcast([P, first, NODES, PACK]),
                     op=ADD,
                 )
-                node_sums[(j, a)] = node_sum
+                handed = stage.tile([P, blocks, PACK], F32)
+                nc.vector.tensor_copy(out=handed[:, first:], in_=source[:, first:])
+                source = handed[:]
+            nc.gpsimd.tensor_tensor(
+                out=summed[:, first:],
+                in0=target[:, first:],
+                in1=source[:, first:].unsqueeze(2).to_broadcast([P, blocks - first, NODES, PACK]),
+                op=ADD,
+            )
+            node_sums[j] = node_sum
 
         def first_layer(j):
             edge_banks[j] = []
@@ -235,7 +246,7 @@ def tile_messagepassing_pa_kernel(
                 nc.vector.tensor_tensor(
                     out=pre_relu[:, a],
                     in0=edge_banks[j][a][:].rearrange("p t r -> p r t"),
-                    in1=node_sums[(j, a)][:],
+                    in1=node_sums[j][:, a],
                     op=ADD,
                 )
                 nc.scalar.activation(

@@ -25,7 +25,7 @@ HALVES = WIDTH // N_TILE
 PLANE_ROWS = 4
 QUADRANT = 32
 SUM_LEAD = 2
-VECTOR_BLOCKS = 4
+VECTOR_BLOCKS = 2
 
 FLOPS = 2 * (2 * GRAPHS * NODES * NODES + 2 * GRAPHS * NODES) * WIDTH * WIDTH
 

@@ -24,7 +24,9 @@ N_TILE = 512
 HALVES = WIDTH // N_TILE
 PLANE_ROWS = 4
 QUADRANT = 32
-SUM_LEAD = 2
+BLOCKS = HALVES * GRAPHS
+SUM_LEAD = 1
+UNSORTED = 5
 VECTOR_BLOCKS = 2
 
 FLOPS = 2 * (2 * GRAPHS * NODES * NODES + 2 * GRAPHS * NODES) * WIDTH * WIDTH
@@ -37,7 +39,7 @@ def tile_messagepassing_pa_kernel(
     with ExitStack() as stack:
         keep = stack.enter_context(tc.tile_pool(name="keep", bufs=1))
         stage = stack.enter_context(tc.tile_pool(name="stage", bufs=3))
-        sorts = stack.enter_context(tc.tile_pool(name="sorts", bufs=5))
+        sorts = stack.enter_context(tc.tile_pool(name="sorts", bufs=4))
         sums = stack.enter_context(tc.tile_pool(name="sums", bufs=SUM_LEAD + 1))
         banks = stack.enter_context(tc.psum_pool(name="banks", bufs=6))
         flips = stack.enter_context(tc.psum_pool(name="flips", bufs=2))
@@ -46,12 +48,11 @@ def tile_messagepassing_pa_kernel(
         ident_f32 = keep.tile([P, P], F32)
         h_rows = keep.tile([P, WIDTH], BF16)
         e_rows = keep.tile([P, NODES, WIDTH], BF16)
-        w1_raw = keep.tile([P, 3 * PASSES, WIDTH], I32)
         w1_words = keep.tile([P, 3 * PASSES, WIDTH], I32, align_bytes=64)
+        we_words = keep.tile([P, PASSES, WIDTH], I32, align_bytes=64)
         w2_words = keep.tile([P, PASSES, WIDTH], I32, align_bytes=64)
-        planes_a_raw = keep.tile([P, WIDTH], U8, align_bytes=64)
+        planes_n = keep.tile([P, WIDTH], U8, align_bytes=64)
         planes_e_raw = keep.tile([P, WIDTH], U8, align_bytes=64)
-        planes_a = keep.tile([P, WIDTH], U8, align_bytes=64)
         planes_e = keep.tile([P, WIDTH], U8, align_bytes=64)
         planes_2 = keep.tile([P, WIDTH], U8, align_bytes=64)
         h_codes = keep.tile([P, PASSES * P], U32, align_bytes=64)
@@ -61,7 +62,6 @@ def tile_messagepassing_pa_kernel(
         ones = keep.tile([P, P], BF16)
         bias_row = keep.tile([P, WIDTH], BF16)
         b1_cols = keep.tile([P, HALVES, PACK], BF16)
-        b2_all = keep.tile([P, WIDTH], F32)
         mask_bf16 = keep.tile([P, NODES], BF16)
         mask_f32 = keep.tile([P, NODES], F32)
         degree = keep.tile([P, 1], F32)
@@ -70,20 +70,19 @@ def tile_messagepassing_pa_kernel(
         result = keep.tile([P, WIDTH], F32)
 
         make_identity(nc, ident_f32[:])
-        nc.vector.memset(planes_a_raw[:].bitcast(I32), 0)
+        nc.vector.memset(planes_n[:].bitcast(I32), 0)
+        nc.vector.memset(planes_e_raw[:].bitcast(I32), 0)
         nc.vector.memset(bias_row[:].bitcast(I32), 0)
         nc.vector.memset(ones[:], 1.0)
-        nc.vector.memset(planes_e_raw[:].bitcast(I32), 0)
         nc.vector.memset(planes_2[:].bitcast(I32), 0)
 
         def load_words(tile, dram, group):
             nc.sync.dma_start(out=tile[:, group, :], in_=dram[group].rearrange("p n t -> p (n t)").bitcast(I32))
 
-        def load_planes(tile, first_plane, dram, first, count):
+        def load_planes(tile, dram, first, count):
             for q in range(P // QUADRANT):
-                row = QUADRANT * q + PLANE_ROWS * first_plane
                 nc.sync.dma_start(
-                    out=tile[row : row + PLANE_ROWS * count, :].bitcast(I32),
+                    out=tile[QUADRANT * q : QUADRANT * q + PLANE_ROWS * count, :].bitcast(I32),
                     in_=dram[first : first + count, PLANE_ROWS * q : PLANE_ROWS * (q + 1), :].bitcast(I32),
                 )
 
@@ -94,17 +93,18 @@ def tile_messagepassing_pa_kernel(
             )
 
         nc.sync.dma_start(out=h_rows[:], in_=h.rearrange("b i k -> (b i) k"))
-        load_planes(planes_a_raw, 0, W_m1_scales, 0, 4)
-        for group in (2, 3, 0, 1):
-            load_words(w1_raw, W_m1_words, group)
+        load_planes(planes_n, W_m1_scales, 0, 4)
+        for group in (2, 3, 0):
+            load_words(w1_words, W_m1_words, group)
+        load_planes(planes_e_raw, W_m1_scales, 4, 2)
         nc.sync.dma_start(out=b1_cols[:], in_=b_m1.rearrange("(a p t) -> p a t", a=HALVES, t=PACK))
-        nc.sync.dma_start(out=mask_bf16[:], in_=adj_mask.rearrange("b i j o -> (b i) (j o)"))
-        nc.sync.dma_start(out=bias_row[0:1, :], in_=b_m2.unsqueeze(0))
-        load_planes(planes_e_raw, 0, W_m1_scales, 4, 2)
+        load_words(w1_words, W_m1_words, 1)
         load_e(0, 2)
         for group in (4, 5):
-            load_words(w1_raw, W_m1_words, group)
-        load_planes(planes_2, 0, W_m2_scales, 0, 2)
+            load_words(w1_words, W_m1_words, group)
+        nc.sync.dma_start(out=mask_bf16[:], in_=adj_mask.rearrange("b i j o -> (b i) (j o)"))
+        nc.sync.dma_start(out=bias_row[0:1, :], in_=b_m2.unsqueeze(0))
+        load_planes(planes_2, W_m2_scales, 0, 2)
         load_e(2, 2)
         load_e(4, 2)
         for group in range(PASSES):
@@ -127,6 +127,14 @@ def tile_messagepassing_pa_kernel(
                     nc.tensor.transpose(flipped[:, c, u, :], sorted_words[:, c, u, :], ident_f32[:])
             return flipped
 
+        def flip_unsorted_rows(rows):
+            words = rows.bitcast(F32)
+            flipped = flips.tile([P, PASSES, 2, P], F32, tag="flip")
+            for c in range(PASSES):
+                for u in range(2):
+                    nc.tensor.transpose(flipped[:, c, u, :], words[:, 2 * P * c + u : 2 * P * (c + 1) : 2], ident_f32[:])
+            return flipped
+
         def group_rows(flipped):
             grouped = stage.tile([P, PASSES * P * PACK], BF16, align_bytes=64)
             nc.scalar.copy(
@@ -135,109 +143,111 @@ def tile_messagepassing_pa_kernel(
             )
             return grouped
 
-        def permute_words(group):
-            nc.vector.tensor_copy(
-                out=w1_words[:, group, :].rearrange("p (a t m) -> p a t m", a=HALVES, t=PACK),
-                in_=w1_raw[:, group, :].rearrange("p (a m t) -> p a t m", a=HALVES, t=PACK),
-            )
-
-        def permute_planes(engine, permuted, raw):
-            engine.tensor_copy(
-                out=permuted[:].rearrange("p (a t m) -> p a m t", a=HALVES, t=PACK),
-                in_=raw[:].rearrange("p (a m t) -> p a m t", a=HALVES, t=PACK),
-            )
-
-        def channel_product(first_group, w_planes, first_plane, a, codes, planes):
-            bank = banks.tile([P, PACK, P], F32, tag="bank")
-            for t in range(PACK):
-                first = P * (PACK * a + t)
-                for c in range(PASSES):
-                    row = PLANE_ROWS * (first_plane + c)
-                    nc.tensor.matmul_mx(
-                        out=bank[:, t, :],
-                        lhsT=w1_words[:, first_group + c, first : first + P].bitcast(FP8X4),
-                        lhsT_scale=w_planes[row:P, first : first + P],
-                        rhs=codes[:, P * c : P * (c + 1)].bitcast(FP8X4),
-                        rhs_scale=planes[:, P * c : P * (c + 1)],
-                        start=(c == 0),
-                        stop=(c == PASSES - 1),
-                    )
+        def node_term_rows(first_group, a):
+            bank = banks.tile([P, N_TILE], F32, tag="bank")
+            for c in range(PASSES):
+                row = PLANE_ROWS * (first_group + c)
+                nc.tensor.matmul_mx(
+                    out=bank[:],
+                    lhsT=h_codes[:, P * c : P * (c + 1)].bitcast(FP8X4),
+                    lhsT_scale=h_planes[:, P * c : P * (c + 1)],
+                    rhs=w1_words[:, first_group + c, N_TILE * a : N_TILE * (a + 1)].bitcast(FP8X4),
+                    rhs_scale=planes_n[row:P, N_TILE * a : N_TILE * (a + 1)],
+                    start=(c == 0),
+                    stop=(c == PASSES - 1),
+                )
             return bank
 
-        h_grouped = group_rows(flip_rows(sort_words(h_rows[:])))
-        nc.vector.quantize_mx(out=h_codes[:].bitcast(FP8X4), scales=h_planes[:], in_=h_grouped[:])
-        permute_planes(nc.vector, planes_a, planes_a_raw)
-        permute_planes(nc.gpsimd, planes_e, planes_e_raw)
+        def sort_term(copy, rows_bank):
+            sorted_rows = stage.tile([P, PACK, P], F32)
+            copy(out=sorted_rows[:], in_=rows_bank[:].rearrange("r (p t) -> r t p", t=PACK))
+            return sorted_rows
 
-        permute_words(2)
-        permute_words(3)
-        for a in range(HALVES):
-            source_bank = channel_product(2, planes_a, 2, a, h_codes[:], h_planes[:])
-            nc.scalar.copy(out=source_term[:, a], in_=source_bank[:].rearrange("p t r -> p r t"))
-        permute_words(0)
-        permute_words(1)
-        for a in range(HALVES):
-            target_bank = channel_product(0, planes_a, 0, a, h_codes[:], h_planes[:])
+        def flip_term(sorted_rows):
+            bank = banks.tile([P, PACK, P], F32, tag="bank")
+            for t in range(PACK):
+                nc.tensor.transpose(bank[:, t, :], sorted_rows[:, t, :], ident_f32[:])
+            return bank
+
+        def keep_source(a, bank):
             nc.vector.tensor_tensor(
-                out=target_term[:, a],
-                in0=target_bank[:].rearrange("p t r -> p r t"),
+                out=source_term[:, a],
+                in0=bank[:].rearrange("p t r -> p r t"),
                 in1=b1_cols[:, a, :].unsqueeze(1).to_broadcast([P, P, PACK]),
                 op=ADD,
             )
 
-        for half in range(HALVES):
-            bias_bank = banks.tile([P, N_TILE], F32, tag="bank")
-            nc.tensor.matmul(
-                out=bias_bank[:],
-                lhsT=ones[:],
-                rhs=bias_row[:, N_TILE * half : N_TILE * (half + 1)],
-                start=True,
-                stop=True,
+        def keep_target(a, bank):
+            nc.scalar.copy(out=target_term[:, a], in_=bank[:].rearrange("p t r -> p r t"))
+
+        def permute_words(c, a):
+            nc.vector.tensor_copy(
+                out=we_words[:, c, N_TILE * a : N_TILE * (a + 1)].rearrange("p (t m) -> p t m", t=PACK),
+                in_=w1_words[:, 2 * PASSES + c, N_TILE * a : N_TILE * (a + 1)].rearrange("p (m t) -> p t m", t=PACK),
             )
-            nc.scalar.copy(out=b2_all[:, N_TILE * half : N_TILE * (half + 1)], in_=bias_bank[:])
-        nc.vector.tensor_copy(out=mask_f32[:], in_=mask_bf16[:])
-        nc.vector.reduce_sum(out=degree[:], in_=mask_f32[:], axis=mybir.AxisListType.X)
-        nc.vector.scalar_tensor_tensor(
-            out=result[:], in0=b2_all[:], scalar=degree[:, 0:1], in1=h_rows[:], op0=MULT, op1=ADD
-        )
+
+        def permute_planes(engine, a):
+            engine.tensor_copy(
+                out=planes_e[:, N_TILE * a : N_TILE * (a + 1)].rearrange("p (t m) -> p m t", t=PACK),
+                in_=planes_e_raw[:, N_TILE * a : N_TILE * (a + 1)].rearrange("p (m t) -> p m t", t=PACK),
+            )
 
         node_sums = {}
         sorted_e = {}
         flipped_e = {}
+        grouped_e = {}
         edge_banks = {}
+        hiddens = {}
         r_operands = {}
         message_banks = {}
 
         def sum_node_terms(j, gated):
-            blocks = HALVES * GRAPHS
             source = source_term[:].rearrange("p a (b j) t -> p (a b) j t", j=NODES)[:, :, j, :]
             node_sum = sums.tile([P, HALVES, P, PACK], F32)
             summed = node_sum[:].rearrange("p a (b i) t -> p (a b) i t", i=NODES)
             target = target_term[:].rearrange("p a (b i) t -> p (a b) i t", i=NODES)
-            first = 0
             if gated:
-                first = VECTOR_BLOCKS
                 nc.vector.tensor_tensor(
-                    out=summed[:, :first],
-                    in0=target[:, :first],
-                    in1=source[:, :first].unsqueeze(2).to_broadcast([P, first, NODES, PACK]),
+                    out=summed[:, :VECTOR_BLOCKS],
+                    in0=target[:, :VECTOR_BLOCKS],
+                    in1=source[:, :VECTOR_BLOCKS].unsqueeze(2).to_broadcast([P, VECTOR_BLOCKS, NODES, PACK]),
                     op=ADD,
                 )
-                handed = stage.tile([P, blocks, PACK], F32)
-                nc.vector.tensor_copy(out=handed[:, first:], in_=source[:, first:])
+                handed = stage.tile([P, BLOCKS, PACK], F32)
+                nc.vector.tensor_copy(out=handed[:, VECTOR_BLOCKS:], in_=source[:, VECTOR_BLOCKS:])
                 source = handed[:]
-            nc.gpsimd.tensor_tensor(
-                out=summed[:, first:],
-                in0=target[:, first:],
-                in1=source[:, first:].unsqueeze(2).to_broadcast([P, blocks - first, NODES, PACK]),
-                op=ADD,
-            )
+                cuts = [VECTOR_BLOCKS, BLOCKS]
+            else:
+                cuts = [0, GRAPHS, BLOCKS]
+            for first, last in zip(cuts[:-1], cuts[1:]):
+                nc.gpsimd.tensor_tensor(
+                    out=summed[:, first:last],
+                    in0=target[:, first:last],
+                    in1=source[:, first:last].unsqueeze(2).to_broadcast([P, last - first, NODES, PACK]),
+                    op=ADD,
+                )
             node_sums[j] = node_sum
+
+        def quantise_edges(j):
+            nc.vector.quantize_mx(out=e_codes[:, j, :].bitcast(FP8X4), scales=e_planes[:, j, :], in_=grouped_e[j][:])
 
         def first_layer(j):
             edge_banks[j] = []
             for a in range(HALVES):
-                edge_banks[j].append(channel_product(4, planes_e, 0, a, e_codes[:, j, :], e_planes[:, j, :]))
+                bank = banks.tile([P, PACK, P], F32, tag="bank")
+                for t in range(PACK):
+                    first = P * (PACK * a + t)
+                    for c in range(PASSES):
+                        nc.tensor.matmul_mx(
+                            out=bank[:, t, :],
+                            lhsT=we_words[:, c, first : first + P].bitcast(FP8X4),
+                            lhsT_scale=planes_e[PLANE_ROWS * c : P, first : first + P],
+                            rhs=e_codes[:, j, P * c : P * (c + 1)].bitcast(FP8X4),
+                            rhs_scale=e_planes[:, j, P * c : P * (c + 1)],
+                            start=(c == 0),
+                            stop=(c == PASSES - 1),
+                        )
+                edge_banks[j].append(bank)
 
         def add_and_relu(j):
             pre_relu = stage.tile([P, HALVES, P, PACK], BF16)
@@ -268,13 +278,12 @@ def tile_messagepassing_pa_kernel(
             for half in range(HALVES):
                 message_bank = banks.tile([P, N_TILE], F32, tag="bank")
                 for c in range(PASSES):
-                    row = PLANE_ROWS * c
                     nc.tensor.matmul_mx(
                         out=message_bank[:],
                         lhsT=r_codes[:, P * c : P * (c + 1)].bitcast(FP8X4),
                         lhsT_scale=r_planes[:, P * c : P * (c + 1)],
                         rhs=w2_words[:, c, N_TILE * half : N_TILE * (half + 1)].bitcast(FP8X4),
-                        rhs_scale=planes_2[row:P, N_TILE * half : N_TILE * (half + 1)],
+                        rhs_scale=planes_2[PLANE_ROWS * c : P, N_TILE * half : N_TILE * (half + 1)],
                         start=(c == 0),
                         stop=(c == PASSES - 1),
                     )
@@ -291,34 +300,52 @@ def tile_messagepassing_pa_kernel(
                 op1=ADD,
             )
 
-        def quantise_edges(j):
-            nc.vector.quantize_mx(out=e_codes[:, j, :].bitcast(FP8X4), scales=e_planes[:, j, :], in_=grouped_e[j][:])
-
+        h_grouped = group_rows(flip_unsorted_rows(h_rows[:]))
+        nc.vector.quantize_mx(out=h_codes[:].bitcast(FP8X4), scales=h_planes[:], in_=h_grouped[:])
+        source_rows = [node_term_rows(2, a) for a in range(HALVES)]
+        source_sorted = [sort_term(nc.vector.tensor_copy, source_rows[0]), sort_term(nc.scalar.copy, source_rows[1])]
+        permute_planes(nc.vector, 0)
+        permute_planes(nc.gpsimd, 1)
+        for a in range(HALVES):
+            keep_source(a, flip_term(source_sorted[a]))
+        target_rows = [node_term_rows(0, a) for a in range(HALVES)]
+        target_sorted = [sort_term(nc.scalar.copy, target_rows[0]), sort_term(nc.vector.tensor_copy, target_rows[1])]
+        target_banks = []
+        for a in range(HALVES):
+            target_banks.append(flip_term(target_sorted[a]))
+            flipped_e[a] = flip_unsorted_rows(e_rows[:, a, :])
+        for a in range(HALVES):
+            keep_target(a, target_banks[a])
+            grouped_e[a] = group_rows(flipped_e[a])
         for j in range(SUM_LEAD):
             sum_node_terms(j, False)
-        for j in range(4):
-            sorted_e[j] = sort_words(e_rows[:, j, :])
-        grouped_e = {}
-        hiddens = {}
-        for j in range(3):
-            flipped_e[j] = flip_rows(sorted_e[j])
-            grouped_e[j] = group_rows(flipped_e[j])
-        flipped_e[3] = flip_rows(sorted_e[3])
+        permute_words(0, 0)
+        permute_words(0, 1)
+        permute_words(1, 0)
         quantise_edges(0)
-        quantise_edges(1)
-        permute_words(4)
-        permute_words(5)
+        permute_words(1, 1)
         first_layer(0)
-        sorted_e[4] = sort_words(e_rows[:, 4, :])
+        bias_banks = []
+        for half in range(HALVES):
+            bias_bank = banks.tile([P, N_TILE], F32, tag="bank")
+            nc.tensor.matmul(
+                out=bias_bank[:],
+                lhsT=ones[:],
+                rhs=bias_row[:, N_TILE * half : N_TILE * (half + 1)],
+                start=True,
+                stop=True,
+            )
+            bias_banks.append(bias_bank)
+        flipped_e[2] = flip_unsorted_rows(e_rows[:, 2, :])
 
-        scratch = out.rearrange("b i n -> (b i) n")
+        rows_out = out.rearrange("b i n -> (b i) n")
         for step in range(NODES + 1):
-            if step + 3 < NODES:
-                grouped_e[step + 3] = group_rows(flipped_e[step + 3])
-            if step + 5 < NODES:
-                sorted_e[step + 5] = sort_words(e_rows[:, step + 5, :])
             if step + 2 < NODES:
-                quantise_edges(step + 2)
+                grouped_e[step + 2] = group_rows(flipped_e[step + 2])
+            if UNSORTED <= step + 4 < NODES:
+                sorted_e[step + 4] = sort_words(e_rows[:, step + 4, :])
+            if step + 1 < NODES:
+                quantise_edges(step + 1)
             if step >= 1:
                 quantise_hidden(step - 1, hiddens[step - 1])
                 second_layer(step - 1)
@@ -326,15 +353,29 @@ def tile_messagepassing_pa_kernel(
                 sum_node_terms(step + SUM_LEAD, True)
             if step < NODES:
                 hiddens[step] = add_and_relu(step)
+            if step == 0:
+                nc.vector.tensor_copy(out=mask_f32[:], in_=mask_bf16[:])
+                nc.vector.reduce_sum(out=degree[:], in_=mask_f32[:], axis=mybir.AxisListType.X)
+                for half in range(HALVES):
+                    nc.vector.scalar_tensor_tensor(
+                        out=result[:, N_TILE * half : N_TILE * (half + 1)],
+                        in0=bias_banks[half][:],
+                        scalar=degree[:, 0:1],
+                        in1=h_rows[:, N_TILE * half : N_TILE * (half + 1)],
+                        op0=MULT,
+                        op1=ADD,
+                    )
             if step >= 1:
                 for half in range(HALVES):
                     gather_messages(step - 1, half)
                     if step == NODES:
                         nc.sync.dma_start(
-                            out=scratch[:, N_TILE * half : N_TILE * (half + 1)],
+                            out=rows_out[:, N_TILE * half : N_TILE * (half + 1)],
                             in_=result[:, N_TILE * half : N_TILE * (half + 1)],
                         )
             if step + 1 < NODES:
                 first_layer(step + 1)
-            if step + 4 < NODES:
-                flipped_e[step + 4] = flip_rows(sorted_e[step + 4])
+            if step + 3 < UNSORTED:
+                flipped_e[step + 3] = flip_unsorted_rows(e_rows[:, step + 3, :])
+            elif step + 3 < NODES:
+                flipped_e[step + 3] = flip_rows(sorted_e[step + 3])

@@ -375,7 +375,9 @@ def tile_messagepassing_pa_kernel(
                         )
             if step + 1 < NODES:
                 first_layer(step + 1)
-            if step + 3 < UNSORTED:
-                flipped_e[step + 3] = flip_unsorted_rows(e_rows[:, step + 3, :])
-            elif step + 3 < NODES:
-                flipped_e[step + 3] = flip_rows(sorted_e[step + 3])
+            if step % 2 == 0:
+                for j in range(step + 3, min(step + 5, NODES)):
+                    if j < UNSORTED:
+                        flipped_e[j] = flip_unsorted_rows(e_rows[:, j, :])
+                    else:
+                        flipped_e[j] = flip_rows(sorted_e[j])

@@ -27,7 +27,7 @@ QUADRANT = 32
 BLOCKS = HALVES * GRAPHS
 SUM_LEAD = 1
 UNSORTED = 5
-VECTOR_BLOCKS = 2
+VECTOR_BLOCKS = 3
 
 FLOPS = 2 * (2 * GRAPHS * NODES * NODES + 2 * GRAPHS * NODES) * WIDTH * WIDTH
 
@@ -272,22 +272,43 @@ def tile_messagepassing_pa_kernel(
             nc.vector.quantize_mx(out=r_codes[:].bitcast(FP8X4), scales=r_planes[:], in_=hidden[:])
             r_operands[j] = (r_codes, r_planes)
 
-        def second_layer(j):
+        def message_pass(j, half, c):
             r_codes, r_planes = r_operands[j]
+            nc.tensor.matmul_mx(
+                out=message_banks[j][half][:],
+                lhsT=r_codes[:, P * c : P * (c + 1)].bitcast(FP8X4),
+                lhsT_scale=r_planes[:, P * c : P * (c + 1)],
+                rhs=w2_words[:, c, N_TILE * half : N_TILE * (half + 1)].bitcast(FP8X4),
+                rhs_scale=planes_2[PLANE_ROWS * c : P, N_TILE * half : N_TILE * (half + 1)],
+                start=(c == 0),
+                stop=(c == PASSES - 1),
+            )
+
+        def second_layer(j):
             message_banks[j] = []
             for half in range(HALVES):
                 message_bank = banks.tile([P, N_TILE], F32, tag="bank")
-                for c in range(PASSES):
-                    nc.tensor.matmul_mx(
-                        out=message_bank[:],
-                        lhsT=r_codes[:, P * c : P * (c + 1)].bitcast(FP8X4),
-                        lhsT_scale=r_planes[:, P * c : P * (c + 1)],
-                        rhs=w2_words[:, c, N_TILE * half : N_TILE * (half + 1)].bitcast(FP8X4),
-                        rhs_scale=planes_2[PLANE_ROWS * c : P, N_TILE * half : N_TILE * (half + 1)],
-                        start=(c == 0),
-                        stop=(c == PASSES - 1),
-                    )
                 message_banks[j].append(message_bank)
+                for c in range(PASSES):
+                    message_pass(j, half, c)
+
+        def last_messages(j, hidden):
+            r_codes = stage.tile([P, PASSES * P], U32, align_bytes=64)
+            r_planes = stage.tile([P, PASSES * P], U8, align_bytes=64)
+            r_operands[j] = (r_codes, r_planes)
+            message_banks[j] = []
+            for half in range(HALVES):
+                message_bank = banks.tile([P, N_TILE], F32, tag="bank")
+                message_banks[j].append(message_bank)
+            for c in range(PASSES):
+                nc.vector.quantize_mx(
+                    out=r_codes[:, P * c : P * (c + 1)].bitcast(FP8X4),
+                    scales=r_planes[:, P * c : P * (c + 1)],
+                    in_=hidden[:, K_PASS * c : K_PASS * (c + 1)],
+                )
+                for half in range(HALVES):
+                    message_pass(j, half, c)
+                gather_messages(j - 1, c)
 
         def gather_messages(j, half):
             columns = result[:, N_TILE * half : N_TILE * (half + 1)]
@@ -346,7 +367,7 @@ def tile_messagepassing_pa_kernel(
                 sorted_e[step + 4] = sort_words(e_rows[:, step + 4, :])
             if step + 1 < NODES:
                 quantise_edges(step + 1)
-            if step >= 1:
+            if 1 <= step < NODES:
                 quantise_hidden(step - 1, hiddens[step - 1])
                 second_layer(step - 1)
             if step + SUM_LEAD < NODES:
@@ -365,14 +386,17 @@ def tile_messagepassing_pa_kernel(
                         op0=MULT,
                         op1=ADD,
                     )
-            if step >= 1:
+            if 1 <= step < NODES - 1:
                 for half in range(HALVES):
                     gather_messages(step - 1, half)
-                    if step == NODES:
-                        nc.sync.dma_start(
-                            out=rows_out[:, N_TILE * half : N_TILE * (half + 1)],
-                            in_=result[:, N_TILE * half : N_TILE * (half + 1)],
-                        )
+            if step == NODES:
+                last_messages(NODES - 1, hiddens[NODES - 1])
+                for half in range(HALVES):
+                    gather_messages(NODES - 1, half)
+                    nc.sync.dma_start(
+                        out=rows_out[:, N_TILE * half : N_TILE * (half + 1)],
+                        in_=result[:, N_TILE * half : N_TILE * (half + 1)],
+                    )
             if step + 1 < NODES:
                 first_layer(step + 1)
             if step % 2 == 0:

@@ -25,8 +25,10 @@ HALVES = WIDTH // N_TILE
 PLANE_ROWS = 4
 QUADRANT = 32
 BLOCKS = HALVES * GRAPHS
-SUM_LEAD = 1
-UNSORTED = 5
+LEAD = 1
+TERM = P * PACK
+BLOCK = NODES * PACK
+UNSORTED = 7
 VECTOR_BLOCKS = 3
 
 FLOPS = 2 * (2 * GRAPHS * NODES * NODES + 2 * GRAPHS * NODES) * WIDTH * WIDTH
@@ -40,7 +42,8 @@ def tile_messagepassing_pa_kernel(
         keep = stack.enter_context(tc.tile_pool(name="keep", bufs=1))
         stage = stack.enter_context(tc.tile_pool(name="stage", bufs=3))
         sorts = stack.enter_context(tc.tile_pool(name="sorts", bufs=4))
-        sums = stack.enter_context(tc.tile_pool(name="sums", bufs=SUM_LEAD + 1))
+        sums = stack.enter_context(tc.tile_pool(name="sums", bufs=3))
+        hidden_pool = stack.enter_context(tc.tile_pool(name="hidden", bufs=LEAD + 3))
         banks = stack.enter_context(tc.psum_pool(name="banks", bufs=6))
         flips = stack.enter_context(tc.psum_pool(name="flips", bufs=2))
         stack.enter_context(tc.manual_schedule())
@@ -48,9 +51,11 @@ def tile_messagepassing_pa_kernel(
         ident_f32 = keep.tile([P, P], F32)
         h_rows = keep.tile([P, WIDTH], BF16)
         e_rows = keep.tile([P, NODES, WIDTH], BF16)
-        w1_words = keep.tile([P, 3 * PASSES, WIDTH], I32, align_bytes=64)
-        we_words = keep.tile([P, PASSES, WIDTH], I32, align_bytes=64)
-        w2_words = keep.tile([P, PASSES, WIDTH], I32, align_bytes=64)
+        wi_words = [keep.tile([P, PASSES, N_TILE], I32, align_bytes=64, name=f"wi_{a}") for a in range(HALVES)]
+        wj_words = [keep.tile([P, PASSES, N_TILE], I32, align_bytes=64, name=f"wj_{a}") for a in range(HALVES)]
+        we_raw = [keep.tile([P, PASSES, N_TILE], I32, align_bytes=64, name=f"we_raw_{a}") for a in range(HALVES)]
+        we_words = [keep.tile([P, PASSES, N_TILE], I32, align_bytes=64, name=f"we_{a}") for a in range(HALVES)]
+        w2_words = [keep.tile([P, PASSES, N_TILE], I32, align_bytes=64, name=f"w2_{a}") for a in range(HALVES)]
         planes_n = keep.tile([P, WIDTH], U8, align_bytes=64)
         planes_e_raw = keep.tile([P, WIDTH], U8, align_bytes=64)
         planes_e = keep.tile([P, WIDTH], U8, align_bytes=64)
@@ -59,25 +64,40 @@ def tile_messagepassing_pa_kernel(
         h_planes = keep.tile([P, PASSES * P], U8, align_bytes=64)
         e_codes = keep.tile([P, NODES, PASSES * P], U32, align_bytes=64)
         e_planes = keep.tile([P, NODES, PASSES * P], U8, align_bytes=64)
-        ones = keep.tile([P, P], BF16)
-        bias_row = keep.tile([P, WIDTH], BF16)
+        ones = keep.tile([P, N_TILE], BF16)
+        ident_bf16 = keep.tile([P, P], BF16)
+        bias_rows = keep.tile([P, WIDTH], BF16)
         b1_cols = keep.tile([P, HALVES, PACK], BF16)
-        mask_bf16 = keep.tile([P, NODES], BF16)
+        mask_bf16 = keep.tile([P, P], BF16)
+        mask_turned = keep.tile([P, P], BF16)
         mask_f32 = keep.tile([P, NODES], F32)
-        degree = keep.tile([P, 1], F32)
         target_term = keep.tile([P, HALVES, P, PACK], F32)
-        source_term = keep.tile([P, HALVES, P, PACK], F32)
+        source_term = keep.tile([P, HALVES * TERM + PACK * (NODES + LEAD)], F32)
         result = keep.tile([P, WIDTH], F32)
 
         make_identity(nc, ident_f32[:])
         nc.vector.memset(planes_n[:].bitcast(I32), 0)
-        nc.vector.memset(planes_e_raw[:].bitcast(I32), 0)
-        nc.vector.memset(bias_row[:].bitcast(I32), 0)
         nc.vector.memset(ones[:], 1.0)
+        nc.vector.memset(mask_bf16[:].bitcast(I32), 0)
+        nc.vector.memset(bias_rows[:].bitcast(I32), 0)
+        nc.vector.memset(planes_e_raw[:].bitcast(I32), 0)
         nc.vector.memset(planes_2[:].bitcast(I32), 0)
+        nc.vector.tensor_copy(out=ident_bf16[:], in_=ident_f32[:])
 
-        def load_words(tile, dram, group):
-            nc.sync.dma_start(out=tile[:, group, :], in_=dram[group].rearrange("p n t -> p (n t)").bitcast(I32))
+        def warm(turns):
+            warm_bank = banks.tile([P, N_TILE], F32, tag="bank")
+            for turn in range(turns):
+                nc.tensor.matmul(out=warm_bank[:], lhsT=ones[:, :P], rhs=ones[:], start=True, stop=True)
+
+        warm(5)
+
+        def load_words(tiles, dram, first, a):
+            nc.sync.dma_start(
+                out=tiles[a][:],
+                in_=dram[first : first + PASSES, :, N_TILE * a : N_TILE * (a + 1), :]
+                .rearrange("g p n t -> p g (n t)")
+                .bitcast(I32),
+            )
 
         def load_planes(tile, dram, first, count):
             for q in range(P // QUADRANT):
@@ -92,24 +112,27 @@ def tile_messagepassing_pa_kernel(
                 in_=e[:, :, first : first + count, :].rearrange("b i j k -> (b i) (j k)"),
             )
 
+        nc.gpsimd.dma_start(out=b1_cols[:], in_=b_m1.rearrange("(a p t) -> p a t", a=HALVES, t=PACK))
+        nc.gpsimd.dma_start(out=mask_bf16[:, :NODES], in_=adj_mask.rearrange("b i j o -> (b i) (j o)"))
+        nc.gpsimd.dma_start(out=bias_rows[:NODES, :], in_=b_m2.partition_broadcast(NODES))
         nc.sync.dma_start(out=h_rows[:], in_=h.rearrange("b i k -> (b i) k"))
         load_planes(planes_n, W_m1_scales, 0, 4)
-        for group in (2, 3, 0):
-            load_words(w1_words, W_m1_words, group)
+        load_words(wj_words, W_m1_words, 2, 0)
+        load_words(wi_words, W_m1_words, 0, 0)
+        load_e(0, 1)
         load_planes(planes_e_raw, W_m1_scales, 4, 2)
-        nc.sync.dma_start(out=b1_cols[:], in_=b_m1.rearrange("(a p t) -> p a t", a=HALVES, t=PACK))
-        load_words(w1_words, W_m1_words, 1)
-        load_e(0, 2)
-        for group in (4, 5):
-            load_words(w1_words, W_m1_words, group)
-        nc.sync.dma_start(out=mask_bf16[:], in_=adj_mask.rearrange("b i j o -> (b i) (j o)"))
-        nc.sync.dma_start(out=bias_row[0:1, :], in_=b_m2.unsqueeze(0))
+        load_words(we_raw, W_m1_words, 4, 0)
+        load_e(1, 1)
+        load_words(wj_words, W_m1_words, 2, 1)
+        load_words(wi_words, W_m1_words, 0, 1)
+        load_words(we_raw, W_m1_words, 4, 1)
+        load_e(2, 1)
+        load_e(3, 1)
         load_planes(planes_2, W_m2_scales, 0, 2)
-        load_e(2, 2)
-        load_e(4, 2)
-        for group in range(PASSES):
-            load_words(w2_words, W_m2_words, group)
-        load_e(6, 2)
+        for half in range(HALVES):
+            load_words(w2_words, W_m2_words, 0, half)
+        for first in (4, 6):
+            load_e(first, 2)
         load_e(8, 4)
         load_e(12, 4)
 
@@ -143,7 +166,7 @@ def tile_messagepassing_pa_kernel(
             )
             return grouped
 
-        def node_term_rows(first_group, a):
+        def node_term_rows(words, first_group, a):
             bank = banks.tile([P, N_TILE], F32, tag="bank")
             for c in range(PASSES):
                 row = PLANE_ROWS * (first_group + c)
@@ -151,7 +174,7 @@ def tile_messagepassing_pa_kernel(
                     out=bank[:],
                     lhsT=h_codes[:, P * c : P * (c + 1)].bitcast(FP8X4),
                     lhsT_scale=h_planes[:, P * c : P * (c + 1)],
-                    rhs=w1_words[:, first_group + c, N_TILE * a : N_TILE * (a + 1)].bitcast(FP8X4),
+                    rhs=words[a][:, c, :].bitcast(FP8X4),
                     rhs_scale=planes_n[row:P, N_TILE * a : N_TILE * (a + 1)],
                     start=(c == 0),
                     stop=(c == PASSES - 1),
@@ -170,8 +193,9 @@ def tile_messagepassing_pa_kernel(
             return bank
 
         def keep_source(a, bank):
+            first = a * (TERM + PACK * LEAD)
             nc.vector.tensor_tensor(
-                out=source_term[:, a],
+                out=source_term[:, first : first + TERM].rearrange("p (r t) -> p r t", t=PACK),
                 in0=bank[:].rearrange("p t r -> p r t"),
                 in1=b1_cols[:, a, :].unsqueeze(1).to_broadcast([P, P, PACK]),
                 op=ADD,
@@ -182,12 +206,12 @@ def tile_messagepassing_pa_kernel(
 
         def permute_words(c, a):
             nc.vector.tensor_copy(
-                out=we_words[:, c, N_TILE * a : N_TILE * (a + 1)].rearrange("p (t m) -> p t m", t=PACK),
-                in_=w1_words[:, 2 * PASSES + c, N_TILE * a : N_TILE * (a + 1)].rearrange("p (m t) -> p t m", t=PACK),
+                out=we_words[a][:, c, :].rearrange("p (t m) -> p t m", t=PACK),
+                in_=we_raw[a][:, c, :].rearrange("p (m t) -> p t m", t=PACK),
             )
 
-        def permute_planes(engine, a):
-            engine.tensor_copy(
+        def permute_planes(a):
+            nc.vector.tensor_copy(
                 out=planes_e[:, N_TILE * a : N_TILE * (a + 1)].rearrange("p (t m) -> p m t", t=PACK),
                 in_=planes_e_raw[:, N_TILE * a : N_TILE * (a + 1)].rearrange("p (m t) -> p m t", t=PACK),
             )
@@ -201,76 +225,106 @@ def tile_messagepassing_pa_kernel(
         r_operands = {}
         message_banks = {}
 
-        def sum_node_terms(j, gated):
-            source = source_term[:].rearrange("p a (b j) t -> p (a b) j t", j=NODES)[:, :, j, :]
-            node_sum = sums.tile([P, HALVES, P, PACK], F32)
-            summed = node_sum[:].rearrange("p a (b i) t -> p (a b) i t", i=NODES)
-            target = target_term[:].rearrange("p a (b i) t -> p (a b) i t", i=NODES)
-            if gated:
-                nc.vector.tensor_tensor(
-                    out=summed[:, :VECTOR_BLOCKS],
-                    in0=target[:, :VECTOR_BLOCKS],
-                    in1=source[:, :VECTOR_BLOCKS].unsqueeze(2).to_broadcast([P, VECTOR_BLOCKS, NODES, PACK]),
-                    op=ADD,
-                )
-                handed = stage.tile([P, BLOCKS, PACK], F32)
-                nc.vector.tensor_copy(out=handed[:, VECTOR_BLOCKS:], in_=source[:, VECTOR_BLOCKS:])
-                source = handed[:]
-                cuts = [VECTOR_BLOCKS, BLOCKS]
+        def halves_of(step):
+            return [(a, j) for a, j in ((0, step + LEAD), (1, step)) if 0 <= j < NODES]
+
+        def new_sum(step):
+            node_sums[step] = sums.tile([P, HALVES, P, PACK], F32, name="node_sum")
+
+        def source_blocks(step, first, last):
+            start = PACK * (step + LEAD)
+            words = source_term[:, start + BLOCK * first : start + BLOCK * last]
+            return words.rearrange("p (k x) -> p k x", x=BLOCK)[:, :, :PACK]
+
+        def add_blocks(engine, step, first, last, source):
+            blocks = "p a (b i) t -> p (a b) i t"
+            engine.tensor_tensor(
+                out=node_sums[step][:].rearrange(blocks, i=NODES)[:, first:last],
+                in0=target_term[:].rearrange(blocks, i=NODES)[:, first:last],
+                in1=source.unsqueeze(2).to_broadcast([P, last - first, NODES, PACK]),
+                op=ADD,
+            )
+
+        def sum_from_bank(step, a, bank):
+            nc.vector.tensor_tensor(
+                out=node_sums[step][:, a].rearrange("p (b i) t -> p b i t", i=NODES),
+                in0=bank[:].rearrange("p t (b i) -> p b i t", i=NODES),
+                in1=source_blocks(step, GRAPHS * a, GRAPHS * (a + 1))
+                .unsqueeze(2)
+                .to_broadcast([P, GRAPHS, NODES, PACK]),
+                op=ADD,
+            )
+
+        def sum_on_gpsimd(step, first, last):
+            handed = stage.tile([P, BLOCKS, PACK], F32)
+            nc.vector.tensor_copy(out=handed[:, first:last], in_=source_blocks(step, first, last))
+            add_blocks(nc.gpsimd, step, first, last, handed[:, first:last])
+
+        def sum_node_terms(step):
+            new_sum(step)
+            present = halves_of(step)
+            if len(present) == HALVES:
+                add_blocks(nc.vector, step, 0, VECTOR_BLOCKS, source_blocks(step, 0, VECTOR_BLOCKS))
+                sum_on_gpsimd(step, VECTOR_BLOCKS, BLOCKS)
             else:
-                cuts = [0, GRAPHS, BLOCKS]
-            for first, last in zip(cuts[:-1], cuts[1:]):
-                nc.gpsimd.tensor_tensor(
-                    out=summed[:, first:last],
-                    in0=target[:, first:last],
-                    in1=source[:, first:last].unsqueeze(2).to_broadcast([P, last - first, NODES, PACK]),
-                    op=ADD,
-                )
-            node_sums[j] = node_sum
+                a = present[0][0]
+                sum_on_gpsimd(step, GRAPHS * a, GRAPHS * (a + 1))
 
         def quantise_edges(j):
             nc.vector.quantize_mx(out=e_codes[:, j, :].bitcast(FP8X4), scales=e_planes[:, j, :], in_=grouped_e[j][:])
 
-        def first_layer(j):
-            edge_banks[j] = []
-            for a in range(HALVES):
-                bank = banks.tile([P, PACK, P], F32, tag="bank")
-                for t in range(PACK):
-                    first = P * (PACK * a + t)
-                    for c in range(PASSES):
-                        nc.tensor.matmul_mx(
-                            out=bank[:, t, :],
-                            lhsT=we_words[:, c, first : first + P].bitcast(FP8X4),
-                            lhsT_scale=planes_e[PLANE_ROWS * c : P, first : first + P],
-                            rhs=e_codes[:, j, P * c : P * (c + 1)].bitcast(FP8X4),
-                            rhs_scale=e_planes[:, j, P * c : P * (c + 1)],
-                            start=(c == 0),
-                            stop=(c == PASSES - 1),
-                        )
-                edge_banks[j].append(bank)
+        def first_layer(j, a):
+            bank = banks.tile([P, PACK, P], F32, tag="bank")
+            for t in range(PACK):
+                plane = P * (PACK * a + t)
+                for c in range(PASSES):
+                    nc.tensor.matmul_mx(
+                        out=bank[:, t, :],
+                        lhsT=we_words[a][:, c, P * t : P * (t + 1)].bitcast(FP8X4),
+                        lhsT_scale=planes_e[PLANE_ROWS * c : P, plane : plane + P],
+                        rhs=e_codes[:, j, P * c : P * (c + 1)].bitcast(FP8X4),
+                        rhs_scale=e_planes[:, j, P * c : P * (c + 1)],
+                        start=(c == 0),
+                        stop=(c == PASSES - 1),
+                    )
+            edge_banks[j, a] = bank
 
-        def add_and_relu(j):
-            pre_relu = stage.tile([P, HALVES, P, PACK], BF16)
-            hidden = stage.tile([P, WIDTH], BF16, align_bytes=64)
-            for a in range(HALVES):
-                nc.vector.tensor_tensor(
-                    out=pre_relu[:, a],
-                    in0=edge_banks[j][a][:].rearrange("p t r -> p r t"),
-                    in1=node_sums[j][:, a],
-                    op=ADD,
-                )
-                nc.scalar.activation(
-                    out=hidden[:, N_TILE * a : N_TILE * (a + 1)],
-                    in_=pre_relu[:, a].rearrange("p r t -> p (r t)"),
-                    func=RELU,
-                )
-            return hidden
+        def add_terms(step, a, j):
+            pre_relu = stage.tile([P, P, PACK], BF16)
+            nc.vector.tensor_tensor(
+                out=pre_relu[:],
+                in0=edge_banks[j, a][:].rearrange("p t r -> p r t"),
+                in1=node_sums[step][:, a],
+                op=ADD,
+            )
+            return pre_relu
 
-        def quantise_hidden(j, hidden):
+        def relu(j, a, pre_relu):
+            if a == 0:
+                hiddens[j] = hidden_pool.tile([P, WIDTH], BF16, align_bytes=64, name="hidden")
+            nc.scalar.activation(
+                out=hiddens[j][:, N_TILE * a : N_TILE * (a + 1)],
+                in_=pre_relu[:].rearrange("p r t -> p (r t)"),
+                func=RELU,
+            )
+
+        def open_hidden(j):
             r_codes = stage.tile([P, PASSES * P], U32, align_bytes=64)
             r_planes = stage.tile([P, PASSES * P], U8, align_bytes=64)
-            nc.vector.quantize_mx(out=r_codes[:].bitcast(FP8X4), scales=r_planes[:], in_=hidden[:])
             r_operands[j] = (r_codes, r_planes)
+
+        def quantise_hidden(j):
+            open_hidden(j)
+            r_codes, r_planes = r_operands[j]
+            nc.vector.quantize_mx(out=r_codes[:].bitcast(FP8X4), scales=r_planes[:], in_=hiddens[j][:])
+
+        def quantise_hidden_half(j, c):
+            r_codes, r_planes = r_operands[j]
+            nc.vector.quantize_mx(
+                out=r_codes[:, P * c : P * (c + 1)].bitcast(FP8X4),
+                scales=r_planes[:, P * c : P * (c + 1)],
+                in_=hiddens[j][:, K_PASS * c : K_PASS * (c + 1)],
+            )
 
         def message_pass(j, half, c):
             r_codes, r_planes = r_operands[j]
@@ -278,37 +332,23 @@ def tile_messagepassing_pa_kernel(
                 out=message_banks[j][half][:],
                 lhsT=r_codes[:, P * c : P * (c + 1)].bitcast(FP8X4),
                 lhsT_scale=r_planes[:, P * c : P * (c + 1)],
-                rhs=w2_words[:, c, N_TILE * half : N_TILE * (half + 1)].bitcast(FP8X4),
+                rhs=w2_words[half][:, c, :].bitcast(FP8X4),
                 rhs_scale=planes_2[PLANE_ROWS * c : P, N_TILE * half : N_TILE * (half + 1)],
                 start=(c == 0),
                 stop=(c == PASSES - 1),
             )
 
-        def second_layer(j):
+        def open_messages(j):
             message_banks[j] = []
             for half in range(HALVES):
                 message_bank = banks.tile([P, N_TILE], F32, tag="bank")
                 message_banks[j].append(message_bank)
+
+        def second_layer(j):
+            open_messages(j)
+            for half in range(HALVES):
                 for c in range(PASSES):
                     message_pass(j, half, c)
-
-        def last_messages(j, hidden):
-            r_codes = stage.tile([P, PASSES * P], U32, align_bytes=64)
-            r_planes = stage.tile([P, PASSES * P], U8, align_bytes=64)
-            r_operands[j] = (r_codes, r_planes)
-            message_banks[j] = []
-            for half in range(HALVES):
-                message_bank = banks.tile([P, N_TILE], F32, tag="bank")
-                message_banks[j].append(message_bank)
-            for c in range(PASSES):
-                nc.vector.quantize_mx(
-                    out=r_codes[:, P * c : P * (c + 1)].bitcast(FP8X4),
-                    scales=r_planes[:, P * c : P * (c + 1)],
-                    in_=hidden[:, K_PASS * c : K_PASS * (c + 1)],
-                )
-                for half in range(HALVES):
-                    message_pass(j, half, c)
-                gather_messages(j - 1, c)
 
         def gather_messages(j, half):
             columns = result[:, N_TILE * half : N_TILE * (half + 1)]
@@ -323,85 +363,111 @@ def tile_messagepassing_pa_kernel(
 
         h_grouped = group_rows(flip_unsorted_rows(h_rows[:]))
         nc.vector.quantize_mx(out=h_codes[:].bitcast(FP8X4), scales=h_planes[:], in_=h_grouped[:])
-        source_rows = [node_term_rows(2, a) for a in range(HALVES)]
-        source_sorted = [sort_term(nc.vector.tensor_copy, source_rows[0]), sort_term(nc.scalar.copy, source_rows[1])]
-        permute_planes(nc.vector, 0)
-        permute_planes(nc.gpsimd, 1)
-        for a in range(HALVES):
-            keep_source(a, flip_term(source_sorted[a]))
-        target_rows = [node_term_rows(0, a) for a in range(HALVES)]
-        target_sorted = [sort_term(nc.scalar.copy, target_rows[0]), sort_term(nc.vector.tensor_copy, target_rows[1])]
-        target_banks = []
-        for a in range(HALVES):
-            target_banks.append(flip_term(target_sorted[a]))
-            flipped_e[a] = flip_unsorted_rows(e_rows[:, a, :])
-        for a in range(HALVES):
-            keep_target(a, target_banks[a])
-            grouped_e[a] = group_rows(flipped_e[a])
-        for j in range(SUM_LEAD):
-            sum_node_terms(j, False)
-        permute_words(0, 0)
-        permute_words(0, 1)
-        permute_words(1, 0)
+        source_rows = node_term_rows(wj_words, 2, 0)
+        target_rows = node_term_rows(wi_words, 0, 0)
+        source_sorted = sort_term(nc.vector.tensor_copy, source_rows)
+        target_sorted = sort_term(nc.scalar.copy, target_rows)
+        source_bank = flip_term(source_sorted)
+        permute_planes(0)
+        flipped_e[0] = flip_unsorted_rows(e_rows[:, 0, :])
+        target_bank = flip_term(target_sorted)
+        grouped_e[0] = group_rows(flipped_e[0])
+        keep_target(0, target_bank)
+        warm(2)
+        keep_source(0, source_bank)
+        for c in range(PASSES):
+            permute_words(c, 0)
         quantise_edges(0)
-        permute_words(1, 1)
-        first_layer(0)
-        bias_banks = []
-        for half in range(HALVES):
-            bias_bank = banks.tile([P, N_TILE], F32, tag="bank")
-            nc.tensor.matmul(
-                out=bias_bank[:],
-                lhsT=ones[:],
-                rhs=bias_row[:, N_TILE * half : N_TILE * (half + 1)],
-                start=True,
-                stop=True,
-            )
-            bias_banks.append(bias_bank)
+        first_layer(0, 0)
+        new_sum(-LEAD)
+        sum_from_bank(-LEAD, 0, target_bank)
+        new_sum(0)
+        sum_on_gpsimd(0, 0, GRAPHS)
+        permute_planes(1)
+        flipped_e[1] = flip_unsorted_rows(e_rows[:, 1, :])
+        grouped_e[1] = group_rows(flipped_e[1])
+        pre_relu_0 = add_terms(-LEAD, 0, 0)
+
+        source_rows = node_term_rows(wj_words, 2, 1)
+        source_sorted = sort_term(nc.scalar.copy, source_rows)
+        target_rows = node_term_rows(wi_words, 0, 1)
+        target_sorted = sort_term(nc.scalar.copy, target_rows)
+        quantise_edges(1)
+        source_bank = flip_term(source_sorted)
+        first_layer(1, 0)
+        target_bank = flip_term(target_sorted)
         flipped_e[2] = flip_unsorted_rows(e_rows[:, 2, :])
+        keep_source(1, source_bank)
+        for c in range(PASSES):
+            permute_words(c, 1)
+        first_layer(0, 1)
+        sum_from_bank(0, 1, target_bank)
+        keep_target(1, target_bank)
+        grouped_e[2] = group_rows(flipped_e[2])
+        pre_relu_1 = add_terms(0, 0, 1)
+        relu(0, 0, pre_relu_0)
+        sum_node_terms(1)
+        pre_relu_0 = add_terms(0, 1, 0)
+        relu(0, 1, pre_relu_0)
+        quantise_edges(2)
+        flipped_e[3] = flip_unsorted_rows(e_rows[:, 3, :])
+        grouped_e[3] = group_rows(flipped_e[3])
+        relu(1, 0, pre_relu_1)
+
+        nc.vector.tensor_copy(out=mask_f32[:], in_=mask_bf16[:, :NODES])
+        turned_bank = flips.tile([P, P], BF16, tag="flip")
+        nc.tensor.transpose(turned_bank[:], mask_bf16[:], ident_bf16[:])
+        nc.scalar.copy(out=mask_turned[:], in_=turned_bank[:])
+        for a, j in halves_of(1):
+            first_layer(j, a)
+        for half in range(HALVES):
+            columns = slice(N_TILE * half, N_TILE * (half + 1))
+            first_bank = banks.tile([P, N_TILE], F32, tag="bank")
+            nc.tensor.matmul(out=first_bank[:], lhsT=ident_bf16[:], rhs=h_rows[:, columns], start=True, stop=False)
+            nc.tensor.matmul(out=first_bank[:], lhsT=mask_turned[:], rhs=bias_rows[:, columns], start=False, stop=True)
+            nc.scalar.copy(out=result[:, columns], in_=first_bank[:])
+        flipped_e[4] = flip_unsorted_rows(e_rows[:, 4, :])
 
         rows_out = out.rearrange("b i n -> (b i) n")
-        for step in range(NODES + 1):
-            if step + 2 < NODES:
-                grouped_e[step + 2] = group_rows(flipped_e[step + 2])
-            if UNSORTED <= step + 4 < NODES:
-                sorted_e[step + 4] = sort_words(e_rows[:, step + 4, :])
-            if step + 1 < NODES:
-                quantise_edges(step + 1)
-            if 1 <= step < NODES:
-                quantise_hidden(step - 1, hiddens[step - 1])
-                second_layer(step - 1)
-            if step + SUM_LEAD < NODES:
-                sum_node_terms(step + SUM_LEAD, True)
-            if step < NODES:
-                hiddens[step] = add_and_relu(step)
-            if step == 0:
-                nc.vector.tensor_copy(out=mask_f32[:], in_=mask_bf16[:])
-                nc.vector.reduce_sum(out=degree[:], in_=mask_f32[:], axis=mybir.AxisListType.X)
+        for step in range(1, NODES):
+            if step + LEAD + 2 < NODES:
+                grouped_e[step + LEAD + 2] = group_rows(flipped_e[step + LEAD + 2])
+            if UNSORTED <= step + LEAD + 4 < NODES:
+                sorted_e[step + LEAD + 4] = sort_words(e_rows[:, step + LEAD + 4, :])
+            quantise_hidden(step - 1)
+            if step + LEAD + 1 < NODES:
+                quantise_edges(step + LEAD + 1)
+            second_layer(step - 1)
+            if step == NODES - 1:
+                open_hidden(step)
+                quantise_hidden_half(step, 0)
+                open_messages(step)
                 for half in range(HALVES):
-                    nc.vector.scalar_tensor_tensor(
-                        out=result[:, N_TILE * half : N_TILE * (half + 1)],
-                        in0=bias_banks[half][:],
-                        scalar=degree[:, 0:1],
-                        in1=h_rows[:, N_TILE * half : N_TILE * (half + 1)],
-                        op0=MULT,
-                        op1=ADD,
-                    )
-            if 1 <= step < NODES - 1:
+                    message_pass(step, half, 0)
+            if step + 1 < NODES:
+                sum_node_terms(step + 1)
+            for a, j in halves_of(step):
+                relu(j, a, add_terms(step, a, j))
+            if step < NODES - 1:
                 for half in range(HALVES):
                     gather_messages(step - 1, half)
-            if step == NODES:
-                last_messages(NODES - 1, hiddens[NODES - 1])
-                for half in range(HALVES):
-                    gather_messages(NODES - 1, half)
-                    nc.sync.dma_start(
-                        out=rows_out[:, N_TILE * half : N_TILE * (half + 1)],
-                        in_=result[:, N_TILE * half : N_TILE * (half + 1)],
-                    )
-            if step + 1 < NODES:
-                first_layer(step + 1)
-            if step % 2 == 0:
-                for j in range(step + 3, min(step + 5, NODES)):
+                for a, j in halves_of(step + 1):
+                    first_layer(j, a)
+            if step % 2 == 1:
+                for j in range(step + LEAD + 3, min(step + LEAD + 5, NODES)):
                     if j < UNSORTED:
                         flipped_e[j] = flip_unsorted_rows(e_rows[:, j, :])
                     else:
                         flipped_e[j] = flip_rows(sorted_e[j])
+
+        gather_messages(NODES - 2, 0)
+        quantise_hidden_half(NODES - 1, 1)
+        for half in range(HALVES):
+            message_pass(NODES - 1, half, 1)
+        gather_messages(NODES - 2, 1)
+        for half in range(HALVES):
+            gather_messages(NODES - 1, half)
+            nc.sync.dma_start(
+                out=rows_out[:, N_TILE * half : N_TILE * (half + 1)],
+                in_=result[:, N_TILE * half : N_TILE * (half + 1)],
+            )

@@ -29,7 +29,7 @@ LEAD = 1
 TERM = P * PACK
 BLOCK = NODES * PACK
 UNSORTED = 7
-VECTOR_BLOCKS = 3
+VECTOR_BLOCKS = 2
 
 FLOPS = 2 * (2 * GRAPHS * NODES * NODES + 2 * GRAPHS * NODES) * WIDTH * WIDTH
 
@@ -44,7 +44,8 @@ def tile_messagepassing_pa_kernel(
         sorts = stack.enter_context(tc.tile_pool(name="sorts", bufs=4))
         sums = stack.enter_context(tc.tile_pool(name="sums", bufs=3))
         hidden_pool = stack.enter_context(tc.tile_pool(name="hidden", bufs=LEAD + 3))
-        banks = stack.enter_context(tc.psum_pool(name="banks", bufs=6))
+        banks = stack.enter_context(tc.psum_pool(name="banks", bufs=5))
+        kept = stack.enter_context(tc.psum_pool(name="kept", bufs=1))
         flips = stack.enter_context(tc.psum_pool(name="flips", bufs=2))
         stack.enter_context(tc.manual_schedule())
 
@@ -89,7 +90,7 @@ def tile_messagepassing_pa_kernel(
             for turn in range(turns):
                 nc.tensor.matmul(out=warm_bank[:], lhsT=ones[:, :P], rhs=ones[:], start=True, stop=True)
 
-        warm(5)
+        warm(4)
 
         def load_words(tiles, dram, first, a):
             nc.sync.dma_start(
@@ -112,21 +113,21 @@ def tile_messagepassing_pa_kernel(
                 in_=e[:, :, first : first + count, :].rearrange("b i j k -> (b i) (j k)"),
             )
 
-        nc.gpsimd.dma_start(out=b1_cols[:], in_=b_m1.rearrange("(a p t) -> p a t", a=HALVES, t=PACK))
-        nc.gpsimd.dma_start(out=mask_bf16[:, :NODES], in_=adj_mask.rearrange("b i j o -> (b i) (j o)"))
-        nc.gpsimd.dma_start(out=bias_rows[:NODES, :], in_=b_m2.partition_broadcast(NODES))
         nc.sync.dma_start(out=h_rows[:], in_=h.rearrange("b i k -> (b i) k"))
         load_planes(planes_n, W_m1_scales, 0, 4)
         load_words(wj_words, W_m1_words, 2, 0)
         load_words(wi_words, W_m1_words, 0, 0)
         load_e(0, 1)
         load_planes(planes_e_raw, W_m1_scales, 4, 2)
+        nc.sync.dma_start(out=b1_cols[:], in_=b_m1.rearrange("(a p t) -> p a t", a=HALVES, t=PACK))
         load_words(we_raw, W_m1_words, 4, 0)
         load_e(1, 1)
         load_words(wj_words, W_m1_words, 2, 1)
         load_words(wi_words, W_m1_words, 0, 1)
         load_words(we_raw, W_m1_words, 4, 1)
         load_e(2, 1)
+        nc.sync.dma_start(out=mask_bf16[:, :NODES], in_=adj_mask.rearrange("b i j o -> (b i) (j o)"))
+        nc.sync.dma_start(out=bias_rows[:NODES, :], in_=b_m2.partition_broadcast(NODES))
         load_e(3, 1)
         load_planes(planes_2, W_m2_scales, 0, 2)
         for half in range(HALVES):
@@ -186,8 +187,8 @@ def tile_messagepassing_pa_kernel(
             copy(out=sorted_rows[:], in_=rows_bank[:].rearrange("r (p t) -> r t p", t=PACK))
             return sorted_rows
 
-        def flip_term(sorted_rows):
-            bank = banks.tile([P, PACK, P], F32, tag="bank")
+        def flip_term(sorted_rows, pool=banks):
+            bank = pool.tile([P, PACK, P], F32, tag="bank")
             for t in range(PACK):
                 nc.tensor.transpose(bank[:, t, :], sorted_rows[:, t, :], ident_f32[:])
             return bank
@@ -210,8 +211,8 @@ def tile_messagepassing_pa_kernel(
                 in_=we_raw[a][:, c, :].rearrange("p (m t) -> p t m", t=PACK),
             )
 
-        def permute_planes(a):
-            nc.vector.tensor_copy(
+        def permute_planes(engine, a):
+            engine.tensor_copy(
                 out=planes_e[:, N_TILE * a : N_TILE * (a + 1)].rearrange("p (t m) -> p m t", t=PACK),
                 in_=planes_e_raw[:, N_TILE * a : N_TILE * (a + 1)].rearrange("p (m t) -> p m t", t=PACK),
             )
@@ -245,13 +246,13 @@ def tile_messagepassing_pa_kernel(
                 op=ADD,
             )
 
-        def sum_from_bank(step, a, bank):
+        def sum_from_bank(step, a, bank, count):
             nc.vector.tensor_tensor(
-                out=node_sums[step][:, a].rearrange("p (b i) t -> p b i t", i=NODES),
-                in0=bank[:].rearrange("p t (b i) -> p b i t", i=NODES),
-                in1=source_blocks(step, GRAPHS * a, GRAPHS * (a + 1))
+                out=node_sums[step][:, a].rearrange("p (b i) t -> p b i t", i=NODES)[:, :count],
+                in0=bank[:].rearrange("p t (b i) -> p b i t", i=NODES)[:, :count],
+                in1=source_blocks(step, GRAPHS * a, GRAPHS * a + count)
                 .unsqueeze(2)
-                .to_broadcast([P, GRAPHS, NODES, PACK]),
+                .to_broadcast([P, count, NODES, PACK]),
                 op=ADD,
             )
 
@@ -264,8 +265,8 @@ def tile_messagepassing_pa_kernel(
             new_sum(step)
             present = halves_of(step)
             if len(present) == HALVES:
-                add_blocks(nc.vector, step, 0, VECTOR_BLOCKS, source_blocks(step, 0, VECTOR_BLOCKS))
                 sum_on_gpsimd(step, VECTOR_BLOCKS, BLOCKS)
+                sum_from_bank(step, 0, kept_bank, VECTOR_BLOCKS)
             else:
                 a = present[0][0]
                 sum_on_gpsimd(step, GRAPHS * a, GRAPHS * (a + 1))
@@ -307,6 +308,19 @@ def tile_messagepassing_pa_kernel(
                 in_=pre_relu[:].rearrange("p r t -> p (r t)"),
                 func=RELU,
             )
+
+        def add_and_relu_in_parts(step, a, j):
+            pre_relu = stage.tile([P, P, PACK], BF16)
+            hidden = hiddens[j][:, N_TILE * a : N_TILE * (a + 1)].rearrange("p (r t) -> p r t", t=PACK)
+            for part in range(2):
+                rows = slice(P // 2 * part, P // 2 * (part + 1))
+                nc.vector.tensor_tensor(
+                    out=pre_relu[:, rows, :],
+                    in0=edge_banks[j, a][:].rearrange("p t r -> p r t")[:, rows, :],
+                    in1=node_sums[step][:, a, rows, :],
+                    op=ADD,
+                )
+                nc.scalar.activation(out=hidden[:, rows, :], in_=pre_relu[:, rows, :], func=RELU)
 
         def open_hidden(j):
             r_codes = stage.tile([P, PASSES * P], U32, align_bytes=64)
@@ -350,11 +364,11 @@ def tile_messagepassing_pa_kernel(
                 for c in range(PASSES):
                     message_pass(j, half, c)
 
-        def gather_messages(j, half):
-            columns = result[:, N_TILE * half : N_TILE * (half + 1)]
+        def gather_messages(j, half, first=0, last=N_TILE):
+            columns = result[:, N_TILE * half + first : N_TILE * half + last]
             nc.vector.scalar_tensor_tensor(
                 out=columns,
-                in0=message_banks[j][half][:],
+                in0=message_banks[j][half][:, first:last],
                 scalar=mask_f32[:, j : j + 1],
                 in1=columns,
                 op0=MULT,
@@ -362,82 +376,96 @@ def tile_messagepassing_pa_kernel(
             )
 
         h_grouped = group_rows(flip_unsorted_rows(h_rows[:]))
+        warm(2)
         nc.vector.quantize_mx(out=h_codes[:].bitcast(FP8X4), scales=h_planes[:], in_=h_grouped[:])
         source_rows = node_term_rows(wj_words, 2, 0)
         target_rows = node_term_rows(wi_words, 0, 0)
+        permute_planes(nc.vector, 0)
+        permute_planes(nc.gpsimd, 1)
         source_sorted = sort_term(nc.vector.tensor_copy, source_rows)
         target_sorted = sort_term(nc.scalar.copy, target_rows)
-        source_bank = flip_term(source_sorted)
-        permute_planes(0)
         flipped_e[0] = flip_unsorted_rows(e_rows[:, 0, :])
-        target_bank = flip_term(target_sorted)
+        source_bank = flip_term(source_sorted)
         grouped_e[0] = group_rows(flipped_e[0])
-        keep_target(0, target_bank)
-        warm(2)
-        keep_source(0, source_bank)
+        kept_bank = flip_term(target_sorted, kept)
         for c in range(PASSES):
             permute_words(c, 0)
         quantise_edges(0)
+        keep_target(0, kept_bank)
+        keep_source(0, source_bank)
+        warm(1)
         first_layer(0, 0)
-        new_sum(-LEAD)
-        sum_from_bank(-LEAD, 0, target_bank)
-        new_sum(0)
-        sum_on_gpsimd(0, 0, GRAPHS)
-        permute_planes(1)
-        flipped_e[1] = flip_unsorted_rows(e_rows[:, 1, :])
-        grouped_e[1] = group_rows(flipped_e[1])
-        pre_relu_0 = add_terms(-LEAD, 0, 0)
-
         source_rows = node_term_rows(wj_words, 2, 1)
         source_sorted = sort_term(nc.scalar.copy, source_rows)
+        new_sum(0)
+        sum_on_gpsimd(0, 0, GRAPHS)
+        new_sum(-LEAD)
+        sum_from_bank(-LEAD, 0, kept_bank, GRAPHS)
         target_rows = node_term_rows(wi_words, 0, 1)
         target_sorted = sort_term(nc.scalar.copy, target_rows)
-        quantise_edges(1)
-        source_bank = flip_term(source_sorted)
-        first_layer(1, 0)
-        target_bank = flip_term(target_sorted)
-        flipped_e[2] = flip_unsorted_rows(e_rows[:, 2, :])
-        keep_source(1, source_bank)
+        flipped_e[1] = flip_unsorted_rows(e_rows[:, 1, :])
+        grouped_e[1] = group_rows(flipped_e[1])
+        pre_relu_00 = add_terms(-LEAD, 0, 0)
         for c in range(PASSES):
             permute_words(c, 1)
-        first_layer(0, 1)
-        sum_from_bank(0, 1, target_bank)
-        keep_target(1, target_bank)
-        grouped_e[2] = group_rows(flipped_e[2])
-        pre_relu_1 = add_terms(0, 0, 1)
-        relu(0, 0, pre_relu_0)
-        sum_node_terms(1)
-        pre_relu_0 = add_terms(0, 1, 0)
-        relu(0, 1, pre_relu_0)
-        quantise_edges(2)
-        flipped_e[3] = flip_unsorted_rows(e_rows[:, 3, :])
-        grouped_e[3] = group_rows(flipped_e[3])
-        relu(1, 0, pre_relu_1)
 
-        nc.vector.tensor_copy(out=mask_f32[:], in_=mask_bf16[:, :NODES])
+        source_bank = flip_term(source_sorted)
+        target_bank = flip_term(target_sorted)
+        first_layer(0, 1)
+        keep_source(1, source_bank)
+        quantise_edges(1)
+        sum_from_bank(0, 1, target_bank, GRAPHS)
+        keep_target(1, target_bank)
+        flipped_e[2] = flip_unsorted_rows(e_rows[:, 2, :])
+        first_layer(1, 0)
+
+        first_banks = []
+        for half in range(HALVES):
+            first_bank = banks.tile([P, N_TILE], F32, tag="bank")
+            nc.tensor.matmul(
+                out=first_bank[:],
+                lhsT=ident_bf16[:],
+                rhs=h_rows[:, N_TILE * half : N_TILE * (half + 1)],
+                start=True,
+                stop=False,
+            )
+            first_banks.append(first_bank)
+        grouped_e[2] = group_rows(flipped_e[2])
+        relu(0, 0, pre_relu_00)
+        sum_node_terms(1)
+        pre_relu_01 = add_terms(0, 1, 0)
         turned_bank = flips.tile([P, P], BF16, tag="flip")
         nc.tensor.transpose(turned_bank[:], mask_bf16[:], ident_bf16[:])
         nc.scalar.copy(out=mask_turned[:], in_=turned_bank[:])
+        relu(0, 1, pre_relu_01)
+        pre_relu_10 = add_terms(0, 0, 1)
+        quantise_edges(2)
+        flipped_e[3] = flip_unsorted_rows(e_rows[:, 3, :])
+        grouped_e[3] = group_rows(flipped_e[3])
+        relu(1, 0, pre_relu_10)
+
+        nc.vector.tensor_copy(out=mask_f32[:], in_=mask_bf16[:, :NODES])
         for a, j in halves_of(1):
             first_layer(j, a)
         for half in range(HALVES):
             columns = slice(N_TILE * half, N_TILE * (half + 1))
-            first_bank = banks.tile([P, N_TILE], F32, tag="bank")
-            nc.tensor.matmul(out=first_bank[:], lhsT=ident_bf16[:], rhs=h_rows[:, columns], start=True, stop=False)
-            nc.tensor.matmul(out=first_bank[:], lhsT=mask_turned[:], rhs=bias_rows[:, columns], start=False, stop=True)
-            nc.scalar.copy(out=result[:, columns], in_=first_bank[:])
-        flipped_e[4] = flip_unsorted_rows(e_rows[:, 4, :])
+            nc.tensor.matmul(
+                out=first_banks[half][:], lhsT=mask_turned[:], rhs=bias_rows[:, columns], start=False, stop=True
+            )
+            nc.scalar.copy(out=result[:, columns], in_=first_banks[half][:])
 
         rows_out = out.rearrange("b i n -> (b i) n")
         for step in range(1, NODES):
-            if step + LEAD + 2 < NODES:
+            if 1 < step < NODES - LEAD - 2:
                 grouped_e[step + LEAD + 2] = group_rows(flipped_e[step + LEAD + 2])
-            if UNSORTED <= step + LEAD + 4 < NODES:
-                sorted_e[step + LEAD + 4] = sort_words(e_rows[:, step + LEAD + 4, :])
+            if 2 < step < NODES - LEAD - 1:
+                quantise_edges(step + LEAD + 1)
             quantise_hidden(step - 1)
-            if step + LEAD + 1 < NODES:
+            if step <= 2:
                 quantise_edges(step + LEAD + 1)
             second_layer(step - 1)
+            if step == 1:
+                flipped_e[4] = flip_unsorted_rows(e_rows[:, 4, :])
             if step == NODES - 1:
                 open_hidden(step)
                 quantise_hidden_half(step, 0)
@@ -446,8 +474,15 @@ def tile_messagepassing_pa_kernel(
                     message_pass(step, half, 0)
             if step + 1 < NODES:
                 sum_node_terms(step + 1)
-            for a, j in halves_of(step):
-                relu(j, a, add_terms(step, a, j))
+            if step == NODES - 1:
+                add_and_relu_in_parts(step, 1, step)
+            else:
+                for a, j in halves_of(step):
+                    relu(j, a, add_terms(step, a, j))
+            if UNSORTED <= step + LEAD + 4 < NODES:
+                sorted_e[step + LEAD + 4] = sort_words(e_rows[:, step + LEAD + 4, :])
+            if step == 1:
+                grouped_e[4] = group_rows(flipped_e[4])
             if step < NODES - 1:
                 for half in range(HALVES):
                     gather_messages(step - 1, half)
@@ -465,9 +500,9 @@ def tile_messagepassing_pa_kernel(
         for half in range(HALVES):
             message_pass(NODES - 1, half, 1)
         gather_messages(NODES - 2, 1)
-        for half in range(HALVES):
-            gather_messages(NODES - 1, half)
+        for half, first, last in ((0, 0, N_TILE), (1, 0, N_TILE // 2), (1, N_TILE // 2, N_TILE)):
+            gather_messages(NODES - 1, half, first, last)
             nc.sync.dma_start(
-                out=rows_out[:, N_TILE * half : N_TILE * (half + 1)],
-                in_=result[:, N_TILE * half : N_TILE * (half + 1)],
+                out=rows_out[:, N_TILE * half + first : N_TILE * half + last],
+                in_=result[:, N_TILE * half + first : N_TILE * half + last],
             )

@@ -218,6 +218,7 @@ def tile_messagepassing_pa_kernel(
             )
 
         node_sums = {}
+        handed = {}
         sorted_e = {}
         flipped_e = {}
         grouped_e = {}
@@ -256,20 +257,21 @@ def tile_messagepassing_pa_kernel(
                 op=ADD,
             )
 
-        def sum_on_gpsimd(step, first, last):
-            handed = stage.tile([P, BLOCKS, PACK], F32)
-            nc.vector.tensor_copy(out=handed[:, first:last], in_=source_blocks(step, first, last))
-            add_blocks(nc.gpsimd, step, first, last, handed[:, first:last])
+        def gpsimd_blocks(step):
+            present = [a for a, j in halves_of(step)]
+            return VECTOR_BLOCKS if len(present) == HALVES else GRAPHS * present[0], GRAPHS * (present[-1] + 1)
+
+        def hand_source(step):
+            first, last = gpsimd_blocks(step)
+            handed[step] = stage.tile([P, BLOCKS, PACK], F32, name="handed")
+            nc.vector.tensor_copy(out=handed[step][:, first:last], in_=source_blocks(step, first, last))
 
         def sum_node_terms(step):
             new_sum(step)
-            present = halves_of(step)
-            if len(present) == HALVES:
-                sum_on_gpsimd(step, VECTOR_BLOCKS, BLOCKS)
+            first, last = gpsimd_blocks(step)
+            add_blocks(nc.gpsimd, step, first, last, handed[step][:, first:last])
+            if len(halves_of(step)) == HALVES:
                 sum_from_bank(step, 0, kept_bank, VECTOR_BLOCKS)
-            else:
-                a = present[0][0]
-                sum_on_gpsimd(step, GRAPHS * a, GRAPHS * (a + 1))
 
         def quantise_edges(j):
             nc.vector.quantize_mx(out=e_codes[:, j, :].bitcast(FP8X4), scales=e_planes[:, j, :], in_=grouped_e[j][:])
@@ -398,7 +400,9 @@ def tile_messagepassing_pa_kernel(
         source_rows = node_term_rows(wj_words, 2, 1)
         source_sorted = sort_term(nc.scalar.copy, source_rows)
         new_sum(0)
-        sum_on_gpsimd(0, 0, GRAPHS)
+        handed[0] = stage.tile([P, BLOCKS, PACK], F32, name="handed")
+        nc.vector.tensor_copy(out=handed[0][:, :GRAPHS], in_=source_blocks(0, 0, GRAPHS))
+        add_blocks(nc.gpsimd, 0, 0, GRAPHS, handed[0][:, :GRAPHS])
         new_sum(-LEAD)
         sum_from_bank(-LEAD, 0, kept_bank, GRAPHS)
         target_rows = node_term_rows(wi_words, 0, 1)
@@ -432,6 +436,7 @@ def tile_messagepassing_pa_kernel(
             first_banks.append(first_bank)
         grouped_e[2] = group_rows(flipped_e[2])
         relu(0, 0, pre_relu_00)
+        hand_source(1)
         sum_node_terms(1)
         pre_relu_01 = add_terms(0, 1, 0)
         turned_bank = flips.tile([P, P], BF16, tag="flip")
@@ -458,12 +463,12 @@ def tile_messagepassing_pa_kernel(
         for step in range(1, NODES):
             if 1 < step < NODES - LEAD - 2:
                 grouped_e[step + LEAD + 2] = group_rows(flipped_e[step + LEAD + 2])
-            if 2 < step < NODES - LEAD - 1:
-                quantise_edges(step + LEAD + 1)
             quantise_hidden(step - 1)
-            if step <= 2:
-                quantise_edges(step + LEAD + 1)
             second_layer(step - 1)
+            if step + 1 < NODES:
+                hand_source(step + 1)
+            if step + LEAD + 1 < NODES:
+                quantise_edges(step + LEAD + 1)
             if step == 1:
                 flipped_e[4] = flip_unsorted_rows(e_rows[:, 4, :])
             if step == NODES - 1:

@@ -25,11 +25,11 @@ HALVES = WIDTH // N_TILE
 PLANE_ROWS = 4
 QUADRANT = 32
 BLOCKS = HALVES * GRAPHS
+VECTOR_BLOCKS = 1
 LEAD = 1
 TERM = P * PACK
 BLOCK = NODES * PACK
 UNSORTED = 7
-VECTOR_BLOCKS = 2
 
 FLOPS = 2 * (2 * GRAPHS * NODES * NODES + 2 * GRAPHS * NODES) * WIDTH * WIDTH
 
@@ -43,6 +43,7 @@ def tile_messagepassing_pa_kernel(
         stage = stack.enter_context(tc.tile_pool(name="stage", bufs=3))
         sorts = stack.enter_context(tc.tile_pool(name="sorts", bufs=4))
         sums = stack.enter_context(tc.tile_pool(name="sums", bufs=3))
+        pre_pool = stack.enter_context(tc.tile_pool(name="pre_relu", bufs=6))
         hidden_pool = stack.enter_context(tc.tile_pool(name="hidden", bufs=LEAD + 3))
         banks = stack.enter_context(tc.psum_pool(name="banks", bufs=5))
         kept = stack.enter_context(tc.psum_pool(name="kept", bufs=1))
@@ -57,8 +58,8 @@ def tile_messagepassing_pa_kernel(
         we_raw = [keep.tile([P, PASSES, N_TILE], I32, align_bytes=64, name=f"we_raw_{a}") for a in range(HALVES)]
         we_words = [keep.tile([P, PASSES, N_TILE], I32, align_bytes=64, name=f"we_{a}") for a in range(HALVES)]
         w2_words = [keep.tile([P, PASSES, N_TILE], I32, align_bytes=64, name=f"w2_{a}") for a in range(HALVES)]
-        planes_n = keep.tile([P, WIDTH], U8, align_bytes=64)
-        planes_e_raw = keep.tile([P, WIDTH], U8, align_bytes=64)
+        planes_i = keep.tile([P, WIDTH], U8, align_bytes=64)
+        planes_je = keep.tile([P, WIDTH], U8, align_bytes=64)
         planes_e = keep.tile([P, WIDTH], U8, align_bytes=64)
         planes_2 = keep.tile([P, WIDTH], U8, align_bytes=64)
         h_codes = keep.tile([P, PASSES * P], U32, align_bytes=64)
@@ -77,11 +78,11 @@ def tile_messagepassing_pa_kernel(
         result = keep.tile([P, WIDTH], F32)
 
         make_identity(nc, ident_f32[:])
-        nc.vector.memset(planes_n[:].bitcast(I32), 0)
+        nc.vector.memset(planes_je[:].bitcast(I32), 0)
         nc.vector.memset(ones[:], 1.0)
         nc.vector.memset(mask_bf16[:].bitcast(I32), 0)
         nc.vector.memset(bias_rows[:].bitcast(I32), 0)
-        nc.vector.memset(planes_e_raw[:].bitcast(I32), 0)
+        nc.vector.memset(planes_i[:].bitcast(I32), 0)
         nc.vector.memset(planes_2[:].bitcast(I32), 0)
         nc.vector.tensor_copy(out=ident_bf16[:], in_=ident_f32[:])
 
@@ -100,12 +101,15 @@ def tile_messagepassing_pa_kernel(
                 .bitcast(I32),
             )
 
+        def load_plane(tile, dram, first, count, q):
+            nc.sync.dma_start(
+                out=tile[QUADRANT * q : QUADRANT * q + PLANE_ROWS * count, :].bitcast(I32),
+                in_=dram[first : first + count, PLANE_ROWS * q : PLANE_ROWS * (q + 1), :].bitcast(I32),
+            )
+
         def load_planes(tile, dram, first, count):
             for q in range(P // QUADRANT):
-                nc.sync.dma_start(
-                    out=tile[QUADRANT * q : QUADRANT * q + PLANE_ROWS * count, :].bitcast(I32),
-                    in_=dram[first : first + count, PLANE_ROWS * q : PLANE_ROWS * (q + 1), :].bitcast(I32),
-                )
+                load_plane(tile, dram, first, count, q)
 
         def load_e(first, count):
             nc.sync.dma_start(
@@ -114,26 +118,29 @@ def tile_messagepassing_pa_kernel(
             )
 
         nc.sync.dma_start(out=h_rows[:], in_=h.rearrange("b i k -> (b i) k"))
-        load_planes(planes_n, W_m1_scales, 0, 4)
+        load_planes(planes_je, W_m1_scales, 2, 4)
         load_words(wj_words, W_m1_words, 2, 0)
         load_words(wi_words, W_m1_words, 0, 0)
         load_e(0, 1)
-        load_planes(planes_e_raw, W_m1_scales, 4, 2)
-        nc.sync.dma_start(out=b1_cols[:], in_=b_m1.rearrange("(a p t) -> p a t", a=HALVES, t=PACK))
+        load_planes(planes_i, W_m1_scales, 0, 2)
         load_words(we_raw, W_m1_words, 4, 0)
+        nc.sync.dma_start(out=b1_cols[:], in_=b_m1.rearrange("(a p t) -> p a t", a=HALVES, t=PACK))
         load_e(1, 1)
         load_words(wj_words, W_m1_words, 2, 1)
         load_words(wi_words, W_m1_words, 0, 1)
         load_words(we_raw, W_m1_words, 4, 1)
         load_e(2, 1)
         nc.sync.dma_start(out=mask_bf16[:, :NODES], in_=adj_mask.rearrange("b i j o -> (b i) (j o)"))
-        nc.sync.dma_start(out=bias_rows[:NODES, :], in_=b_m2.partition_broadcast(NODES))
         load_e(3, 1)
-        load_planes(planes_2, W_m2_scales, 0, 2)
-        for half in range(HALVES):
-            load_words(w2_words, W_m2_words, 0, half)
-        for first in (4, 6):
-            load_e(first, 2)
+        nc.sync.dma_start(out=bias_rows[:NODES, :], in_=b_m2.partition_broadcast(NODES))
+        load_words(w2_words, W_m2_words, 0, 0)
+        load_plane(planes_2, W_m2_scales, 0, 2, 0)
+        load_words(w2_words, W_m2_words, 0, 1)
+        load_plane(planes_2, W_m2_scales, 0, 2, 1)
+        load_e(4, 2)
+        load_plane(planes_2, W_m2_scales, 0, 2, 2)
+        load_e(6, 2)
+        load_plane(planes_2, W_m2_scales, 0, 2, 3)
         load_e(8, 4)
         load_e(12, 4)
 
@@ -167,16 +174,15 @@ def tile_messagepassing_pa_kernel(
             )
             return grouped
 
-        def node_term_rows(words, first_group, a):
+        def node_term_rows(words, planes, a):
             bank = banks.tile([P, N_TILE], F32, tag="bank")
             for c in range(PASSES):
-                row = PLANE_ROWS * (first_group + c)
                 nc.tensor.matmul_mx(
                     out=bank[:],
                     lhsT=h_codes[:, P * c : P * (c + 1)].bitcast(FP8X4),
                     lhsT_scale=h_planes[:, P * c : P * (c + 1)],
                     rhs=words[a][:, c, :].bitcast(FP8X4),
-                    rhs_scale=planes_n[row:P, N_TILE * a : N_TILE * (a + 1)],
+                    rhs_scale=planes[PLANE_ROWS * c : P, N_TILE * a : N_TILE * (a + 1)],
                     start=(c == 0),
                     stop=(c == PASSES - 1),
                 )
@@ -211,10 +217,10 @@ def tile_messagepassing_pa_kernel(
                 in_=we_raw[a][:, c, :].rearrange("p (m t) -> p t m", t=PACK),
             )
 
-        def permute_planes(engine, a):
-            engine.tensor_copy(
+        def permute_planes(a):
+            nc.vector.tensor_copy(
                 out=planes_e[:, N_TILE * a : N_TILE * (a + 1)].rearrange("p (t m) -> p m t", t=PACK),
-                in_=planes_e_raw[:, N_TILE * a : N_TILE * (a + 1)].rearrange("p (m t) -> p m t", t=PACK),
+                in_=planes_je[:, N_TILE * a : N_TILE * (a + 1)].rearrange("p (m t) -> p m t", t=PACK),
             )
 
         node_sums = {}
@@ -284,7 +290,7 @@ def tile_messagepassing_pa_kernel(
                     nc.tensor.matmul_mx(
                         out=bank[:, t, :],
                         lhsT=we_words[a][:, c, P * t : P * (t + 1)].bitcast(FP8X4),
-                        lhsT_scale=planes_e[PLANE_ROWS * c : P, plane : plane + P],
+                        lhsT_scale=planes_e[PLANE_ROWS * (PASSES + c) : P, plane : plane + P],
                         rhs=e_codes[:, j, P * c : P * (c + 1)].bitcast(FP8X4),
                         rhs_scale=e_planes[:, j, P * c : P * (c + 1)],
                         start=(c == 0),
@@ -293,7 +299,7 @@ def tile_messagepassing_pa_kernel(
             edge_banks[j, a] = bank
 
         def add_terms(step, a, j):
-            pre_relu = stage.tile([P, P, PACK], BF16)
+            pre_relu = pre_pool.tile([P, P, PACK], BF16)
             nc.vector.tensor_tensor(
                 out=pre_relu[:],
                 in0=edge_banks[j, a][:].rearrange("p t r -> p r t"),
@@ -312,7 +318,7 @@ def tile_messagepassing_pa_kernel(
             )
 
         def add_and_relu_in_parts(step, a, j):
-            pre_relu = stage.tile([P, P, PACK], BF16)
+            pre_relu = pre_pool.tile([P, P, PACK], BF16)
             hidden = hiddens[j][:, N_TILE * a : N_TILE * (a + 1)].rearrange("p (r t) -> p r t", t=PACK)
             for part in range(2):
                 rows = slice(P // 2 * part, P // 2 * (part + 1))
@@ -380,24 +386,26 @@ def tile_messagepassing_pa_kernel(
         h_grouped = group_rows(flip_unsorted_rows(h_rows[:]))
         warm(2)
         nc.vector.quantize_mx(out=h_codes[:].bitcast(FP8X4), scales=h_planes[:], in_=h_grouped[:])
-        source_rows = node_term_rows(wj_words, 2, 0)
-        target_rows = node_term_rows(wi_words, 0, 0)
-        permute_planes(nc.vector, 0)
-        permute_planes(nc.gpsimd, 1)
+        permute_planes(0)
+        source_rows = node_term_rows(wj_words, planes_je, 0)
+        target_rows = node_term_rows(wi_words, planes_i, 0)
         source_sorted = sort_term(nc.vector.tensor_copy, source_rows)
         target_sorted = sort_term(nc.scalar.copy, target_rows)
+        permute_planes(1)
         flipped_e[0] = flip_unsorted_rows(e_rows[:, 0, :])
         source_bank = flip_term(source_sorted)
-        grouped_e[0] = group_rows(flipped_e[0])
         kept_bank = flip_term(target_sorted, kept)
+        grouped_e[0] = group_rows(flipped_e[0])
+        keep_target(0, kept_bank)
         for c in range(PASSES):
             permute_words(c, 0)
-        quantise_edges(0)
-        keep_target(0, kept_bank)
         keep_source(0, source_bank)
+        quantise_edges(0)
         warm(1)
+        flipped_e[1] = flip_unsorted_rows(e_rows[:, 1, :])
+        grouped_e[1] = group_rows(flipped_e[1])
         first_layer(0, 0)
-        source_rows = node_term_rows(wj_words, 2, 1)
+        source_rows = node_term_rows(wj_words, planes_je, 1)
         source_sorted = sort_term(nc.scalar.copy, source_rows)
         new_sum(0)
         handed[0] = stage.tile([P, BLOCKS, PACK], F32, name="handed")
@@ -405,10 +413,8 @@ def tile_messagepassing_pa_kernel(
         add_blocks(nc.gpsimd, 0, 0, GRAPHS, handed[0][:, :GRAPHS])
         new_sum(-LEAD)
         sum_from_bank(-LEAD, 0, kept_bank, GRAPHS)
-        target_rows = node_term_rows(wi_words, 0, 1)
+        target_rows = node_term_rows(wi_words, planes_i, 1)
         target_sorted = sort_term(nc.scalar.copy, target_rows)
-        flipped_e[1] = flip_unsorted_rows(e_rows[:, 1, :])
-        grouped_e[1] = group_rows(flipped_e[1])
         pre_relu_00 = add_terms(-LEAD, 0, 0)
         for c in range(PASSES):
             permute_words(c, 1)
@@ -420,8 +426,9 @@ def tile_messagepassing_pa_kernel(
         quantise_edges(1)
         sum_from_bank(0, 1, target_bank, GRAPHS)
         keep_target(1, target_bank)
-        flipped_e[2] = flip_unsorted_rows(e_rows[:, 2, :])
+        relu(0, 0, pre_relu_00)
         first_layer(1, 0)
+        flipped_e[2] = flip_unsorted_rows(e_rows[:, 2, :])
 
         first_banks = []
         for half in range(HALVES):
@@ -435,29 +442,27 @@ def tile_messagepassing_pa_kernel(
             )
             first_banks.append(first_bank)
         grouped_e[2] = group_rows(flipped_e[2])
-        relu(0, 0, pre_relu_00)
         hand_source(1)
         sum_node_terms(1)
+        pre_relu_10 = add_terms(0, 0, 1)
         pre_relu_01 = add_terms(0, 1, 0)
         turned_bank = flips.tile([P, P], BF16, tag="flip")
         nc.tensor.transpose(turned_bank[:], mask_bf16[:], ident_bf16[:])
         nc.scalar.copy(out=mask_turned[:], in_=turned_bank[:])
         relu(0, 1, pre_relu_01)
-        pre_relu_10 = add_terms(0, 0, 1)
         quantise_edges(2)
         flipped_e[3] = flip_unsorted_rows(e_rows[:, 3, :])
         grouped_e[3] = group_rows(flipped_e[3])
-        relu(1, 0, pre_relu_10)
-
-        nc.vector.tensor_copy(out=mask_f32[:], in_=mask_bf16[:, :NODES])
-        for a, j in halves_of(1):
-            first_layer(j, a)
         for half in range(HALVES):
             columns = slice(N_TILE * half, N_TILE * (half + 1))
             nc.tensor.matmul(
                 out=first_banks[half][:], lhsT=mask_turned[:], rhs=bias_rows[:, columns], start=False, stop=True
             )
             nc.scalar.copy(out=result[:, columns], in_=first_banks[half][:])
+        relu(1, 0, pre_relu_10)
+        nc.vector.tensor_copy(out=mask_f32[:], in_=mask_bf16[:, :NODES])
+        for a, j in halves_of(1):
+            first_layer(j, a)
 
         rows_out = out.rearrange("b i n -> (b i) n")
         for step in range(1, NODES):

@@ -405,29 +405,35 @@ def tile_messagepassing_pa_kernel(
         flipped_e[1] = flip_unsorted_rows(e_rows[:, 1, :])
         grouped_e[1] = group_rows(flipped_e[1])
         first_layer(0, 0)
-        source_rows = node_term_rows(wj_words, planes_je, 1)
-        source_sorted = sort_term(nc.scalar.copy, source_rows)
         new_sum(0)
         handed[0] = stage.tile([P, BLOCKS, PACK], F32, name="handed")
         nc.vector.tensor_copy(out=handed[0][:, :GRAPHS], in_=source_blocks(0, 0, GRAPHS))
         add_blocks(nc.gpsimd, 0, 0, GRAPHS, handed[0][:, :GRAPHS])
+        new_sum(1)
         new_sum(-LEAD)
         sum_from_bank(-LEAD, 0, kept_bank, GRAPHS)
+        source_rows = node_term_rows(wj_words, planes_je, 1)
+        source_sorted = sort_term(nc.scalar.copy, source_rows)
+        pre_relu_00 = add_terms(-LEAD, 0, 0)
+        quantise_edges(1)
+        handed[1] = stage.tile([P, BLOCKS, PACK], F32, name="handed")
+        nc.vector.tensor_copy(out=handed[1][:, :GRAPHS], in_=source_blocks(1, 0, GRAPHS))
+        add_blocks(nc.gpsimd, 1, 0, GRAPHS, handed[1][:, :GRAPHS])
+        first_layer(1, 0)
         target_rows = node_term_rows(wi_words, planes_i, 1)
         target_sorted = sort_term(nc.scalar.copy, target_rows)
-        pre_relu_00 = add_terms(-LEAD, 0, 0)
+        pre_relu_10 = add_terms(0, 0, 1)
         for c in range(PASSES):
             permute_words(c, 1)
 
         source_bank = flip_term(source_sorted)
+        relu(0, 0, pre_relu_00)
         target_bank = flip_term(target_sorted)
         first_layer(0, 1)
         keep_source(1, source_bank)
-        quantise_edges(1)
-        sum_from_bank(0, 1, target_bank, GRAPHS)
         keep_target(1, target_bank)
-        relu(0, 0, pre_relu_00)
-        first_layer(1, 0)
+        sum_from_bank(0, 1, target_bank, GRAPHS)
+        relu(1, 0, pre_relu_10)
         flipped_e[2] = flip_unsorted_rows(e_rows[:, 2, :])
 
         first_banks = []
@@ -442,9 +448,8 @@ def tile_messagepassing_pa_kernel(
             )
             first_banks.append(first_bank)
         grouped_e[2] = group_rows(flipped_e[2])
-        hand_source(1)
-        sum_node_terms(1)
-        pre_relu_10 = add_terms(0, 0, 1)
+        nc.vector.tensor_copy(out=handed[1][:, GRAPHS:], in_=source_blocks(1, GRAPHS, BLOCKS))
+        add_blocks(nc.gpsimd, 1, GRAPHS, BLOCKS, handed[1][:, GRAPHS:])
         pre_relu_01 = add_terms(0, 1, 0)
         turned_bank = flips.tile([P, P], BF16, tag="flip")
         nc.tensor.transpose(turned_bank[:], mask_bf16[:], ident_bf16[:])
@@ -459,7 +464,6 @@ def tile_messagepassing_pa_kernel(
                 out=first_banks[half][:], lhsT=mask_turned[:], rhs=bias_rows[:, columns], start=False, stop=True
             )
             nc.scalar.copy(out=result[:, columns], in_=first_banks[half][:])
-        relu(1, 0, pre_relu_10)
         nc.vector.tensor_copy(out=mask_f32[:], in_=mask_bf16[:, :NODES])
         for a, j in halves_of(1):
             first_layer(j, a)
@@ -476,6 +480,8 @@ def tile_messagepassing_pa_kernel(
                 quantise_edges(step + LEAD + 1)
             if step == 1:
                 flipped_e[4] = flip_unsorted_rows(e_rows[:, 4, :])
+            if step == 2:
+                flipped_e[6] = flip_unsorted_rows(e_rows[:, 6, :])
             if step == NODES - 1:
                 open_hidden(step)
                 quantise_hidden_half(step, 0)
@@ -499,7 +505,7 @@ def tile_messagepassing_pa_kernel(
                 for a, j in halves_of(step + 1):
                     first_layer(j, a)
             if step % 2 == 1:
-                for j in range(step + LEAD + 3, min(step + LEAD + 5, NODES)):
+                for j in range(step + LEAD + 3, min(step + LEAD + 5, NODES) if step > 1 else step + LEAD + 4):
                     if j < UNSORTED:
                         flipped_e[j] = flip_unsorted_rows(e_rows[:, j, :])
                     else:

@@ -53,19 +53,19 @@ def tile_messagepassing_pa_kernel(
         ident_f32 = keep.tile([P, P], F32)
         h_rows = keep.tile([P, WIDTH], BF16)
         e_rows = keep.tile([P, NODES, WIDTH], BF16)
-        wi_words = [keep.tile([P, PASSES, N_TILE], I32, align_bytes=64, name=f"wi_{a}") for a in range(HALVES)]
-        wj_words = [keep.tile([P, PASSES, N_TILE], I32, align_bytes=64, name=f"wj_{a}") for a in range(HALVES)]
-        we_raw = [keep.tile([P, PASSES, N_TILE], I32, align_bytes=64, name=f"we_raw_{a}") for a in range(HALVES)]
-        we_words = [keep.tile([P, PASSES, N_TILE], I32, align_bytes=64, name=f"we_{a}") for a in range(HALVES)]
-        w2_words = [keep.tile([P, PASSES, N_TILE], I32, align_bytes=64, name=f"w2_{a}") for a in range(HALVES)]
-        planes_i = keep.tile([P, WIDTH], U8, align_bytes=64)
-        planes_je = keep.tile([P, WIDTH], U8, align_bytes=64)
-        planes_e = keep.tile([P, WIDTH], U8, align_bytes=64)
-        planes_2 = keep.tile([P, WIDTH], U8, align_bytes=64)
-        h_codes = keep.tile([P, PASSES * P], U32, align_bytes=64)
-        h_planes = keep.tile([P, PASSES * P], U8, align_bytes=64)
-        e_codes = keep.tile([P, NODES, PASSES * P], U32, align_bytes=64)
-        e_planes = keep.tile([P, NODES, PASSES * P], U8, align_bytes=64)
+        wi_words = [keep.tile([P, PASSES, N_TILE], I32, align_bytes=256, name=f"wi_{a}") for a in range(HALVES)]
+        wj_words = [keep.tile([P, PASSES, N_TILE], I32, align_bytes=256, name=f"wj_{a}") for a in range(HALVES)]
+        we_raw = [keep.tile([P, PASSES, N_TILE], I32, align_bytes=256, name=f"we_raw_{a}") for a in range(HALVES)]
+        we_words = [keep.tile([P, PASSES, N_TILE], I32, align_bytes=256, name=f"we_{a}") for a in range(HALVES)]
+        w2_words = [keep.tile([P, PASSES, N_TILE], I32, align_bytes=256, name=f"w2_{a}") for a in range(HALVES)]
+        planes_i = keep.tile([P, WIDTH], U8, align_bytes=256)
+        planes_je = keep.tile([P, WIDTH], U8, align_bytes=256)
+        planes_e = keep.tile([P, WIDTH], U8, align_bytes=256)
+        planes_2 = keep.tile([P, WIDTH], U8, align_bytes=256)
+        h_codes = keep.tile([P, PASSES * P], U32, align_bytes=256)
+        h_planes = keep.tile([P, PASSES * P], U8, align_bytes=256)
+        e_codes = keep.tile([P, NODES, PASSES * P], U32, align_bytes=256)
+        e_planes = keep.tile([P, NODES, PASSES * P], U8, align_bytes=256)
         ones = keep.tile([P, N_TILE], BF16)
         ident_bf16 = keep.tile([P, P], BF16)
         bias_rows = keep.tile([P, WIDTH], BF16)
@@ -167,7 +167,7 @@ def tile_messagepassing_pa_kernel(
             return flipped
 
         def group_rows(flipped):
-            grouped = stage.tile([P, PASSES * P * PACK], BF16, align_bytes=64)
+            grouped = stage.tile([P, PASSES * P * PACK], BF16, align_bytes=256)
             nc.scalar.copy(
                 out=grouped[:].bitcast(F32).rearrange("p (c r u) -> p c r u", c=PASSES, u=2),
                 in_=flipped[:].rearrange("p c u r -> p c r u"),
@@ -310,7 +310,7 @@ def tile_messagepassing_pa_kernel(
 
         def relu(j, a, pre_relu):
             if a == 0:
-                hiddens[j] = hidden_pool.tile([P, WIDTH], BF16, align_bytes=64, name="hidden")
+                hiddens[j] = hidden_pool.tile([P, WIDTH], BF16, align_bytes=256, name="hidden")
             nc.scalar.activation(
                 out=hiddens[j][:, N_TILE * a : N_TILE * (a + 1)],
                 in_=pre_relu[:].rearrange("p r t -> p (r t)"),
@@ -331,8 +331,8 @@ def tile_messagepassing_pa_kernel(
                 nc.scalar.activation(out=hidden[:, rows, :], in_=pre_relu[:, rows, :], func=RELU)
 
         def open_hidden(j):
-            r_codes = stage.tile([P, PASSES * P], U32, align_bytes=64)
-            r_planes = stage.tile([P, PASSES * P], U8, align_bytes=64)
+            r_codes = stage.tile([P, PASSES * P], U32, align_bytes=256)
+            r_planes = stage.tile([P, PASSES * P], U8, align_bytes=256)
             r_operands[j] = (r_codes, r_planes)
 
         def quantise_hidden(j):

@@ -50,9 +50,9 @@ def tile_messagepassing_pa_kernel(
         flips = stack.enter_context(tc.psum_pool(name="flips", bufs=2))
         stack.enter_context(tc.manual_schedule())
 
-        ident_f32 = keep.tile([P, P], F32)
-        h_rows = keep.tile([P, WIDTH], BF16)
-        e_rows = keep.tile([P, NODES, WIDTH], BF16)
+        ident_f32 = keep.tile([P, P], F32, align_bytes=256)
+        h_rows = keep.tile([P, WIDTH], BF16, align_bytes=256)
+        e_rows = keep.tile([P, NODES, WIDTH], BF16, align_bytes=256)
         wi_words = [keep.tile([P, PASSES, N_TILE], I32, align_bytes=256, name=f"wi_{a}") for a in range(HALVES)]
         wj_words = [keep.tile([P, PASSES, N_TILE], I32, align_bytes=256, name=f"wj_{a}") for a in range(HALVES)]
         we_raw = [keep.tile([P, PASSES, N_TILE], I32, align_bytes=256, name=f"we_raw_{a}") for a in range(HALVES)]
@@ -66,16 +66,16 @@ def tile_messagepassing_pa_kernel(
         h_planes = keep.tile([P, PASSES * P], U8, align_bytes=256)
         e_codes = keep.tile([P, NODES, PASSES * P], U32, align_bytes=256)
         e_planes = keep.tile([P, NODES, PASSES * P], U8, align_bytes=256)
-        ones = keep.tile([P, N_TILE], BF16)
-        ident_bf16 = keep.tile([P, P], BF16)
-        bias_rows = keep.tile([P, WIDTH], BF16)
-        b1_cols = keep.tile([P, HALVES, PACK], BF16)
-        mask_bf16 = keep.tile([P, P], BF16)
-        mask_turned = keep.tile([P, P], BF16)
-        mask_f32 = keep.tile([P, NODES], F32)
-        target_term = keep.tile([P, HALVES, P, PACK], F32)
-        source_term = keep.tile([P, HALVES * TERM + PACK * (NODES + LEAD)], F32)
-        result = keep.tile([P, WIDTH], F32)
+        ones = keep.tile([P, N_TILE], BF16, align_bytes=256)
+        ident_bf16 = keep.tile([P, P], BF16, align_bytes=256)
+        bias_rows = keep.tile([P, WIDTH], BF16, align_bytes=256)
+        b1_cols = keep.tile([P, HALVES, PACK], BF16, align_bytes=256)
+        mask_bf16 = keep.tile([P, P], BF16, align_bytes=256)
+        mask_turned = keep.tile([P, P], BF16, align_bytes=256)
+        mask_f32 = keep.tile([P, NODES], F32, align_bytes=256)
+        target_term = keep.tile([P, HALVES, P, PACK], F32, align_bytes=256)
+        source_term = keep.tile([P, HALVES * TERM + PACK * (NODES + LEAD)], F32, align_bytes=256)
+        result = keep.tile([P, WIDTH], F32, align_bytes=256)
 
         make_identity(nc, ident_f32[:])
         nc.vector.memset(planes_je[:].bitcast(I32), 0)
@@ -145,7 +145,7 @@ def tile_messagepassing_pa_kernel(
         load_e(12, 4)
 
         def sort_words(rows):
-            sorted_words = sorts.tile([P, PASSES, 2, P], F32)
+            sorted_words = sorts.tile([P, PASSES, 2, P], F32, align_bytes=256)
             nc.scalar.copy(
                 out=sorted_words[:], in_=rows.bitcast(F32).rearrange("r (c p u) -> r c u p", c=PASSES, u=2)
             )
@@ -189,7 +189,7 @@ def tile_messagepassing_pa_kernel(
             return bank
 
         def sort_term(copy, rows_bank):
-            sorted_rows = stage.tile([P, PACK, P], F32)
+            sorted_rows = stage.tile([P, PACK, P], F32, align_bytes=256)
             copy(out=sorted_rows[:], in_=rows_bank[:].rearrange("r (p t) -> r t p", t=PACK))
             return sorted_rows
 
@@ -237,7 +237,7 @@ def tile_messagepassing_pa_kernel(
             return [(a, j) for a, j in ((0, step + LEAD), (1, step)) if 0 <= j < NODES]
 
         def new_sum(step):
-            node_sums[step] = sums.tile([P, HALVES, P, PACK], F32, name="node_sum")
+            node_sums[step] = sums.tile([P, HALVES, P, PACK], F32, align_bytes=256, name="node_sum")
 
         def source_blocks(step, first, last):
             start = PACK * (step + LEAD)
@@ -269,7 +269,7 @@ def tile_messagepassing_pa_kernel(
 
         def hand_source(step):
             first, last = gpsimd_blocks(step)
-            handed[step] = stage.tile([P, BLOCKS, PACK], F32, name="handed")
+            handed[step] = stage.tile([P, BLOCKS, PACK], F32, align_bytes=256, name="handed")
             nc.vector.tensor_copy(out=handed[step][:, first:last], in_=source_blocks(step, first, last))
 
         def sum_node_terms(step):
@@ -299,7 +299,7 @@ def tile_messagepassing_pa_kernel(
             edge_banks[j, a] = bank
 
         def add_terms(step, a, j):
-            pre_relu = pre_pool.tile([P, P, PACK], BF16)
+            pre_relu = pre_pool.tile([P, P, PACK], BF16, align_bytes=256)
             nc.vector.tensor_tensor(
                 out=pre_relu[:],
                 in0=edge_banks[j, a][:].rearrange("p t r -> p r t"),
@@ -318,7 +318,7 @@ def tile_messagepassing_pa_kernel(
             )
 
         def add_and_relu_in_parts(step, a, j):
-            pre_relu = pre_pool.tile([P, P, PACK], BF16)
+            pre_relu = pre_pool.tile([P, P, PACK], BF16, align_bytes=256)
             hidden = hiddens[j][:, N_TILE * a : N_TILE * (a + 1)].rearrange("p (r t) -> p r t", t=PACK)
             for part in range(2):
                 rows = slice(P // 2 * part, P // 2 * (part + 1))
@@ -406,7 +406,7 @@ def tile_messagepassing_pa_kernel(
         grouped_e[1] = group_rows(flipped_e[1])
         first_layer(0, 0)
         new_sum(0)
-        handed[0] = stage.tile([P, BLOCKS, PACK], F32, name="handed")
+        handed[0] = stage.tile([P, BLOCKS, PACK], F32, align_bytes=256, name="handed")
         nc.vector.tensor_copy(out=handed[0][:, :GRAPHS], in_=source_blocks(0, 0, GRAPHS))
         add_blocks(nc.gpsimd, 0, 0, GRAPHS, handed[0][:, :GRAPHS])
         new_sum(1)
@@ -416,7 +416,7 @@ def tile_messagepassing_pa_kernel(
         source_sorted = sort_term(nc.scalar.copy, source_rows)
         pre_relu_00 = add_terms(-LEAD, 0, 0)
         quantise_edges(1)
-        handed[1] = stage.tile([P, BLOCKS, PACK], F32, name="handed")
+        handed[1] = stage.tile([P, BLOCKS, PACK], F32, align_bytes=256, name="handed")
         nc.vector.tensor_copy(out=handed[1][:, :GRAPHS], in_=source_blocks(1, 0, GRAPHS))
         add_blocks(nc.gpsimd, 1, 0, GRAPHS, handed[1][:, :GRAPHS])
         first_layer(1, 0)

from contextlib import ExitStack

import concourse.mybir as mybir
from concourse.masks import make_identity

F32 = mybir.dt.float32
BF16 = mybir.dt.bfloat16
I32 = mybir.dt.int32
U32 = mybir.dt.uint32
U8 = mybir.dt.uint8
FP8X4 = mybir.dt.float8_e4m3fn_x4
ADD = mybir.AluOpType.add
MULT = mybir.AluOpType.mult
RELU = mybir.ActivationFunctionType.Relu

P = 128
GRAPHS = 8
NODES = 16
WIDTH = 1024
PACK = 4
K_PASS = P * PACK
PASSES = WIDTH // K_PASS
N_TILE = 512
HALVES = WIDTH // N_TILE
PLANE_ROWS = 4
QUADRANT = 32
BLOCKS = HALVES * GRAPHS
VECTOR_BLOCKS = 1
LEAD = 1
TERM = P * PACK
BLOCK = NODES * PACK
UNSORTED = 7

FLOPS = 2 * (2 * GRAPHS * NODES * NODES + 2 * GRAPHS * NODES) * WIDTH * WIDTH


def tile_messagepassing_pa_kernel(
    tc, h, e, adj_mask, W_m1_words, W_m1_scales, b_m1, W_m2_words, W_m2_scales, b_m2, out
):
    nc = tc.nc
    with ExitStack() as stack:
        keep = stack.enter_context(tc.tile_pool(name="keep", bufs=1))
        stage = stack.enter_context(tc.tile_pool(name="stage", bufs=3))
        sorts = stack.enter_context(tc.tile_pool(name="sorts", bufs=4))
        sums = stack.enter_context(tc.tile_pool(name="sums", bufs=3))
        pre_pool = stack.enter_context(tc.tile_pool(name="pre_relu", bufs=6))
        hidden_pool = stack.enter_context(tc.tile_pool(name="hidden", bufs=LEAD + 3))
        banks = stack.enter_context(tc.psum_pool(name="banks", bufs=5))
        kept = stack.enter_context(tc.psum_pool(name="kept", bufs=1))
        flips = stack.enter_context(tc.psum_pool(name="flips", bufs=2))
        stack.enter_context(tc.manual_schedule())

        ident_f32 = keep.tile([P, P], F32, align_bytes=256)
        h_rows = keep.tile([P, WIDTH], BF16, align_bytes=256)
        e_rows = keep.tile([P, NODES, WIDTH], BF16, align_bytes=256)
        wi_words = [keep.tile([P, PASSES, N_TILE], I32, align_bytes=256, name=f"wi_{a}") for a in range(HALVES)]
        wj_words = [keep.tile([P, PASSES, N_TILE], I32, align_bytes=256, name=f"wj_{a}") for a in range(HALVES)]
        we_raw = [keep.tile([P, PASSES, N_TILE], I32, align_bytes=256, name=f"we_raw_{a}") for a in range(HALVES)]
        we_words = [keep.tile([P, PASSES, N_TILE], I32, align_bytes=256, name=f"we_{a}") for a in range(HALVES)]
        w2_words = [keep.tile([P, PASSES, N_TILE], I32, align_bytes=256, name=f"w2_{a}") for a in range(HALVES)]
        planes_i = keep.tile([P, WIDTH], U8, align_bytes=256)
        planes_je = keep.tile([P, WIDTH], U8, align_bytes=256)
        planes_e = keep.tile([P, WIDTH], U8, align_bytes=256)
        planes_2 = keep.tile([P, WIDTH], U8, align_bytes=256)
        h_codes = keep.tile([P, PASSES * P], U32, align_bytes=256)
        h_planes = keep.tile([P, PASSES * P], U8, align_bytes=256)
        e_codes = keep.tile([P, NODES, PASSES * P], U32, align_bytes=256)
        e_planes = keep.tile([P, NODES, PASSES * P], U8, align_bytes=256)
        ones = keep.tile([P, N_TILE], BF16, align_bytes=256)
        ident_bf16 = keep.tile([P, P], BF16, align_bytes=256)
        bias_rows = keep.tile([P, WIDTH], BF16, align_bytes=256)
        b1_cols = keep.tile([P, HALVES, PACK], BF16, align_bytes=256)
        mask_bf16 = keep.tile([P, P], BF16, align_bytes=256)
        mask_turned = keep.tile([P, P], BF16, align_bytes=256)
        mask_f32 = keep.tile([P, NODES], F32, align_bytes=256)
        target_term = keep.tile([P, HALVES, P, PACK], F32, align_bytes=256)
        source_term = keep.tile([P, HALVES * TERM + PACK * (NODES + LEAD)], F32, align_bytes=256)
        result = keep.tile([P, WIDTH], F32, align_bytes=256)

        make_identity(nc, ident_f32[:])
        nc.vector.memset(planes_je[:].bitcast(I32), 0)
        nc.vector.memset(ones[:], 1.0)
        nc.vector.memset(mask_bf16[:].bitcast(I32), 0)
        nc.vector.memset(bias_rows[:].bitcast(I32), 0)
        nc.vector.memset(planes_i[:].bitcast(I32), 0)
        nc.vector.memset(planes_2[:].bitcast(I32), 0)
        nc.vector.tensor_copy(out=ident_bf16[:], in_=ident_f32[:])

        def warm(turns):
            warm_bank = banks.tile([P, N_TILE], F32, tag="bank")
            for turn in range(turns):
                nc.tensor.matmul(out=warm_bank[:], lhsT=ones[:, :P], rhs=ones[:], start=True, stop=True)

        warm(4)

        def load_words(tiles, dram, first, a):
            nc.sync.dma_start(
                out=tiles[a][:],
                in_=dram[first : first + PASSES, :, N_TILE * a : N_TILE * (a + 1), :]
                .rearrange("g p n t -> p g (n t)")
                .bitcast(I32),
            )

        def load_plane(tile, dram, first, count, q):
            nc.sync.dma_start(
                out=tile[QUADRANT * q : QUADRANT * q + PLANE_ROWS * count, :].bitcast(I32),
                in_=dram[first : first + count, PLANE_ROWS * q : PLANE_ROWS * (q + 1), :].bitcast(I32),
            )

        def load_planes(tile, dram, first, count):
            for q in range(P // QUADRANT):
                load_plane(tile, dram, first, count, q)

        def load_e(first, count):
            nc.sync.dma_start(
                out=e_rows[:, first : first + count, :].rearrange("r j k -> r (j k)"),
                in_=e[:, :, first : first + count, :].rearrange("b i j k -> (b i) (j k)"),
            )

        nc.sync.dma_start(out=h_rows[:], in_=h.rearrange("b i k -> (b i) k"))
        load_planes(planes_je, W_m1_scales, 2, 4)
        load_words(wj_words, W_m1_words, 2, 0)
        load_words(wi_words, W_m1_words, 0, 0)
        load_e(0, 1)
        load_planes(planes_i, W_m1_scales, 0, 2)
        load_words(we_raw, W_m1_words, 4, 0)
        nc.sync.dma_start(out=b1_cols[:], in_=b_m1.rearrange("(a p t) -> p a t", a=HALVES, t=PACK))
        load_e(1, 1)
        load_words(wj_words, W_m1_words, 2, 1)
        load_words(wi_words, W_m1_words, 0, 1)
        load_words(we_raw, W_m1_words, 4, 1)
        load_e(2, 1)
        nc.sync.dma_start(out=mask_bf16[:, :NODES], in_=adj_mask.rearrange("b i j o -> (b i) (j o)"))
        load_e(3, 1)
        nc.sync.dma_start(out=bias_rows[:NODES, :], in_=b_m2.partition_broadcast(NODES))
        load_words(w2_words, W_m2_words, 0, 0)
        load_plane(planes_2, W_m2_scales, 0, 2, 0)
        load_words(w2_words, W_m2_words, 0, 1)
        load_plane(planes_2, W_m2_scales, 0, 2, 1)
        load_e(4, 2)
        load_plane(planes_2, W_m2_scales, 0, 2, 2)
        load_e(6, 2)
        load_plane(planes_2, W_m2_scales, 0, 2, 3)
        load_e(8, 4)
        load_e(12, 4)

        def sort_words(rows):
            sorted_words = sorts.tile([P, PASSES, 2, P], F32, align_bytes=256)
            nc.scalar.copy(
                out=sorted_words[:], in_=rows.bitcast(F32).rearrange("r (c p u) -> r c u p", c=PASSES, u=2)
            )
            return sorted_words

        def flip_rows(sorted_words):
            flipped = flips.tile([P, PASSES, 2, P], F32, tag="flip")
            for c in range(PASSES):
                for u in range(2):
                    nc.tensor.transpose(flipped[:, c, u, :], sorted_words[:, c, u, :], ident_f32[:])
            return flipped

        def flip_unsorted_rows(rows):
            words = rows.bitcast(F32)
            flipped = flips.tile([P, PASSES, 2, P], F32, tag="flip")
            for c in range(PASSES):
                for u in range(2):
                    nc.tensor.transpose(flipped[:, c, u, :], words[:, 2 * P * c + u : 2 * P * (c + 1) : 2], ident_f32[:])
            return flipped

        def group_rows(flipped):
            grouped = stage.tile([P, PASSES * P * PACK], BF16, align_bytes=256)
            nc.scalar.copy(
                out=grouped[:].bitcast(F32).rearrange("p (c r u) -> p c r u", c=PASSES, u=2),
                in_=flipped[:].rearrange("p c u r -> p c r u"),
            )
            return grouped

        def node_term_rows(words, planes, a):
            bank = banks.tile([P, N_TILE], F32, tag="bank")
            for c in range(PASSES):
                nc.tensor.matmul_mx(
                    out=bank[:],
                    lhsT=h_codes[:, P * c : P * (c + 1)].bitcast(FP8X4),
                    lhsT_scale=h_planes[:, P * c : P * (c + 1)],
                    rhs=words[a][:, c, :].bitcast(FP8X4),
                    rhs_scale=planes[PLANE_ROWS * c : P, N_TILE * a : N_TILE * (a + 1)],
                    start=(c == 0),
                    stop=(c == PASSES - 1),
                )
            return bank

        def sort_term(copy, rows_bank):
            sorted_rows = stage.tile([P, PACK, P], F32, align_bytes=256)
            copy(out=sorted_rows[:], in_=rows_bank[:].rearrange("r (p t) -> r t p", t=PACK))
            return sorted_rows

        def flip_term(sorted_rows, pool=banks):
            bank = pool.tile([P, PACK, P], F32, tag="bank")
            for t in range(PACK):
                nc.tensor.transpose(bank[:, t, :], sorted_rows[:, t, :], ident_f32[:])
            return bank

        def keep_source(a, bank):
            first = a * (TERM + PACK * LEAD)
            nc.vector.tensor_tensor(
                out=source_term[:, first : first + TERM].rearrange("p (r t) -> p r t", t=PACK),
                in0=bank[:].rearrange("p t r -> p r t"),
                in1=b1_cols[:, a, :].unsqueeze(1).to_broadcast([P, P, PACK]),
                op=ADD,
            )

        def keep_target(a, bank):
            nc.scalar.copy(out=target_term[:, a], in_=bank[:].rearrange("p t r -> p r t"))

        def permute_words(c, a):
            nc.vector.tensor_copy(
                out=we_words[a][:, c, :].rearrange("p (t m) -> p t m", t=PACK),
                in_=we_raw[a][:, c, :].rearrange("p (m t) -> p t m", t=PACK),
            )

        def permute_planes(a):
            nc.vector.tensor_copy(
                out=planes_e[:, N_TILE * a : N_TILE * (a + 1)].rearrange("p (t m) -> p m t", t=PACK),
                in_=planes_je[:, N_TILE * a : N_TILE * (a + 1)].rearrange("p (m t) -> p m t", t=PACK),
            )

        node_sums = {}
        handed = {}
        sorted_e = {}
        flipped_e = {}
        grouped_e = {}
        edge_banks = {}
        hiddens = {}
        r_operands = {}
        message_banks = {}

        def halves_of(step):
            return [(a, j) for a, j in ((0, step + LEAD), (1, step)) if 0 <= j < NODES]

        def new_sum(step):
            node_sums[step] = sums.tile([P, HALVES, P, PACK], F32, align_bytes=256, name="node_sum")

        def source_blocks(step, first, last):
            start = PACK * (step + LEAD)
            words = source_term[:, start + BLOCK * first : start + BLOCK * last]
            return words.rearrange("p (k x) -> p k x", x=BLOCK)[:, :, :PACK]

        def add_blocks(engine, step, first, last, source):
            blocks = "p a (b i) t -> p (a b) i t"
            engine.tensor_tensor(
                out=node_sums[step][:].rearrange(blocks, i=NODES)[:, first:last],
                in0=target_term[:].rearrange(blocks, i=NODES)[:, first:last],
                in1=source.unsqueeze(2).to_broadcast([P, last - first, NODES, PACK]),
                op=ADD,
            )

        def sum_from_bank(step, a, bank, count):
            nc.vector.tensor_tensor(
                out=node_sums[step][:, a].rearrange("p (b i) t -> p b i t", i=NODES)[:, :count],
                in0=bank[:].rearrange("p t (b i) -> p b i t", i=NODES)[:, :count],
                in1=source_blocks(step, GRAPHS * a, GRAPHS * a + count)
                .unsqueeze(2)
                .to_broadcast([P, count, NODES, PACK]),
                op=ADD,
            )

        def gpsimd_blocks(step):
            present = [a for a, j in halves_of(step)]
            return VECTOR_BLOCKS if len(present) == HALVES else GRAPHS * present[0], GRAPHS * (present[-1] + 1)

        def hand_source(step):
            first, last = gpsimd_blocks(step)
            handed[step] = stage.tile([P, BLOCKS, PACK], F32, align_bytes=256, name="handed")
            nc.vector.tensor_copy(out=handed[step][:, first:last], in_=source_blocks(step, first, last))

        def sum_node_terms(step):
            new_sum(step)
            first, last = gpsimd_blocks(step)
            add_blocks(nc.gpsimd, step, first, last, handed[step][:, first:last])
            if len(halves_of(step)) == HALVES:
                sum_from_bank(step, 0, kept_bank, VECTOR_BLOCKS)

        def quantise_edges(j):
            nc.vector.quantize_mx(out=e_codes[:, j, :].bitcast(FP8X4), scales=e_planes[:, j, :], in_=grouped_e[j][:])

        def first_layer(j, a):
            bank = banks.tile([P, PACK, P], F32, tag="bank")
            for t in range(PACK):
                plane = P * (PACK * a + t)
                for c in range(PASSES):
                    nc.tensor.matmul_mx(
                        out=bank[:, t, :],
                        lhsT=we_words[a][:, c, P * t : P * (t + 1)].bitcast(FP8X4),
                        lhsT_scale=planes_e[PLANE_ROWS * (PASSES + c) : P, plane : plane + P],
                        rhs=e_codes[:, j, P * c : P * (c + 1)].bitcast(FP8X4),
                        rhs_scale=e_planes[:, j, P * c : P * (c + 1)],
                        start=(c == 0),
                        stop=(c == PASSES - 1),
                    )
            edge_banks[j, a] = bank

        def add_terms(step, a, j):
            pre_relu = pre_pool.tile([P, P, PACK], BF16, align_bytes=256)
            nc.vector.tensor_tensor(
                out=pre_relu[:],
                in0=edge_banks[j, a][:].rearrange("p t r -> p r t"),
                in1=node_sums[step][:, a],
                op=ADD,
            )
            return pre_relu

        def relu(j, a, pre_relu):
            if a == 0:
                hiddens[j] = hidden_pool.tile([P, WIDTH], BF16, align_bytes=256, name="hidden")
            nc.scalar.activation(
                out=hiddens[j][:, N_TILE * a : N_TILE * (a + 1)],
                in_=pre_relu[:].rearrange("p r t -> p (r t)"),
                func=RELU,
            )

        def add_and_relu_in_parts(step, a, j):
            pre_relu = pre_pool.tile([P, P, PACK], BF16, align_bytes=256)
            hidden = hiddens[j][:, N_TILE * a : N_TILE * (a + 1)].rearrange("p (r t) -> p r t", t=PACK)
            for part in range(2):
                rows = slice(P // 2 * part, P // 2 * (part + 1))
                nc.vector.tensor_tensor(
                    out=pre_relu[:, rows, :],
                    in0=edge_banks[j, a][:].rearrange("p t r -> p r t")[:, rows, :],
                    in1=node_sums[step][:, a, rows, :],
                    op=ADD,
                )
                nc.scalar.activation(out=hidden[:, rows, :], in_=pre_relu[:, rows, :], func=RELU)

        def open_hidden(j):
            r_codes = stage.tile([P, PASSES * P], U32, align_bytes=256)
            r_planes = stage.tile([P, PASSES * P], U8, align_bytes=256)
            r_operands[j] = (r_codes, r_planes)

        def quantise_hidden(j):
            open_hidden(j)
            r_codes, r_planes = r_operands[j]
            nc.vector.quantize_mx(out=r_codes[:].bitcast(FP8X4), scales=r_planes[:], in_=hiddens[j][:])

        def quantise_hidden_half(j, c):
            r_codes, r_planes = r_operands[j]
            nc.vector.quantize_mx(
                out=r_codes[:, P * c : P * (c + 1)].bitcast(FP8X4),
                scales=r_planes[:, P * c : P * (c + 1)],
                in_=hiddens[j][:, K_PASS * c : K_PASS * (c + 1)],
            )

        def message_pass(j, half, c):
            r_codes, r_planes = r_operands[j]
            nc.tensor.matmul_mx(
                out=message_banks[j][half][:],
                lhsT=r_codes[:, P * c : P * (c + 1)].bitcast(FP8X4),
                lhsT_scale=r_planes[:, P * c : P * (c + 1)],
                rhs=w2_words[half][:, c, :].bitcast(FP8X4),
                rhs_scale=planes_2[PLANE_ROWS * c : P, N_TILE * half : N_TILE * (half + 1)],
                start=(c == 0),
                stop=(c == PASSES - 1),
            )

        def open_messages(j):
            message_banks[j] = []
            for half in range(HALVES):
                message_bank = banks.tile([P, N_TILE], F32, tag="bank")
                message_banks[j].append(message_bank)

        def second_layer(j):
            open_messages(j)
            for half in range(HALVES):
                for c in range(PASSES):
                    message_pass(j, half, c)

        def gather_messages(j, half, first=0, last=N_TILE):
            columns = result[:, N_TILE * half + first : N_TILE * half + last]
            nc.vector.scalar_tensor_tensor(
                out=columns,
                in0=message_banks[j][half][:, first:last],
                scalar=mask_f32[:, j : j + 1],
                in1=columns,
                op0=MULT,
                op1=ADD,
            )

        h_grouped = group_rows(flip_unsorted_rows(h_rows[:]))
        warm(2)
        nc.vector.quantize_mx(out=h_codes[:].bitcast(FP8X4), scales=h_planes[:], in_=h_grouped[:])
        permute_planes(0)
        source_rows = node_term_rows(wj_words, planes_je, 0)
        target_rows = node_term_rows(wi_words, planes_i, 0)
        source_sorted = sort_term(nc.vector.tensor_copy, source_rows)
        target_sorted = sort_term(nc.scalar.copy, target_rows)
        permute_planes(1)
        flipped_e[0] = flip_unsorted_rows(e_rows[:, 0, :])
        source_bank = flip_term(source_sorted)
        kept_bank = flip_term(target_sorted, kept)
        grouped_e[0] = group_rows(flipped_e[0])
        keep_target(0, kept_bank)
        for c in range(PASSES):
            permute_words(c, 0)
        keep_source(0, source_bank)
        quantise_edges(0)
        warm(1)
        flipped_e[1] = flip_unsorted_rows(e_rows[:, 1, :])
        grouped_e[1] = group_rows(flipped_e[1])
        first_layer(0, 0)
        new_sum(0)
        handed[0] = stage.tile([P, BLOCKS, PACK], F32, align_bytes=256, name="handed")
        nc.vector.tensor_copy(out=handed[0][:, :GRAPHS], in_=source_blocks(0, 0, GRAPHS))
        add_blocks(nc.gpsimd, 0, 0, GRAPHS, handed[0][:, :GRAPHS])
        new_sum(1)
        new_sum(-LEAD)
        sum_from_bank(-LEAD, 0, kept_bank, GRAPHS)
        source_rows = node_term_rows(wj_words, planes_je, 1)
        source_sorted = sort_term(nc.scalar.copy, source_rows)
        pre_relu_00 = add_terms(-LEAD, 0, 0)
        quantise_edges(1)
        handed[1] = stage.tile([P, BLOCKS, PACK], F32, align_bytes=256, name="handed")
        nc.vector.tensor_copy(out=handed[1][:, :GRAPHS], in_=source_blocks(1, 0, GRAPHS))
        add_blocks(nc.gpsimd, 1, 0, GRAPHS, handed[1][:, :GRAPHS])
        first_layer(1, 0)
        target_rows = node_term_rows(wi_words, planes_i, 1)
        target_sorted = sort_term(nc.scalar.copy, target_rows)
        pre_relu_10 = add_terms(0, 0, 1)
        for c in range(PASSES):
            permute_words(c, 1)

        source_bank = flip_term(source_sorted)
        relu(0, 0, pre_relu_00)
        target_bank = flip_term(target_sorted)
        first_layer(0, 1)
        keep_source(1, source_bank)
        keep_target(1, target_bank)
        sum_from_bank(0, 1, target_bank, GRAPHS)
        relu(1, 0, pre_relu_10)
        flipped_e[2] = flip_unsorted_rows(e_rows[:, 2, :])

        first_banks = []
        for half in range(HALVES):
            first_bank = banks.tile([P, N_TILE], F32, tag="bank")
            nc.tensor.matmul(
                out=first_bank[:],
                lhsT=ident_bf16[:],
                rhs=h_rows[:, N_TILE * half : N_TILE * (half + 1)],
                start=True,
                stop=False,
            )
            first_banks.append(first_bank)
        grouped_e[2] = group_rows(flipped_e[2])
        nc.vector.tensor_copy(out=handed[1][:, GRAPHS:], in_=source_blocks(1, GRAPHS, BLOCKS))
        add_blocks(nc.gpsimd, 1, GRAPHS, BLOCKS, handed[1][:, GRAPHS:])
        pre_relu_01 = add_terms(0, 1, 0)
        turned_bank = flips.tile([P, P], BF16, tag="flip")
        nc.tensor.transpose(turned_bank[:], mask_bf16[:], ident_bf16[:])
        nc.scalar.copy(out=mask_turned[:], in_=turned_bank[:])
        relu(0, 1, pre_relu_01)
        quantise_edges(2)
        flipped_e[3] = flip_unsorted_rows(e_rows[:, 3, :])
        grouped_e[3] = group_rows(flipped_e[3])
        for half in range(HALVES):
            columns = slice(N_TILE * half, N_TILE * (half + 1))
            nc.tensor.matmul(
                out=first_banks[half][:], lhsT=mask_turned[:], rhs=bias_rows[:, columns], start=False, stop=True
            )
            nc.scalar.copy(out=result[:, columns], in_=first_banks[half][:])
        nc.vector.tensor_copy(out=mask_f32[:], in_=mask_bf16[:, :NODES])
        for a, j in halves_of(1):
            first_layer(j, a)

        rows_out = out.rearrange("b i n -> (b i) n")
        for step in range(1, NODES):
            if 1 < step < NODES - LEAD - 2:
                grouped_e[step + LEAD + 2] = group_rows(flipped_e[step + LEAD + 2])
            quantise_hidden(step - 1)
            second_layer(step - 1)
            if step + 1 < NODES:
                hand_source(step + 1)
            if step + LEAD + 1 < NODES:
                quantise_edges(step + LEAD + 1)
            if step == 1:
                flipped_e[4] = flip_unsorted_rows(e_rows[:, 4, :])
            if step == 2:
                flipped_e[6] = flip_unsorted_rows(e_rows[:, 6, :])
            if step == NODES - 1:
                open_hidden(step)
                quantise_hidden_half(step, 0)
                open_messages(step)
                for half in range(HALVES):
                    message_pass(step, half, 0)
            if step + 1 < NODES:
                sum_node_terms(step + 1)
            if step == NODES - 1:
                add_and_relu_in_parts(step, 1, step)
            else:
                for a, j in halves_of(step):
                    relu(j, a, add_terms(step, a, j))
            if UNSORTED <= step + LEAD + 4 < NODES:
                sorted_e[step + LEAD + 4] = sort_words(e_rows[:, step + LEAD + 4, :])
            if step == 1:
                grouped_e[4] = group_rows(flipped_e[4])
            if step < NODES - 1:
                for half in range(HALVES):
                    gather_messages(step - 1, half)
                for a, j in halves_of(step + 1):
                    first_layer(j, a)
            if step % 2 == 1:
                for j in range(step + LEAD + 3, min(step + LEAD + 5, NODES) if step > 1 else step + LEAD + 4):
                    if j < UNSORTED:
                        flipped_e[j] = flip_unsorted_rows(e_rows[:, j, :])
                    else:
                        flipped_e[j] = flip_rows(sorted_e[j])

        gather_messages(NODES - 2, 0)
        quantise_hidden_half(NODES - 1, 1)
        for half in range(HALVES):
            message_pass(NODES - 1, half, 1)
        gather_messages(NODES - 2, 1)
        for half, first, last in ((0, 0, N_TILE), (1, 0, N_TILE // 2), (1, N_TILE // 2, N_TILE)):
            gather_messages(NODES - 1, half, first, last)
            nc.sync.dma_start(
                out=rows_out[:, N_TILE * half + first : N_TILE * half + last],
                in_=result[:, N_TILE * half + first : N_TILE * half + last],
            )
